import numpy as np
import ml_dtypes


def mxq(x, axis, fmt="e4m3"):
    dtype, down = {"e4m3": (ml_dtypes.float8_e4m3fn, 7), "e5m2": (ml_dtypes.float8_e5m2, 14)}[fmt]
    v = np.moveaxis(np.asarray(x, np.float32).astype(ml_dtypes.bfloat16).astype(np.float64), axis, -1)
    blocks = v.reshape(v.shape[:-1] + (-1, 32))
    amax = np.abs(blocks).max(-1, keepdims=True)
    byte = np.maximum(np.where(amax > 0, np.frexp(amax)[1] - 1 + 127, 0) - down, 1)
    scale = np.exp2(byte - 127.0)
    codes = (blocks / scale).astype(np.float32).astype(dtype).astype(np.float64)
    return np.moveaxis((codes * scale).reshape(v.shape), -1, axis)


WIDE = False


def mx_kscale(k):
    if not WIDE:
        return np.ones(k)
    levels = np.array([10, -10, 5, -5, 0])
    a = np.random.permutation(np.resize(levels, k // 512 * 4)).reshape(k // 512, 4)
    idx = np.arange(k)
    return np.exp2(a[idx // 512, idx % 128 // 32])


BF16 = ml_dtypes.bfloat16


def bf(x):
    return np.asarray(x, np.float32).astype(BF16)


def f64(x):
    return np.asarray(x).astype(np.float64)


E2M1 = np.array([0.0, 0.5, 1.0, 1.5, 2.0, 3.0, 4.0, 6.0, -0.0, -0.5, -1.0, -1.5, -2.0, -3.0, -4.0, -6.0])


def pack_weight(w, fmt):
    k, n = w.shape
    w = f64(bf(w)).reshape(k // 32, 32, n)
    amax = np.abs(w).max(1)
    if fmt == "e4m3":
        byte = np.frexp(amax)[1] - 1 + 127 - 7
    else:
        mant, ex = np.frexp(amax / 6.0)
        byte = np.where(mant > 0.5, ex, ex - 1) + 127
    byte = np.clip(np.where(amax > 0, byte, 1), 1, 254)
    scaled = (w * np.exp2(127.0 - byte)[:, None, :]).reshape(k, n).astype(np.float32)
    by_word = np.ascontiguousarray(scaled.reshape(k // 512, 128, 4, n).transpose(0, 1, 3, 2))
    if fmt == "e4m3":
        words = by_word.astype(ml_dtypes.float8_e4m3fn).view(np.uint8)
    else:
        c = by_word.astype(ml_dtypes.float4_e2m1fn).view(np.uint8) & 0xF
        words = c[..., 0::2] | (c[..., 1::2] << 4)
    return np.ascontiguousarray(words), np.ascontiguousarray(byte.astype(np.uint8).reshape(k // 512, 16, n))


def unpack_weight(words, scales, fmt):
    g, p, n, _ = words.shape
    if fmt == "e4m3":
        vals = np.ascontiguousarray(words).view(ml_dtypes.float8_e4m3fn).astype(np.float64)
    else:
        nib = np.empty((g, p, n, 4), np.uint8)
        nib[..., 0::2] = words & 0xF
        nib[..., 1::2] = words >> 4
        vals = E2M1[nib]
    vals = vals * np.repeat(np.exp2(scales.astype(np.float64) - 127.0), 8, axis=1)[..., None]
    return vals.transpose(0, 1, 3, 2).reshape(g * 512, n)


B, T, N, M, A, C, Q, D = 2, 2, 512, 128, 384, 128, 512, 512
G = A + C
DILATION = 1.5
MIN_EXTENT = 0.5
GATE_TEMP = 3.0
FEAT_TEMP = 6.0
KEEP_W = 0.5
FMT = "e4m3"


def l2norm(x, eps=1e-12):
    n = np.sqrt((x * x).sum(axis=-1, keepdims=True))
    return x / np.maximum(n, eps)


def setup_inputs():
    s, u = mx_kscale(G), mx_kscale(Q)
    d = {}
    d["center"] = bf(np.random.standard_normal((B, T, N * 3)) * 5.0)
    d["instance_affinity"] = bf(np.random.standard_normal((B, T, N, A)) * s[:A])
    d["motion_code"] = bf(np.random.standard_normal((B, T, N, C)) * s[A:])
    d["keep_score"] = bf(np.maximum(np.random.uniform(-0.05, 0.99, (B, T, N)), 0.0))
    d["query_box3d"] = bf(np.random.standard_normal((B, T, M, 7)) * 3.0)
    d["query_feat"] = bf(np.random.standard_normal((B, T, M, Q)) * u)
    d["presence_logit"] = bf(np.random.standard_normal((B, T, M)))
    wq = np.random.standard_normal((D, Q)) / np.sqrt(Q) / u
    d["Wq_words"], d["Wq_scales"] = pack_weight(np.ascontiguousarray(wq.T), FMT)
    d["bq"] = bf(np.random.standard_normal(D) * 0.5)
    wg = np.random.standard_normal((D, G)) / np.sqrt(G) / s
    d["Wg_words"], d["Wg_scales"] = pack_weight(np.ascontiguousarray(wg.T), FMT)
    d["bg"] = bf(np.random.standard_normal(D) * 0.5)
    d["background_bias"] = bf(0.5 + 0.1 * np.random.standard_normal(1))
    return d


def reference(center, instance_affinity, motion_code, keep_score, query_box3d,
              query_feat, presence_logit, Wq_words, Wq_scales, bq, Wg_words, Wg_scales, bg, background_bias):
    b, t = center.shape[:2]
    centers = f64(center).reshape(b, t, -1, 3)
    qbox = f64(query_box3d)[..., :7]
    q_centers = qbox[..., :3]
    q_sizes = np.maximum(np.abs(qbox[..., 3:6]), MIN_EXTENT)

    delta = np.abs(centers[:, :, :, None, :] - q_centers[:, :, None, :, :])
    normalized = delta / (0.5 * DILATION * q_sizes[:, :, None, :, :])
    signed_distance = normalized.max(axis=-1) - 1.0
    gate_logit = np.clip(-signed_distance * GATE_TEMP, -8.0, 8.0)

    gfeat = np.concatenate([f64(instance_affinity), f64(motion_code)], axis=-1)
    gfeat = gfeat.reshape(b, t, -1, gfeat.shape[-1])
    qf = l2norm((mxq(f64(query_feat), 3, "e4m3") @ unpack_weight(Wq_words, Wq_scales, FMT)) + f64(bq))
    gf = l2norm((mxq(gfeat, 3, "e4m3") @ unpack_weight(Wg_words, Wg_scales, FMT)) + f64(bg))
    feature_similarity = mxq(gf, 3, "e4m3") @ mxq(qf, 3, "e4m3").transpose(0, 1, 3, 2)

    presence = f64(presence_logit)[:, :, None, :]
    ks = np.clip(f64(keep_score).reshape(b, t, -1, 1), 1e-4, 1.0 - 1e-4)
    routing_keep = np.log(ks) - np.log1p(-ks)

    fg_logits = presence + FEAT_TEMP * feature_similarity + gate_logit + KEEP_W * routing_keep
    bg_logits = np.zeros_like(fg_logits[..., :1]) + f64(background_bias)
    logits = np.concatenate([bg_logits, fg_logits], axis=-1)
    e = np.exp(logits - logits.max(axis=-1, keepdims=True))
    probs = e / e.sum(axis=-1, keepdims=True)
    return probs.reshape(b, -1, probs.shape[-1])

@@ -1,0 +1,410 @@
+from contextlib import ExitStack
+
+import concourse.mybir as mybir
+from concourse.masks import make_identity
+
+F32 = mybir.dt.float32
+BF16 = mybir.dt.bfloat16
+I32 = mybir.dt.int32
+U32 = mybir.dt.uint32
+U8 = mybir.dt.uint8
+FP8X4 = mybir.dt.float8_e4m3fn_x4
+ALU = mybir.AluOpType
+ACT = mybir.ActivationFunctionType
+
+P = 128
+PACK = 4
+PAIRS = 4
+TILES = 4
+ROWS = TILES * P
+QUERIES = 128
+K = 512
+AFFINITY = 384
+D = 512
+CLASSES = QUERIES + 1
+UNITS = 1 + PAIRS
+
+DILATION = 1.5
+MIN_EXTENT = 0.5
+GATE_TEMP = 3.0
+GATE_CLIP = 8.0
+FEAT_TEMP = 6.0
+KEEP_W = 0.5
+KEEP_EPS = 1e-4
+NORM_EPS = 1e-12
+
+FLOPS = 2 * (PAIRS * QUERIES + PAIRS * ROWS) * K * D + 2 * PAIRS * ROWS * QUERIES * D
+
+
+def tile_gaussianqueryassignment_kernel(
+    tc,
+    center,
+    instance_affinity,
+    motion_code,
+    keep_score,
+    query_box3d,
+    query_feat,
+    presence_logit,
+    Wq_words,
+    Wq_scales,
+    bq,
+    Wg_words,
+    Wg_scales,
+    bg,
+    background_bias,
+    out,
+):
+    nc = tc.nc
+    with ExitStack() as ctx:
+        keep = ctx.enter_context(tc.tile_pool(name="keep", bufs=1))
+        work = ctx.enter_context(tc.tile_pool(name="work", bufs=2))
+        rows_pool = ctx.enter_context(tc.tile_pool(name="rows", bufs=UNITS * TILES))
+        psum = ctx.enter_context(tc.psum_pool(name="psum", bufs=1))
+
+        ident_f32 = keep.tile([P, P], F32)
+        make_identity(nc, ident_f32[:])
+        ident_bf16 = keep.tile([P, P], BF16)
+        make_identity(nc, ident_bf16[:])
+        minus_half = keep.tile([P, TILES], F32)
+        nc.gpsimd.memset(minus_half[:], -0.5)
+
+        keep_in = keep.tile([P, PAIRS, TILES], BF16)
+        nc.sync.dma_start(out=keep_in[:], in_=keep_score.rearrange("b t (p j) -> p (b t) j", j=TILES))
+        bg_bias = keep.tile([P, 1], BF16)
+        nc.sync.dma_start(out=bg_bias[:], in_=background_bias.partition_broadcast(P))
+        box = keep.tile([P, PAIRS, 7], BF16)
+        nc.sync.dma_start(out=box[:], in_=query_box3d.rearrange("b t m c -> m (b t) c"))
+        position = keep.tile([P, PAIRS, TILES, 3], BF16)
+        nc.sync.dma_start(
+            out=position[:].rearrange("p g j c -> p g (j c)"),
+            in_=center.rearrange("b t (p c) -> p (b t) c", c=3 * TILES),
+        )
+        presence = keep.tile([P, PAIRS], BF16)
+        with nc.allow_non_contiguous_dma(reason="512 two-byte elements, one query to a partition"):
+            nc.sync.dma_start(out=presence[:], in_=presence_logit.rearrange("b t m -> m (b t)"))
+        xq = keep.tile([P, PAIRS, K], BF16)
+        nc.sync.dma_start(out=xq[:], in_=query_feat.rearrange("b t m k -> m (b t) k"))
+
+        def load_weight(bias_in, words_in, scales_in, bias_rows, words, plane):
+            nc.vector.memset(plane[:].bitcast(I32), 0)
+            nc.sync.dma_start(out=bias_rows[:], in_=bias_in.partition_broadcast(P))
+            nc.sync.dma_start(
+                out=words[:].bitcast(I32),
+                in_=words_in[0].rearrange("p n t -> p (n t)").bitcast(I32),
+            )
+            for quadrant in range(4):
+                nc.sync.dma_start(
+                    out=plane[32 * quadrant : 32 * quadrant + 4, :].bitcast(I32),
+                    in_=scales_in[0, 4 * quadrant : 4 * quadrant + 4, :].bitcast(I32),
+                )
+
+        xg = keep.tile([P, PAIRS, TILES, K], BF16)
+        affinity_in = instance_affinity.rearrange("b t (p j) a -> (b t) p j a", j=TILES)
+        motion_in = motion_code.rearrange("b t (p j) c -> (b t) p j c", j=TILES)
+
+        def load_gaussians(g):
+            nc.sync.dma_start(out=xg[:, g, :, 0:AFFINITY], in_=affinity_in[g])
+            nc.sync.dma_start(out=xg[:, g, :, AFFINITY:K], in_=motion_in[g])
+
+        bq_rows = keep.tile([P, D], BF16)
+        wq_words = keep.tile([P, D], U32, align_bytes=64)
+        wq_plane = keep.tile([P, D], U8, align_bytes=64)
+        load_weight(bq, Wq_words, Wq_scales, bq_rows, wq_words, wq_plane)
+        load_gaussians(0)
+        bg_rows = keep.tile([P, D], BF16)
+        wg_words = keep.tile([P, D], U32, align_bytes=64)
+        wg_plane = keep.tile([P, D], U8, align_bytes=64)
+        load_weight(bg, Wg_words, Wg_scales, bg_rows, wg_words, wg_plane)
+        for g in range(1, PAIRS):
+            load_gaussians(g)
+
+        k_and_rest = keep.tile([P, 2, PAIRS, TILES], F32)
+        nc.vector.tensor_scalar(
+            out=k_and_rest[:, 0], in0=keep_in[:], scalar1=KEEP_EPS, scalar2=1.0 - KEEP_EPS, op0=ALU.max, op1=ALU.min
+        )
+        nc.vector.tensor_scalar(
+            out=k_and_rest[:, 1], in0=k_and_rest[:, 0], scalar1=-1.0, scalar2=1.0, op0=ALU.mult, op1=ALU.add
+        )
+        logs = keep.tile([P, 2, PAIRS, TILES], F32)
+        nc.scalar.activation(out=logs[:], in_=k_and_rest[:], func=ACT.Ln)
+
+        size = keep.tile([P, PAIRS, 3], F32)
+        nc.vector.scalar_tensor_tensor(
+            out=size[:], in0=box[:, :, 3:6], scalar=-1.0, in1=box[:, :, 3:6], op0=ALU.mult, op1=ALU.max
+        )
+        nc.vector.tensor_scalar(
+            out=size[:],
+            in0=size[:],
+            scalar1=MIN_EXTENT,
+            scalar2=0.5 * DILATION / GATE_TEMP,
+            op0=ALU.max,
+            op1=ALU.mult,
+        )
+        rate = keep.tile([P, PAIRS, 3], F32)
+        nc.vector.reciprocal(out=rate[:], in_=size[:])
+        shift = keep.tile([P, PAIRS, 3], F32)
+        nc.vector.scalar_tensor_tensor(
+            out=shift[:], in0=box[:, :, 0:3], scalar=-1.0, in1=rate[:], op0=ALU.mult, op1=ALU.mult
+        )
+        presence_plus = keep.tile([P, PAIRS], F32)
+        nc.vector.tensor_scalar_add(out=presence_plus[:], in0=presence[:], scalar1=GATE_TEMP)
+        position_f32 = keep.tile([P, PAIRS, TILES, 3], F32)
+        nc.vector.tensor_copy(out=position_f32[:], in_=position[:])
+
+        neg_background = keep.tile([P, PAIRS, TILES], F32)
+        nc.vector.tensor_tensor(out=neg_background[:], in0=logs[:, 0], in1=logs[:, 1], op=ALU.subtract)
+        nc.vector.tensor_scalar(
+            out=neg_background[:],
+            in0=neg_background[:],
+            scalar1=KEEP_W,
+            scalar2=bg_bias[:, 0:1],
+            op0=ALU.mult,
+            op1=ALU.subtract,
+        )
+
+        x_grouped, x_words, x_plane = {}, {}, {}
+        y, square_sum, inv_norm = {}, {}, {}
+        f, f_grouped, f_words, f_plane = {}, {}, {}, {}
+
+        def is_unit(u):
+            return 0 <= u < UNITS
+
+        def is_pair(g):
+            return 0 <= g < PAIRS
+
+        def transpose_inputs(u, half):
+            if not is_unit(u):
+                return
+            x_unit = xq if u == 0 else xg[:, u - 1]
+            if half == 0:
+                x_grouped[u] = work.tile([P, ROWS, PACK], BF16, tag="x_grouped", name="x_grouped", align_bytes=64)
+            grouped_pairs = x_grouped[u][:].bitcast(F32)
+            x_t = psum.tile([P, 2, 2, P], F32, tag="transposed_words", bufs=3)
+            for i in range(2):
+                x_pairs = x_unit[:, 2 * half + i, :].bitcast(F32)
+                for u2 in range(2):
+                    nc.tensor.transpose(x_t[:, i, u2, :], x_pairs[:, u2 : K // 2 : 2], ident_f32[:])
+            copy_out = nc.scalar.copy if half == 0 else nc.vector.tensor_copy
+            copy_out(
+                out=grouped_pairs[:, 2 * P * half : 2 * P * (half + 1), :].rearrange("p (i r) u2 -> p i r u2", i=2),
+                in_=x_t[:].rearrange("p i u2 r -> p i r u2"),
+            )
+
+        def quantise_inputs(u):
+            if not is_unit(u):
+                return
+            x_words[u] = work.tile([P, ROWS], U32, tag="x_words", name="x_words", bufs=3, align_bytes=64)
+            x_plane[u] = work.tile([P, ROWS], U8, tag="x_plane", name="x_plane", bufs=3, align_bytes=64)
+            nc.vector.quantize_mx(
+                out=x_words[u][:].bitcast(FP8X4),
+                scales=x_plane[u][:],
+                in_=x_grouped[u][:].rearrange("p r t -> p (r t)"),
+            )
+
+        y_psum = {}
+
+        def multiply(u, i):
+            if not is_unit(u):
+                return
+            tile_cols = slice(P * i, P * (i + 1))
+            y_psum[u, i] = psum.tile([P, D], F32, tag="y_psum", name="y_psum", bufs=2)
+            nc.tensor.matmul_mx(
+                out=y_psum[u, i][:],
+                lhsT=x_words[u][:, tile_cols].bitcast(FP8X4),
+                lhsT_scale=x_plane[u][:, tile_cols],
+                rhs=(wq_words if u == 0 else wg_words)[:].bitcast(FP8X4),
+                rhs_scale=(wq_plane if u == 0 else wg_plane)[:],
+                start=True,
+                stop=True,
+            )
+
+        def add_bias_and_square(u, i):
+            if not is_unit(u):
+                return
+            if i == 0:
+                square_sum[u] = work.tile([P, TILES], F32, tag="square_sum", name="square_sum", bufs=UNITS)
+            y[u, i] = rows_pool.tile([P, D], F32, tag="y", name="y")
+            nc.vector.tensor_tensor(
+                out=y[u, i][:], in0=y_psum[u, i][:], in1=(bq_rows if u == 0 else bg_rows)[:], op=ALU.add
+            )
+            squares = work.tile([P, D], BF16, tag="squares")
+            nc.scalar.activation(
+                out=squares[:], in_=y[u, i][:], func=ACT.Square, accum_out=square_sum[u][:, i : i + 1]
+            )
+
+        def normalise(u):
+            if not is_unit(u):
+                return
+            inv_norm[u] = work.tile([P, TILES], F32, tag="inv_norm", name="inv_norm", bufs=UNITS)
+            nc.gpsimd.tensor_scalar_max(out=inv_norm[u][:], in0=square_sum[u][:], scalar1=NORM_EPS * NORM_EPS)
+            nc.gpsimd.tensor_tensor(out=inv_norm[u][:], in0=inv_norm[u][:], in1=minus_half[:], op=ALU.pow)
+            f[u] = work.tile([P, TILES, D], BF16, tag="f", name="f", bufs=UNITS)
+            for i in range(TILES):
+                nc.gpsimd.tensor_scalar(
+                    out=f[u][:, i, :],
+                    in0=y[u, i][:],
+                    scalar1=inv_norm[u][:, i : i + 1],
+                    scalar2=0.0,
+                    op0=ALU.mult,
+                    op1=ALU.add,
+                )
+
+        def transpose_features(u, half):
+            if not is_unit(u):
+                return
+            if half == 0:
+                f_grouped[u] = work.tile([P, ROWS, PACK], BF16, tag="f_grouped", name="f_grouped", align_bytes=64)
+            f_t = psum.tile([P, 2, PACK, P], BF16, tag="f_t", bufs=2)
+            for i in range(2):
+                for t in range(PACK):
+                    nc.tensor.transpose(f_t[:, i, t, :], f[u][:, 2 * half + i, P * t : P * (t + 1)], ident_bf16[:])
+            nc.scalar.copy(
+                out=f_grouped[u][:, 2 * P * half : 2 * P * (half + 1), :].rearrange("p (i r) t -> p i r t", i=2),
+                in_=f_t[:].rearrange("p i t r -> p i r t"),
+            )
+
+        def quantise_features(u):
+            if not is_unit(u):
+                return
+            pool = keep if u == 0 else work
+            f_words[u] = pool.tile([P, ROWS], U32, tag="qf_words" if u == 0 else "gf_words", name="f_words", align_bytes=64)
+            f_plane[u] = pool.tile([P, ROWS], U8, tag="qf_plane" if u == 0 else "gf_plane", name="f_plane", align_bytes=64)
+            nc.vector.quantize_mx(
+                out=f_words[u][:].bitcast(FP8X4),
+                scales=f_plane[u][:],
+                in_=f_grouped[u][:].rearrange("p r t -> p (r t)"),
+            )
+
+        reach = {}
+        penalty = keep.tile([P, PAIRS, ROWS], F32)
+
+        def gate_reach(g, c):
+            if not is_pair(g):
+                return
+            if c == 0:
+                reach[g] = work.tile([P, 3, ROWS], F32, tag="reach", name="reach")
+            spread = psum.tile([P, TILES, P], F32, tag="transposed_words", bufs=3)
+            for j in range(TILES):
+                nc.tensor.transpose(
+                    spread[:, j, :], position_f32[:, g, j, c : c + 1].to_broadcast([P, P]), ident_f32[:]
+                )
+            nc.scalar.activation(
+                out=reach[g][:, c, :],
+                in_=spread[:].rearrange("m j p -> m (j p)"),
+                func=ACT.Abs,
+                scale=rate[:, g, c : c + 1],
+                bias=shift[:, g, c : c + 1],
+            )
+
+        def gate_penalty(g):
+            if not is_pair(g):
+                return
+            farthest = reach[g][:, 0, :]
+            nc.vector.tensor_tensor(out=farthest, in0=farthest, in1=reach[g][:, 1, :], op=ALU.max)
+            nc.vector.tensor_tensor(out=farthest, in0=farthest, in1=reach[g][:, 2, :], op=ALU.max)
+            nc.vector.tensor_scalar(
+                out=penalty[:, g, :],
+                in0=farthest,
+                scalar1=GATE_TEMP + GATE_CLIP,
+                scalar2=presence_plus[:, g : g + 1],
+                op0=ALU.min,
+                op1=ALU.subtract,
+            )
+
+        logits_t, logits, neg_max, background_gap, probs, query_sum = {}, {}, {}, {}, {}, {}
+        out_rows = out.rearrange("b (t p j) c -> (b t) p (j c)", p=P, j=TILES)
+
+        def similarity(g):
+            if not is_pair(g):
+                return
+            query_cols = slice(QUERIES * g, QUERIES * (g + 1))
+            sim = psum.tile([P, ROWS], F32, tag="y_psum", bufs=2)
+            nc.tensor.matmul_mx(
+                out=sim[:],
+                lhsT=f_words[0][:, query_cols].bitcast(FP8X4),
+                lhsT_scale=f_plane[0][:, query_cols],
+                rhs=f_words[1 + g][:].bitcast(FP8X4),
+                rhs_scale=f_plane[1 + g][:],
+                start=True,
+                stop=True,
+            )
+            logits_t[g] = work.tile([P, ROWS], F32, tag="logits_t", name="logits_t")
+            nc.vector.scalar_tensor_tensor(
+                out=logits_t[g][:], in0=sim[:], scalar=FEAT_TEMP, in1=penalty[:, g, :], op0=ALU.mult, op1=ALU.subtract
+            )
+
+        def rows_to_partitions(g):
+            if not is_pair(g):
+                return
+            logits[g] = psum.tile([P, TILES, QUERIES], F32, tag="transposed_words", name="logits", bufs=3)
+            for j in range(TILES):
+                nc.tensor.transpose(logits[g][:, j, :], logits_t[g][:, P * j : P * (j + 1)], ident_f32[:])
+
+        def row_maxima(g):
+            if not is_pair(g):
+                return
+            query_max = work.tile([P, TILES], F32, tag="query_max")
+            nc.vector.tensor_reduce(out=query_max[:], in_=logits[g][:], axis=mybir.AxisListType.X, op=ALU.max)
+            neg_max[g] = work.tile([P, TILES], F32, tag="neg_max", name="neg_max")
+            nc.vector.scalar_tensor_tensor(
+                out=neg_max[g][:], in0=query_max[:], scalar=-1.0, in1=neg_background[:, g, :], op0=ALU.mult, op1=ALU.min
+            )
+            background_gap[g] = work.tile([P, TILES, 1], F32, tag="background_gap", name="background_gap")
+            nc.vector.tensor_tensor(
+                out=background_gap[g][:, :, 0], in0=neg_background[:, g, :], in1=neg_max[g][:], op=ALU.subtract
+            )
+
+        def exponentials(g):
+            if not is_pair(g):
+                return
+            probs[g] = work.tile([P, TILES, CLASSES], F32, tag="probs", name="probs")
+            query_sum[g] = work.tile([P, TILES, 1], F32, tag="query_sum", name="query_sum")
+            for j in range(TILES):
+                nc.scalar.activation(
+                    out=probs[g][:, j, 1:CLASSES],
+                    in_=logits[g][:, j, :],
+                    func=ACT.Exp,
+                    bias=neg_max[g][:, j : j + 1],
+                    accum_out=query_sum[g][:, j, :],
+                )
+            nc.scalar.activation(out=probs[g][:, :, 0:1], in_=background_gap[g][:], func=ACT.Exp, scale=-1.0)
+
+        def finish(g):
+            if not is_pair(g):
+                return
+            total = work.tile([P, TILES, 1], F32, tag="total")
+            nc.vector.tensor_tensor(out=total[:], in0=query_sum[g][:], in1=probs[g][:, :, 0:1], op=ALU.add)
+            nc.vector.reciprocal(out=total[:], in_=total[:])
+            nc.vector.tensor_tensor(
+                out=probs[g][:], in0=probs[g][:], in1=total[:].to_broadcast([P, TILES, CLASSES]), op=ALU.mult
+            )
+            nc.sync.dma_start(out=out_rows[g], in_=probs[g][:].rearrange("p j c -> p (j c)"))
+
+        with tc.manual_schedule():
+            for step in range(-2, UNITS):
+                ahead = step + 2
+                multiply(step, 0)
+                multiply(step, 1)
+                transpose_inputs(ahead, 0)
+                add_bias_and_square(step, 0)
+                add_bias_and_square(step, 1)
+                transpose_inputs(ahead, 1)
+                multiply(step, 2)
+                gate_reach(ahead, 0)
+                add_bias_and_square(step, 2)
+                quantise_inputs(ahead)
+                multiply(step, 3)
+                gate_reach(ahead, 1)
+                add_bias_and_square(step, 3)
+                gate_reach(ahead, 2)
+                gate_penalty(ahead - 1)
+                normalise(step)
+            for step in range(UNITS + 4):
+                transpose_features(step, 0)
+                transpose_features(step, 1)
+                finish(step - 4)
+                quantise_features(step - 1)
+                row_maxima(step - 3)
+                similarity(step - 2)
+                rows_to_partitions(step - 2)
+                exponentials(step - 3)

@@ -59,7 +59,7 @@ def tile_gaussianqueryassignment_kernel(
         keep = ctx.enter_context(tc.tile_pool(name="keep", bufs=1))
         work = ctx.enter_context(tc.tile_pool(name="work", bufs=2))
         rows_pool = ctx.enter_context(tc.tile_pool(name="rows", bufs=UNITS * TILES))
-        psum = ctx.enter_context(tc.psum_pool(name="psum", bufs=1))
+        psum = ctx.enter_context(tc.psum_pool(name="psum", bufs=8))
 
         ident_f32 = keep.tile([P, P], F32)
         make_identity(nc, ident_f32[:])
@@ -68,22 +68,12 @@ def tile_gaussianqueryassignment_kernel(
         minus_half = keep.tile([P, TILES], F32)
         nc.gpsimd.memset(minus_half[:], -0.5)
 
+        xq = keep.tile([P, PAIRS, K], BF16)
+        nc.sync.dma_start(out=xq[:], in_=query_feat.rearrange("b t m k -> m (b t) k"))
         keep_in = keep.tile([P, PAIRS, TILES], BF16)
         nc.sync.dma_start(out=keep_in[:], in_=keep_score.rearrange("b t (p j) -> p (b t) j", j=TILES))
         bg_bias = keep.tile([P, 1], BF16)
         nc.sync.dma_start(out=bg_bias[:], in_=background_bias.partition_broadcast(P))
-        box = keep.tile([P, PAIRS, 7], BF16)
-        nc.sync.dma_start(out=box[:], in_=query_box3d.rearrange("b t m c -> m (b t) c"))
-        position = keep.tile([P, PAIRS, TILES, 3], BF16)
-        nc.sync.dma_start(
-            out=position[:].rearrange("p g j c -> p g (j c)"),
-            in_=center.rearrange("b t (p c) -> p (b t) c", c=3 * TILES),
-        )
-        presence = keep.tile([P, PAIRS], BF16)
-        with nc.allow_non_contiguous_dma(reason="512 two-byte elements, one query to a partition"):
-            nc.sync.dma_start(out=presence[:], in_=presence_logit.rearrange("b t m -> m (b t)"))
-        xq = keep.tile([P, PAIRS, K], BF16)
-        nc.sync.dma_start(out=xq[:], in_=query_feat.rearrange("b t m k -> m (b t) k"))
 
         def load_weight(bias_in, words_in, scales_in, bias_rows, words, plane):
             nc.vector.memset(plane[:].bitcast(I32), 0)
@@ -117,6 +107,16 @@ def tile_gaussianqueryassignment_kernel(
         load_weight(bg, Wg_words, Wg_scales, bg_rows, wg_words, wg_plane)
         for g in range(1, PAIRS):
             load_gaussians(g)
+        box = keep.tile([P, PAIRS, 7], BF16)
+        nc.sync.dma_start(out=box[:], in_=query_box3d.rearrange("b t m c -> m (b t) c"))
+        position = keep.tile([P, PAIRS, TILES, 3], BF16)
+        nc.sync.dma_start(
+            out=position[:].rearrange("p g j c -> p g (j c)"),
+            in_=center.rearrange("b t (p c) -> p (b t) c", c=3 * TILES),
+        )
+        presence = keep.tile([P, PAIRS], BF16)
+        with nc.allow_non_contiguous_dma(reason="512 two-byte elements, one query to a partition"):
+            nc.sync.dma_start(out=presence[:], in_=presence_logit.rearrange("b t m -> m (b t)"))
 
         k_and_rest = keep.tile([P, 2, PAIRS, TILES], F32)
         nc.vector.tensor_scalar(
@@ -128,29 +128,6 @@ def tile_gaussianqueryassignment_kernel(
         logs = keep.tile([P, 2, PAIRS, TILES], F32)
         nc.scalar.activation(out=logs[:], in_=k_and_rest[:], func=ACT.Ln)
 
-        size = keep.tile([P, PAIRS, 3], F32)
-        nc.vector.scalar_tensor_tensor(
-            out=size[:], in0=box[:, :, 3:6], scalar=-1.0, in1=box[:, :, 3:6], op0=ALU.mult, op1=ALU.max
-        )
-        nc.vector.tensor_scalar(
-            out=size[:],
-            in0=size[:],
-            scalar1=MIN_EXTENT,
-            scalar2=0.5 * DILATION / GATE_TEMP,
-            op0=ALU.max,
-            op1=ALU.mult,
-        )
-        rate = keep.tile([P, PAIRS, 3], F32)
-        nc.vector.reciprocal(out=rate[:], in_=size[:])
-        shift = keep.tile([P, PAIRS, 3], F32)
-        nc.vector.scalar_tensor_tensor(
-            out=shift[:], in0=box[:, :, 0:3], scalar=-1.0, in1=rate[:], op0=ALU.mult, op1=ALU.mult
-        )
-        presence_plus = keep.tile([P, PAIRS], F32)
-        nc.vector.tensor_scalar_add(out=presence_plus[:], in0=presence[:], scalar1=GATE_TEMP)
-        position_f32 = keep.tile([P, PAIRS, TILES, 3], F32)
-        nc.vector.tensor_copy(out=position_f32[:], in_=position[:])
-
         neg_background = keep.tile([P, PAIRS, TILES], F32)
         nc.vector.tensor_tensor(out=neg_background[:], in0=logs[:, 0], in1=logs[:, 1], op=ALU.subtract)
         nc.vector.tensor_scalar(
@@ -161,6 +138,29 @@ def tile_gaussianqueryassignment_kernel(
             op0=ALU.mult,
             op1=ALU.subtract,
         )
+
+        size = keep.tile([P, PAIRS, 3], F32)
+        rate = keep.tile([P, PAIRS, 3], F32)
+        shift = keep.tile([P, PAIRS, 3], F32)
+        presence_plus = keep.tile([P, PAIRS], F32)
+
+        def prepare_boxes():
+            nc.vector.scalar_tensor_tensor(
+                out=size[:], in0=box[:, :, 3:6], scalar=-1.0, in1=box[:, :, 3:6], op0=ALU.mult, op1=ALU.max
+            )
+            nc.vector.tensor_scalar(
+                out=size[:],
+                in0=size[:],
+                scalar1=MIN_EXTENT,
+                scalar2=0.5 * DILATION / GATE_TEMP,
+                op0=ALU.max,
+                op1=ALU.mult,
+            )
+            nc.vector.reciprocal(out=rate[:], in_=size[:])
+            nc.vector.scalar_tensor_tensor(
+                out=shift[:], in0=box[:, :, 0:3], scalar=-1.0, in1=rate[:], op0=ALU.mult, op1=ALU.mult
+            )
+            nc.vector.tensor_scalar_add(out=presence_plus[:], in0=presence[:], scalar1=GATE_TEMP)
 
         x_grouped, x_words, x_plane = {}, {}, {}
         y, square_sum, inv_norm = {}, {}, {}
@@ -179,7 +179,7 @@ def tile_gaussianqueryassignment_kernel(
             if half == 0:
                 x_grouped[u] = work.tile([P, ROWS, PACK], BF16, tag="x_grouped", name="x_grouped", align_bytes=64)
             grouped_pairs = x_grouped[u][:].bitcast(F32)
-            x_t = psum.tile([P, 2, 2, P], F32, tag="transposed_words", bufs=3)
+            x_t = psum.tile([P, 2, 2, P], F32, tag="bank")
             for i in range(2):
                 x_pairs = x_unit[:, 2 * half + i, :].bitcast(F32)
                 for u2 in range(2):
@@ -207,7 +207,7 @@ def tile_gaussianqueryassignment_kernel(
             if not is_unit(u):
                 return
             tile_cols = slice(P * i, P * (i + 1))
-            y_psum[u, i] = psum.tile([P, D], F32, tag="y_psum", name="y_psum", bufs=2)
+            y_psum[u, i] = psum.tile([P, D], F32, tag="bank", name="y_psum")
             nc.tensor.matmul_mx(
                 out=y_psum[u, i][:],
                 lhsT=x_words[u][:, tile_cols].bitcast(FP8X4),
@@ -254,7 +254,7 @@ def tile_gaussianqueryassignment_kernel(
                 return
             if half == 0:
                 f_grouped[u] = work.tile([P, ROWS, PACK], BF16, tag="f_grouped", name="f_grouped", align_bytes=64)
-            f_t = psum.tile([P, 2, PACK, P], BF16, tag="f_t", bufs=2)
+            f_t = psum.tile([P, 2, PACK, P], BF16, tag="bank")
             for i in range(2):
                 for t in range(PACK):
                     nc.tensor.transpose(f_t[:, i, t, :], f[u][:, 2 * half + i, P * t : P * (t + 1)], ident_bf16[:])
@@ -283,10 +283,10 @@ def tile_gaussianqueryassignment_kernel(
                 return
             if c == 0:
                 reach[g] = work.tile([P, 3, ROWS], F32, tag="reach", name="reach")
-            spread = psum.tile([P, TILES, P], F32, tag="transposed_words", bufs=3)
+            spread = psum.tile([P, TILES, P], BF16, tag="bank")
             for j in range(TILES):
                 nc.tensor.transpose(
-                    spread[:, j, :], position_f32[:, g, j, c : c + 1].to_broadcast([P, P]), ident_f32[:]
+                    spread[:, j, :], position[:, g, j, c : c + 1].to_broadcast([P, P]), ident_bf16[:]
                 )
             nc.scalar.activation(
                 out=reach[g][:, c, :],
@@ -318,7 +318,7 @@ def tile_gaussianqueryassignment_kernel(
             if not is_pair(g):
                 return
             query_cols = slice(QUERIES * g, QUERIES * (g + 1))
-            sim = psum.tile([P, ROWS], F32, tag="y_psum", bufs=2)
+            sim = psum.tile([P, ROWS], F32, tag="bank")
             nc.tensor.matmul_mx(
                 out=sim[:],
                 lhsT=f_words[0][:, query_cols].bitcast(FP8X4),
@@ -336,7 +336,7 @@ def tile_gaussianqueryassignment_kernel(
         def rows_to_partitions(g):
             if not is_pair(g):
                 return
-            logits[g] = psum.tile([P, TILES, QUERIES], F32, tag="transposed_words", name="logits", bufs=3)
+            logits[g] = psum.tile([P, TILES, QUERIES], F32, tag="bank", name="logits")
             for j in range(TILES):
                 nc.tensor.transpose(logits[g][:, j, :], logits_t[g][:, P * j : P * (j + 1)], ident_f32[:])
 
@@ -383,28 +383,26 @@ def tile_gaussianqueryassignment_kernel(
         with tc.manual_schedule():
             for step in range(-2, UNITS):
                 ahead = step + 2
-                multiply(step, 0)
-                multiply(step, 1)
-                transpose_inputs(ahead, 0)
+                for i in range(TILES):
+                    multiply(step, i)
                 add_bias_and_square(step, 0)
                 add_bias_and_square(step, 1)
-                transpose_inputs(ahead, 1)
-                multiply(step, 2)
-                gate_reach(ahead, 0)
+                transpose_inputs(ahead, 0)
                 add_bias_and_square(step, 2)
-                quantise_inputs(ahead)
-                multiply(step, 3)
-                gate_reach(ahead, 1)
+                transpose_inputs(ahead, 1)
                 add_bias_and_square(step, 3)
-                gate_reach(ahead, 2)
-                gate_penalty(ahead - 1)
+                quantise_inputs(ahead)
                 normalise(step)
+            prepare_boxes()
             for step in range(UNITS + 4):
                 transpose_features(step, 0)
                 transpose_features(step, 1)
+                for c in range(3):
+                    gate_reach(step, c)
                 finish(step - 4)
                 quantise_features(step - 1)
                 row_maxima(step - 3)
+                gate_penalty(step - 1)
                 similarity(step - 2)
                 rows_to_partitions(step - 2)
                 exponentials(step - 3)

@@ -32,6 +32,7 @@ FEAT_TEMP = 6.0
 KEEP_W = 0.5
 KEEP_EPS = 1e-4
 NORM_EPS = 1e-12
+GAP_MAX = 80.0
 
 FLOPS = 2 * (PAIRS * QUERIES + PAIRS * ROWS) * K * D + 2 * PAIRS * ROWS * QUERIES * D
 
@@ -67,17 +68,17 @@ def tile_gaussianqueryassignment_kernel(
         make_identity(nc, ident_bf16[:])
         minus_half = keep.tile([P, TILES], F32)
         nc.gpsimd.memset(minus_half[:], -0.5)
+        ones = keep.tile([P, 1], F32)
+        nc.gpsimd.memset(ones[:], 1.0)
 
-        xq = keep.tile([P, PAIRS, K], BF16)
-        nc.sync.dma_start(out=xq[:], in_=query_feat.rearrange("b t m k -> m (b t) k"))
-        keep_in = keep.tile([P, PAIRS, TILES], BF16)
-        nc.sync.dma_start(out=keep_in[:], in_=keep_score.rearrange("b t (p j) -> p (b t) j", j=TILES))
-        bg_bias = keep.tile([P, 1], BF16)
-        nc.sync.dma_start(out=bg_bias[:], in_=background_bias.partition_broadcast(P))
+        wq_words = keep.tile([P, D], U32, align_bytes=64)
+        wq_plane = keep.tile([P, D], U8, align_bytes=64)
+        wg_words = keep.tile([P, D], U32, align_bytes=64)
+        wg_plane = keep.tile([P, D], U8, align_bytes=64)
+        nc.vector.memset(wq_plane[:].bitcast(I32), 0)
+        nc.vector.memset(wg_plane[:].bitcast(I32), 0)
 
-        def load_weight(bias_in, words_in, scales_in, bias_rows, words, plane):
-            nc.vector.memset(plane[:].bitcast(I32), 0)
-            nc.sync.dma_start(out=bias_rows[:], in_=bias_in.partition_broadcast(P))
+        def load_weight(words_in, scales_in, words, plane):
             nc.sync.dma_start(
                 out=words[:].bitcast(I32),
                 in_=words_in[0].rearrange("p n t -> p (n t)").bitcast(I32),
@@ -96,53 +97,48 @@ def tile_gaussianqueryassignment_kernel(
             nc.sync.dma_start(out=xg[:, g, :, 0:AFFINITY], in_=affinity_in[g])
             nc.sync.dma_start(out=xg[:, g, :, AFFINITY:K], in_=motion_in[g])
 
-        bq_rows = keep.tile([P, D], BF16)
-        wq_words = keep.tile([P, D], U32, align_bytes=64)
-        wq_plane = keep.tile([P, D], U8, align_bytes=64)
-        load_weight(bq, Wq_words, Wq_scales, bq_rows, wq_words, wq_plane)
-        load_gaussians(0)
-        bg_rows = keep.tile([P, D], BF16)
-        wg_words = keep.tile([P, D], U32, align_bytes=64)
-        wg_plane = keep.tile([P, D], U8, align_bytes=64)
-        load_weight(bg, Wg_words, Wg_scales, bg_rows, wg_words, wg_plane)
-        for g in range(1, PAIRS):
-            load_gaussians(g)
-        box = keep.tile([P, PAIRS, 7], BF16)
-        nc.sync.dma_start(out=box[:], in_=query_box3d.rearrange("b t m c -> m (b t) c"))
+        keep_in = keep.tile([P, PAIRS, TILES], BF16)
+        nc.sync.dma_start(out=keep_in[:], in_=keep_score.rearrange("b t (p j) -> p (b t) j", j=TILES))
         position = keep.tile([P, PAIRS, TILES, 3], BF16)
         nc.sync.dma_start(
             out=position[:].rearrange("p g j c -> p g (j c)"),
             in_=center.rearrange("b t (p c) -> p (b t) c", c=3 * TILES),
         )
+        box = keep.tile([P, PAIRS, 7], BF16)
+        nc.sync.dma_start(out=box[:], in_=query_box3d.rearrange("b t m c -> m (b t) c"))
         presence = keep.tile([P, PAIRS], BF16)
         with nc.allow_non_contiguous_dma(reason="512 two-byte elements, one query to a partition"):
             nc.sync.dma_start(out=presence[:], in_=presence_logit.rearrange("b t m -> m (b t)"))
+        bg_bias = keep.tile([P, 1], BF16)
+        nc.sync.dma_start(out=bg_bias[:], in_=background_bias.partition_broadcast(P))
+        xq = keep.tile([P, PAIRS, K], BF16)
+        nc.sync.dma_start(out=xq[:], in_=query_feat.rearrange("b t m k -> m (b t) k"))
+        load_weight(Wq_words, Wq_scales, wq_words, wq_plane)
+        load_gaussians(0)
+        bq_rows = keep.tile([P, D], BF16)
+        nc.sync.dma_start(out=bq_rows[:], in_=bq.partition_broadcast(P))
+        load_weight(Wg_words, Wg_scales, wg_words, wg_plane)
+        bg_rows = keep.tile([P, D], BF16)
+        nc.sync.dma_start(out=bg_rows[:], in_=bg.partition_broadcast(P))
+        load_gaussians(1)
+        load_gaussians(2)
+        load_gaussians(3)
 
         k_and_rest = keep.tile([P, 2, PAIRS, TILES], F32)
-        nc.vector.tensor_scalar(
-            out=k_and_rest[:, 0], in0=keep_in[:], scalar1=KEEP_EPS, scalar2=1.0 - KEEP_EPS, op0=ALU.max, op1=ALU.min
-        )
-        nc.vector.tensor_scalar(
-            out=k_and_rest[:, 1], in0=k_and_rest[:, 0], scalar1=-1.0, scalar2=1.0, op0=ALU.mult, op1=ALU.add
-        )
         logs = keep.tile([P, 2, PAIRS, TILES], F32)
-        nc.scalar.activation(out=logs[:], in_=k_and_rest[:], func=ACT.Ln)
 
-        neg_background = keep.tile([P, PAIRS, TILES], F32)
-        nc.vector.tensor_tensor(out=neg_background[:], in0=logs[:, 0], in1=logs[:, 1], op=ALU.subtract)
-        nc.vector.tensor_scalar(
-            out=neg_background[:],
-            in0=neg_background[:],
-            scalar1=KEEP_W,
-            scalar2=bg_bias[:, 0:1],
-            op0=ALU.mult,
-            op1=ALU.subtract,
-        )
+        def keep_logs():
+            nc.vector.tensor_scalar(
+                out=k_and_rest[:, 0], in0=keep_in[:], scalar1=KEEP_EPS, scalar2=1.0 - KEEP_EPS, op0=ALU.max, op1=ALU.min
+            )
+            nc.vector.tensor_scalar(
+                out=k_and_rest[:, 1], in0=k_and_rest[:, 0], scalar1=-1.0, scalar2=1.0, op0=ALU.mult, op1=ALU.add
+            )
+            nc.scalar.activation(out=logs[:], in_=k_and_rest[:], func=ACT.Ln)
 
         size = keep.tile([P, PAIRS, 3], F32)
         rate = keep.tile([P, PAIRS, 3], F32)
         shift = keep.tile([P, PAIRS, 3], F32)
-        presence_plus = keep.tile([P, PAIRS], F32)
 
         def prepare_boxes():
             nc.vector.scalar_tensor_tensor(
@@ -152,7 +148,7 @@ def tile_gaussianqueryassignment_kernel(
                 out=size[:],
                 in0=size[:],
                 scalar1=MIN_EXTENT,
-                scalar2=0.5 * DILATION / GATE_TEMP,
+                scalar2=0.5 * DILATION * FEAT_TEMP / GATE_TEMP,
                 op0=ALU.max,
                 op1=ALU.mult,
             )
@@ -160,7 +156,38 @@ def tile_gaussianqueryassignment_kernel(
             nc.vector.scalar_tensor_tensor(
                 out=shift[:], in0=box[:, :, 0:3], scalar=-1.0, in1=rate[:], op0=ALU.mult, op1=ALU.mult
             )
-            nc.vector.tensor_scalar_add(out=presence_plus[:], in0=presence[:], scalar1=GATE_TEMP)
+
+        presence_gap = keep.tile([P, PAIRS], F32)
+        presence_max = keep.tile([P, PAIRS], F32)
+        background_shift = keep.tile([P, PAIRS, 1], F32)
+        background = keep.tile([P, PAIRS, TILES], F32)
+
+        def prepare_presence():
+            spread = psum.tile([P, PAIRS, P], BF16, tag="bank", name="spread")
+            for g in range(PAIRS):
+                nc.tensor.transpose(spread[:, g, :], presence[:, g : g + 1].to_broadcast([P, P]), ident_bf16[:])
+            nc.vector.tensor_reduce(out=presence_max[:], in_=spread[:], axis=mybir.AxisListType.X, op=ALU.max)
+            nc.vector.tensor_tensor(
+                out=background[:], in0=logs[:, 0], in1=logs[:, 1], op=ALU.subtract
+            )
+            nc.vector.tensor_tensor(out=presence_gap[:], in0=presence[:], in1=presence_max[:], op=ALU.subtract)
+            nc.vector.tensor_scalar(
+                out=background_shift[:, :, 0], in0=presence_max[:], scalar1=-1.0, scalar2=bg_bias[:, 0:1], op0=ALU.mult, op1=ALU.add
+            )
+            nc.vector.scalar_tensor_tensor(
+                out=background[:],
+                in0=background[:],
+                scalar=-KEEP_W,
+                in1=background_shift[:].to_broadcast([P, PAIRS, TILES]),
+                op0=ALU.mult,
+                op1=ALU.add,
+            )
+            nc.vector.tensor_scalar(
+                out=background[:], in0=background[:], scalar1=GATE_TEMP, scalar2=GAP_MAX, op0=ALU.subtract, op1=ALU.min
+            )
+
+        def background_exponentials():
+            nc.scalar.activation(out=background[:], in_=background[:], func=ACT.Exp)
 
         x_grouped, x_words, x_plane = {}, {}, {}
         y, square_sum, inv_norm = {}, {}, {}
@@ -172,23 +199,33 @@ def tile_gaussianqueryassignment_kernel(
         def is_pair(g):
             return 0 <= g < PAIRS
 
-        def transpose_inputs(u, half):
-            if not is_unit(u):
-                return
-            x_unit = xq if u == 0 else xg[:, u - 1]
-            if half == 0:
-                x_grouped[u] = work.tile([P, ROWS, PACK], BF16, tag="x_grouped", name="x_grouped", align_bytes=64)
-            grouped_pairs = x_grouped[u][:].bitcast(F32)
-            x_t = psum.tile([P, 2, 2, P], F32, tag="bank")
+        def turn(rows, half):
+            turned = psum.tile([P, 2, 2, P], F32, tag="bank", name="turned")
             for i in range(2):
-                x_pairs = x_unit[:, 2 * half + i, :].bitcast(F32)
+                row_pairs = rows[:, 2 * half + i, :].bitcast(F32)
                 for u2 in range(2):
-                    nc.tensor.transpose(x_t[:, i, u2, :], x_pairs[:, u2 : K // 2 : 2], ident_f32[:])
-            copy_out = nc.scalar.copy if half == 0 else nc.vector.tensor_copy
+                    nc.tensor.transpose(turned[:, i, u2, :], row_pairs[:, u2 : K // 2 : 2], ident_f32[:])
+            return turned
+
+        def lay_side_by_side(turned, grouped, half, copy_out):
+            grouped_pairs = grouped[:].bitcast(F32)
             copy_out(
                 out=grouped_pairs[:, 2 * P * half : 2 * P * (half + 1), :].rearrange("p (i r) u2 -> p i r u2", i=2),
-                in_=x_t[:].rearrange("p i u2 r -> p i r u2"),
+                in_=turned[:].rearrange("p i u2 r -> p i r u2"),
             )
+
+        x_turned, f_turned = {}, {}
+
+        def turn_inputs(u, half):
+            if is_unit(u):
+                x_turned[u, half] = turn(xq if u == 0 else xg[:, u - 1], half)
+
+        def group_inputs(u, half, copy_out):
+            if not is_unit(u):
+                return
+            if half == 0:
+                x_grouped[u] = work.tile([P, ROWS, PACK], BF16, tag="x_grouped", name="x_grouped", align_bytes=64)
+            lay_side_by_side(x_turned[u, half], x_grouped[u], half, copy_out)
 
         def quantise_inputs(u):
             if not is_unit(u):
@@ -218,7 +255,7 @@ def tile_gaussianqueryassignment_kernel(
                 stop=True,
             )
 
-        def add_bias_and_square(u, i):
+        def add_bias(u, i):
             if not is_unit(u):
                 return
             if i == 0:
@@ -227,41 +264,45 @@ def tile_gaussianqueryassignment_kernel(
             nc.vector.tensor_tensor(
                 out=y[u, i][:], in0=y_psum[u, i][:], in1=(bq_rows if u == 0 else bg_rows)[:], op=ALU.add
             )
-            squares = work.tile([P, D], BF16, tag="squares")
+
+        def square(u, i):
+            if not is_unit(u):
+                return
+            squares = work.tile([P, D], BF16, tag="squares", name="squares")
             nc.scalar.activation(
                 out=squares[:], in_=y[u, i][:], func=ACT.Square, accum_out=square_sum[u][:, i : i + 1]
             )
 
-        def normalise(u):
+        def inverse_norm(u):
             if not is_unit(u):
                 return
             inv_norm[u] = work.tile([P, TILES], F32, tag="inv_norm", name="inv_norm", bufs=UNITS)
             nc.gpsimd.tensor_scalar_max(out=inv_norm[u][:], in0=square_sum[u][:], scalar1=NORM_EPS * NORM_EPS)
             nc.gpsimd.tensor_tensor(out=inv_norm[u][:], in0=inv_norm[u][:], in1=minus_half[:], op=ALU.pow)
             f[u] = work.tile([P, TILES, D], BF16, tag="f", name="f", bufs=UNITS)
-            for i in range(TILES):
-                nc.gpsimd.tensor_scalar(
-                    out=f[u][:, i, :],
-                    in0=y[u, i][:],
-                    scalar1=inv_norm[u][:, i : i + 1],
-                    scalar2=0.0,
-                    op0=ALU.mult,
-                    op1=ALU.add,
-                )
 
-        def transpose_features(u, half):
+        def normalise(engine, u, i):
+            if not is_unit(u):
+                return
+            engine.tensor_scalar(
+                out=f[u][:, i, :],
+                in0=y[u, i][:],
+                scalar1=inv_norm[u][:, i : i + 1],
+                scalar2=0.0,
+                op0=ALU.mult,
+                op1=ALU.add,
+            )
+
+        def turn_features(u, half):
+            if is_unit(u):
+                f_turned[u, half] = turn(f[u], half)
+
+        def group_features(u, half, copy_out):
             if not is_unit(u):
                 return
             if half == 0:
                 f_grouped[u] = work.tile([P, ROWS, PACK], BF16, tag="f_grouped", name="f_grouped", align_bytes=64)
-            f_t = psum.tile([P, 2, PACK, P], BF16, tag="bank")
-            for i in range(2):
-                for t in range(PACK):
-                    nc.tensor.transpose(f_t[:, i, t, :], f[u][:, 2 * half + i, P * t : P * (t + 1)], ident_bf16[:])
-            nc.scalar.copy(
-                out=f_grouped[u][:, 2 * P * half : 2 * P * (half + 1), :].rearrange("p (i r) t -> p i r t", i=2),
-                in_=f_t[:].rearrange("p i t r -> p i r t"),
-            )
+            lay_side_by_side(f_turned[u, half], f_grouped[u], half, copy_out)
 
         def quantise_features(u):
             if not is_unit(u):
@@ -275,15 +316,14 @@ def tile_gaussianqueryassignment_kernel(
                 in_=f_grouped[u][:].rearrange("p r t -> p (r t)"),
             )
 
-        reach = {}
-        penalty = keep.tile([P, PAIRS, ROWS], F32)
+        reach, farthest = {}, {}
 
         def gate_reach(g, c):
             if not is_pair(g):
                 return
             if c == 0:
                 reach[g] = work.tile([P, 3, ROWS], F32, tag="reach", name="reach")
-            spread = psum.tile([P, TILES, P], BF16, tag="bank")
+            spread = psum.tile([P, TILES, P], BF16, tag="bank", name="spread")
             for j in range(TILES):
                 nc.tensor.transpose(
                     spread[:, j, :], position[:, g, j, c : c + 1].to_broadcast([P, P]), ident_bf16[:]
@@ -296,31 +336,27 @@ def tile_gaussianqueryassignment_kernel(
                 bias=shift[:, g, c : c + 1],
             )
 
-        def gate_penalty(g):
+        def gate_farthest(g, c):
             if not is_pair(g):
                 return
-            farthest = reach[g][:, 0, :]
-            nc.vector.tensor_tensor(out=farthest, in0=farthest, in1=reach[g][:, 1, :], op=ALU.max)
-            nc.vector.tensor_tensor(out=farthest, in0=farthest, in1=reach[g][:, 2, :], op=ALU.max)
-            nc.vector.tensor_scalar(
-                out=penalty[:, g, :],
-                in0=farthest,
-                scalar1=GATE_TEMP + GATE_CLIP,
-                scalar2=presence_plus[:, g : g + 1],
-                op0=ALU.min,
-                op1=ALU.subtract,
+            if c == 1:
+                farthest[g] = keep.tile([P, ROWS], F32, tag="farthest%d" % g, name="farthest")
+            nc.vector.tensor_tensor(
+                out=farthest[g][:], in0=(reach[g][:, 0, :] if c == 1 else farthest[g][:]), in1=reach[g][:, c, :], op=ALU.max
             )
 
-        logits_t, logits, neg_max, background_gap, probs, query_sum = {}, {}, {}, {}, {}, {}
+        penalty, weights, probs, row_sum, rows_t = {}, {}, {}, {}, {}
         out_rows = out.rearrange("b (t p j) c -> (b t) p (j c)", p=P, j=TILES)
+
+        sim = {}
 
         def similarity(g):
             if not is_pair(g):
                 return
             query_cols = slice(QUERIES * g, QUERIES * (g + 1))
-            sim = psum.tile([P, ROWS], F32, tag="bank")
+            sim[g] = psum.tile([P, ROWS], F32, tag="bank", name="sim")
             nc.tensor.matmul_mx(
-                out=sim[:],
+                out=sim[g][:],
                 lhsT=f_words[0][:, query_cols].bitcast(FP8X4),
                 lhsT_scale=f_plane[0][:, query_cols],
                 rhs=f_words[1 + g][:].bitcast(FP8X4),
@@ -328,81 +364,146 @@ def tile_gaussianqueryassignment_kernel(
                 start=True,
                 stop=True,
             )
-            logits_t[g] = work.tile([P, ROWS], F32, tag="logits_t", name="logits_t")
+
+        def exponentials(g):
+            if not is_pair(g):
+                return
+            penalty[g] = work.tile([P, ROWS], F32, tag="penalty", name="penalty")
             nc.vector.scalar_tensor_tensor(
-                out=logits_t[g][:], in0=sim[:], scalar=FEAT_TEMP, in1=penalty[:, g, :], op0=ALU.mult, op1=ALU.subtract
+                out=penalty[g][:],
+                in0=farthest[g][:],
+                scalar=(GATE_TEMP + GATE_CLIP) / FEAT_TEMP,
+                in1=sim[g][:],
+                op0=ALU.min,
+                op1=ALU.subtract,
+            )
+            weights[g] = work.tile([P, ROWS], F32, tag="weights", name="weights")
+            nc.scalar.activation(
+                out=weights[g][:], in_=penalty[g][:], func=ACT.Exp, scale=-FEAT_TEMP, bias=presence_gap[:, g : g + 1]
             )
 
         def rows_to_partitions(g):
             if not is_pair(g):
                 return
-            logits[g] = psum.tile([P, TILES, QUERIES], F32, tag="bank", name="logits")
+            row_sum[g] = psum.tile([P, TILES], F32, tag="bank", name="row_sum")
             for j in range(TILES):
-                nc.tensor.transpose(logits[g][:, j, :], logits_t[g][:, P * j : P * (j + 1)], ident_f32[:])
-
-        def row_maxima(g):
-            if not is_pair(g):
-                return
-            query_max = work.tile([P, TILES], F32, tag="query_max")
-            nc.vector.tensor_reduce(out=query_max[:], in_=logits[g][:], axis=mybir.AxisListType.X, op=ALU.max)
-            neg_max[g] = work.tile([P, TILES], F32, tag="neg_max", name="neg_max")
-            nc.vector.scalar_tensor_tensor(
-                out=neg_max[g][:], in0=query_max[:], scalar=-1.0, in1=neg_background[:, g, :], op0=ALU.mult, op1=ALU.min
-            )
-            background_gap[g] = work.tile([P, TILES, 1], F32, tag="background_gap", name="background_gap")
-            nc.vector.tensor_tensor(
-                out=background_gap[g][:, :, 0], in0=neg_background[:, g, :], in1=neg_max[g][:], op=ALU.subtract
-            )
-
-        def exponentials(g):
-            if not is_pair(g):
-                return
-            probs[g] = work.tile([P, TILES, CLASSES], F32, tag="probs", name="probs")
-            query_sum[g] = work.tile([P, TILES, 1], F32, tag="query_sum", name="query_sum")
-            for j in range(TILES):
-                nc.scalar.activation(
-                    out=probs[g][:, j, 1:CLASSES],
-                    in_=logits[g][:, j, :],
-                    func=ACT.Exp,
-                    bias=neg_max[g][:, j : j + 1],
-                    accum_out=query_sum[g][:, j, :],
+                nc.tensor.matmul(
+                    row_sum[g][:, j : j + 1], lhsT=weights[g][:, P * j : P * (j + 1)], rhs=ones[:], start=True, stop=True
                 )
-            nc.scalar.activation(out=probs[g][:, :, 0:1], in_=background_gap[g][:], func=ACT.Exp, scale=-1.0)
+            rows_t[g] = psum.tile([P, TILES, QUERIES], F32, tag="bank", name="rows_t")
+            for j in range(TILES):
+                nc.tensor.transpose(rows_t[g][:, j, :], weights[g][:, P * j : P * (j + 1)], ident_f32[:])
 
         def finish(g):
             if not is_pair(g):
                 return
-            total = work.tile([P, TILES, 1], F32, tag="total")
-            nc.vector.tensor_tensor(out=total[:], in0=query_sum[g][:], in1=probs[g][:, :, 0:1], op=ALU.add)
+            probs[g] = work.tile([P, TILES, CLASSES], F32, tag="probs", name="probs", bufs=PAIRS)
+            total = work.tile([P, TILES, 1], F32, tag="total", name="total")
+            nc.vector.tensor_tensor(out=total[:, :, 0], in0=row_sum[g][:], in1=background[:, g, :], op=ALU.add)
             nc.vector.reciprocal(out=total[:], in_=total[:])
+            nc.vector.tensor_tensor(out=probs[g][:, :, 0], in0=background[:, g, :], in1=total[:, :, 0], op=ALU.mult)
             nc.vector.tensor_tensor(
-                out=probs[g][:], in0=probs[g][:], in1=total[:].to_broadcast([P, TILES, CLASSES]), op=ALU.mult
+                out=probs[g][:, :, 1:CLASSES],
+                in0=rows_t[g][:],
+                in1=total[:].to_broadcast([P, TILES, QUERIES]),
+                op=ALU.mult,
             )
             nc.sync.dma_start(out=out_rows[g], in_=probs[g][:].rearrange("p j c -> p (j c)"))
 
+        def gate(g):
+            for c in range(3):
+                gate_reach(g, c)
+
+        def gate_max(g):
+            gate_farthest(g, 1)
+            gate_farthest(g, 2)
+
+        def project(u):
+            for i in range(TILES):
+                multiply(u, i)
+
+        def turn_both(turn_half, u):
+            turn_half(u, 0)
+            turn_half(u, 1)
+
+        def adds(u):
+            for i in range(TILES):
+                add_bias(u, i)
+
+        def squares(u):
+            for i in range(TILES):
+                square(u, i)
+
+        def features(u):
+            turn_both(turn_features, u)
+            group_features(u, 0, nc.scalar.copy)
+            group_features(u, 1, nc.scalar.copy)
+
+        def normalise_all(engine, u):
+            for i in range(TILES):
+                normalise(engine, u, i)
+
         with tc.manual_schedule():
-            for step in range(-2, UNITS):
-                ahead = step + 2
-                for i in range(TILES):
-                    multiply(step, i)
-                add_bias_and_square(step, 0)
-                add_bias_and_square(step, 1)
-                transpose_inputs(ahead, 0)
-                add_bias_and_square(step, 2)
-                transpose_inputs(ahead, 1)
-                add_bias_and_square(step, 3)
-                quantise_inputs(ahead)
-                normalise(step)
+            keep_logs()
             prepare_boxes()
-            for step in range(UNITS + 4):
-                transpose_features(step, 0)
-                transpose_features(step, 1)
-                for c in range(3):
-                    gate_reach(step, c)
-                finish(step - 4)
-                quantise_features(step - 1)
-                row_maxima(step - 3)
-                gate_penalty(step - 1)
-                similarity(step - 2)
-                rows_to_partitions(step - 2)
-                exponentials(step - 3)
+            prepare_presence()
+            background_exponentials()
+            gate(0)
+            turn_both(turn_inputs, 0)
+            group_inputs(0, 0, nc.vector.tensor_copy)
+            group_inputs(0, 1, nc.vector.tensor_copy)
+            quantise_inputs(0)
+            project(0)
+            turn_both(turn_inputs, 1)
+            adds(0)
+            squares(0)
+            inverse_norm(0)
+            normalise_all(nc.gpsimd, 0)
+            gate(1)
+            group_inputs(1, 0, nc.vector.tensor_copy)
+            group_inputs(1, 1, nc.vector.tensor_copy)
+            quantise_inputs(1)
+            project(1)
+            turn_both(turn_inputs, 2)
+            gate_max(0)
+            group_inputs(2, 0, nc.scalar.copy)
+            for r in range(1, UNITS):
+                adds(r)
+                squares(r)
+                inverse_norm(r)
+                if r < UNITS - 1:
+                    normalise_all(nc.gpsimd, r)
+                group_inputs(r + 1, 1, nc.vector.tensor_copy)
+                quantise_inputs(r + 1)
+                turn_both(turn_inputs, r + 2)
+                group_inputs(r + 2, 0, nc.scalar.copy)
+                project(r + 1)
+                features(r - 1)
+                if r == 1:
+                    gate_max(1)
+                quantise_features(r - 2)
+                if r == UNITS - 2:
+                    similarity(0)
+            similarity(1)
+            exponentials(0)
+            quantise_features(3)
+            exponentials(1)
+            normalise_all(nc.vector, 4)
+            gate(2)
+            features(4)
+            gate_max(2)
+            similarity(2)
+            gate(3)
+            exponentials(2)
+            quantise_features(4)
+            rows_to_partitions(0)
+            rows_to_partitions(1)
+            similarity(3)
+            finish(0)
+            gate_max(3)
+            exponentials(3)
+            finish(1)
+            rows_to_partitions(2)
+            rows_to_partitions(3)
+            finish(2)
+            finish(3)

@@ -385,21 +385,27 @@ def tile_gaussianqueryassignment_kernel(
         def rows_to_partitions(g):
             if not is_pair(g):
                 return
+            rows_t[g] = psum.tile([P, TILES, QUERIES], F32, tag="bank", name="rows_t")
+            for j in range(TILES):
+                nc.tensor.transpose(rows_t[g][:, j, :], weights[g][:, P * j : P * (j + 1)], ident_f32[:])
+
+        def sum_queries(g):
             row_sum[g] = psum.tile([P, TILES], F32, tag="bank", name="row_sum")
             for j in range(TILES):
                 nc.tensor.matmul(
                     row_sum[g][:, j : j + 1], lhsT=weights[g][:, P * j : P * (j + 1)], rhs=ones[:], start=True, stop=True
                 )
-            rows_t[g] = psum.tile([P, TILES, QUERIES], F32, tag="bank", name="rows_t")
-            for j in range(TILES):
-                nc.tensor.transpose(rows_t[g][:, j, :], weights[g][:, P * j : P * (j + 1)], ident_f32[:])
 
         def finish(g):
             if not is_pair(g):
                 return
             probs[g] = work.tile([P, TILES, CLASSES], F32, tag="probs", name="probs", bufs=PAIRS)
             total = work.tile([P, TILES, 1], F32, tag="total", name="total")
-            nc.vector.tensor_tensor(out=total[:, :, 0], in0=row_sum[g][:], in1=background[:, g, :], op=ALU.add)
+            if g in row_sum:
+                nc.vector.tensor_tensor(out=total[:, :, 0], in0=row_sum[g][:], in1=background[:, g, :], op=ALU.add)
+            else:
+                nc.vector.tensor_reduce(out=total[:, :, 0], in_=rows_t[g][:], axis=mybir.AxisListType.X, op=ALU.add)
+                nc.vector.tensor_tensor(out=total[:, :, 0], in0=total[:, :, 0], in1=background[:, g, :], op=ALU.add)
             nc.vector.reciprocal(out=total[:], in_=total[:])
             nc.vector.tensor_tensor(out=probs[g][:, :, 0], in0=background[:, g, :], in1=total[:, :, 0], op=ALU.mult)
             nc.vector.tensor_tensor(
@@ -413,10 +419,6 @@ def tile_gaussianqueryassignment_kernel(
         def gate(g):
             for c in range(3):
                 gate_reach(g, c)
-
-        def gate_max(g):
-            gate_farthest(g, 1)
-            gate_farthest(g, 2)
 
         def project(u):
             for i in range(TILES):
@@ -434,10 +436,10 @@ def tile_gaussianqueryassignment_kernel(
             for i in range(TILES):
                 square(u, i)
 
-        def features(u):
+        def turn_and_group_features(u, engine_1=nc.scalar.copy):
             turn_both(turn_features, u)
             group_features(u, 0, nc.scalar.copy)
-            group_features(u, 1, nc.scalar.copy)
+            group_features(u, 1, engine_1)
 
         def normalise_all(engine, u):
             for i in range(TILES):
@@ -447,62 +449,104 @@ def tile_gaussianqueryassignment_kernel(
             keep_logs()
             prepare_boxes()
             prepare_presence()
-            background_exponentials()
             gate(0)
+            background_exponentials()
             turn_both(turn_inputs, 0)
             group_inputs(0, 0, nc.vector.tensor_copy)
             group_inputs(0, 1, nc.vector.tensor_copy)
+            gate(1)
             quantise_inputs(0)
-            project(0)
             turn_both(turn_inputs, 1)
+            group_inputs(1, 0, nc.scalar.copy)
+            project(0)
+            gate_farthest(0, 1)
+            group_inputs(1, 1, nc.vector.tensor_copy)
+            gate_reach(2, 0)
+            gate_reach(2, 1)
             adds(0)
             squares(0)
             inverse_norm(0)
             normalise_all(nc.gpsimd, 0)
-            gate(1)
-            group_inputs(1, 0, nc.vector.tensor_copy)
-            group_inputs(1, 1, nc.vector.tensor_copy)
             quantise_inputs(1)
+            gate_farthest(0, 2)
             project(1)
             turn_both(turn_inputs, 2)
-            gate_max(0)
             group_inputs(2, 0, nc.scalar.copy)
-            for r in range(1, UNITS):
-                adds(r)
-                squares(r)
-                inverse_norm(r)
-                if r < UNITS - 1:
-                    normalise_all(nc.gpsimd, r)
-                group_inputs(r + 1, 1, nc.vector.tensor_copy)
-                quantise_inputs(r + 1)
-                turn_both(turn_inputs, r + 2)
-                group_inputs(r + 2, 0, nc.scalar.copy)
-                project(r + 1)
-                features(r - 1)
-                if r == 1:
-                    gate_max(1)
-                quantise_features(r - 2)
-                if r == UNITS - 2:
-                    similarity(0)
-            similarity(1)
+            adds(1)
+            squares(1)
+            inverse_norm(1)
+            normalise_all(nc.gpsimd, 1)
+            group_inputs(2, 1, nc.vector.tensor_copy)
+            quantise_inputs(2)
+            turn_both(turn_inputs, 3)
+            group_inputs(3, 0, nc.scalar.copy)
+            gate_farthest(1, 1)
+            project(2)
+            group_inputs(3, 1, nc.vector.tensor_copy)
+            turn_and_group_features(0)
+            turn_both(turn_inputs, 4)
+            add_bias(2, 0)
+            add_bias(2, 1)
+            quantise_inputs(3)
+            project(3)
+            add_bias(2, 2)
+            add_bias(2, 3)
+            squares(2)
+            inverse_norm(2)
+            normalise_all(nc.gpsimd, 2)
+            group_inputs(4, 0, nc.scalar.copy)
+            group_inputs(4, 1, nc.vector.tensor_copy)
+            add_bias(3, 0)
+            add_bias(3, 1)
+            turn_and_group_features(1)
+            quantise_inputs(4)
+            project(4)
+            add_bias(3, 2)
+            add_bias(3, 3)
+            squares(3)
+            inverse_norm(3)
+            normalise(nc.gpsimd, 3, 0)
+            normalise(nc.gpsimd, 3, 1)
+            quantise_features(0)
+            adds(4)
+            squares(4)
+            inverse_norm(4)
+            quantise_features(1)
+            turn_and_group_features(2)
+            gate_reach(2, 2)
+            similarity(0)
+            gate_farthest(1, 2)
+            normalise(nc.vector, 3, 2)
+            normalise(nc.vector, 3, 3)
+            gate_farthest(2, 1)
+            turn_and_group_features(3)
+            quantise_features(2)
+            normalise_all(nc.vector, 4)
             exponentials(0)
+            gate_reach(3, 0)
+            turn_both(turn_features, 4)
+            similarity(1)
+            group_features(4, 0, nc.scalar.copy)
+            gate_reach(3, 1)
+            group_features(4, 1, nc.vector.tensor_copy)
             quantise_features(3)
             exponentials(1)
-            normalise_all(nc.vector, 4)
-            gate(2)
-            features(4)
-            gate_max(2)
-            similarity(2)
-            gate(3)
-            exponentials(2)
             quantise_features(4)
+            gate_reach(3, 2)
+            sum_queries(0)
             rows_to_partitions(0)
+            similarity(2)
+            gate_farthest(2, 2)
+            exponentials(2)
+            finish(0)
+            sum_queries(1)
             rows_to_partitions(1)
             similarity(3)
-            finish(0)
-            gate_max(3)
+            gate_farthest(3, 1)
+            gate_farthest(3, 2)
             exponentials(3)
             finish(1)
+            sum_queries(2)
             rows_to_partitions(2)
             rows_to_partitions(3)
             finish(2)

@@ -66,8 +66,11 @@ def tile_gaussianqueryassignment_kernel(
         make_identity(nc, ident_f32[:])
         ident_bf16 = keep.tile([P, P], BF16)
         make_identity(nc, ident_bf16[:])
-        minus_half = keep.tile([P, TILES], F32)
-        nc.gpsimd.memset(minus_half[:], -0.5)
+        warm = keep.tile([P, 1], F32)
+
+        def load_root_table():
+            nc.scalar.activation(out=warm[:], in_=ones[:], func=ACT.Abs_reciprocal_sqrt)
+
         ones = keep.tile([P, 1], F32)
         nc.gpsimd.memset(ones[:], 1.0)
 
@@ -97,8 +100,8 @@ def tile_gaussianqueryassignment_kernel(
             nc.sync.dma_start(out=xg[:, g, :, 0:AFFINITY], in_=affinity_in[g])
             nc.sync.dma_start(out=xg[:, g, :, AFFINITY:K], in_=motion_in[g])
 
-        keep_in = keep.tile([P, PAIRS, TILES], BF16)
-        nc.sync.dma_start(out=keep_in[:], in_=keep_score.rearrange("b t (p j) -> p (b t) j", j=TILES))
+        xq = keep.tile([P, PAIRS, K], BF16)
+        nc.sync.dma_start(out=xq[:], in_=query_feat.rearrange("b t m k -> m (b t) k"))
         position = keep.tile([P, PAIRS, TILES, 3], BF16)
         nc.sync.dma_start(
             out=position[:].rearrange("p g j c -> p g (j c)"),
@@ -106,35 +109,36 @@ def tile_gaussianqueryassignment_kernel(
         )
         box = keep.tile([P, PAIRS, 7], BF16)
         nc.sync.dma_start(out=box[:], in_=query_box3d.rearrange("b t m c -> m (b t) c"))
+        load_weight(Wq_words, Wq_scales, wq_words, wq_plane)
+        bq_rows = keep.tile([P, D], BF16)
+        nc.sync.dma_start(out=bq_rows[:], in_=bq.partition_broadcast(P))
+        load_gaussians(0)
+        load_weight(Wg_words, Wg_scales, wg_words, wg_plane)
+        bg_rows = keep.tile([P, D], BF16)
+        nc.sync.dma_start(out=bg_rows[:], in_=bg.partition_broadcast(P))
+        load_gaussians(1)
+        keep_in = keep.tile([P, PAIRS, TILES], BF16)
+        nc.sync.dma_start(out=keep_in[:], in_=keep_score.rearrange("b t (p j) -> p (b t) j", j=TILES))
         presence = keep.tile([P, PAIRS], BF16)
         with nc.allow_non_contiguous_dma(reason="512 two-byte elements, one query to a partition"):
             nc.sync.dma_start(out=presence[:], in_=presence_logit.rearrange("b t m -> m (b t)"))
         bg_bias = keep.tile([P, 1], BF16)
         nc.sync.dma_start(out=bg_bias[:], in_=background_bias.partition_broadcast(P))
-        xq = keep.tile([P, PAIRS, K], BF16)
-        nc.sync.dma_start(out=xq[:], in_=query_feat.rearrange("b t m k -> m (b t) k"))
-        load_weight(Wq_words, Wq_scales, wq_words, wq_plane)
-        load_gaussians(0)
-        bq_rows = keep.tile([P, D], BF16)
-        nc.sync.dma_start(out=bq_rows[:], in_=bq.partition_broadcast(P))
-        load_weight(Wg_words, Wg_scales, wg_words, wg_plane)
-        bg_rows = keep.tile([P, D], BF16)
-        nc.sync.dma_start(out=bg_rows[:], in_=bg.partition_broadcast(P))
-        load_gaussians(1)
         load_gaussians(2)
         load_gaussians(3)
 
-        k_and_rest = keep.tile([P, 2, PAIRS, TILES], F32)
-        logs = keep.tile([P, 2, PAIRS, TILES], F32)
+        kept = keep.tile([P, PAIRS, TILES], F32)
+        odds = keep.tile([P, PAIRS, TILES], F32)
+        keep_factor = keep.tile([P, PAIRS, TILES], F32)
 
-        def keep_logs():
+        def prepare_keeps():
             nc.vector.tensor_scalar(
-                out=k_and_rest[:, 0], in0=keep_in[:], scalar1=KEEP_EPS, scalar2=1.0 - KEEP_EPS, op0=ALU.max, op1=ALU.min
+                out=kept[:], in0=keep_in[:], scalar1=KEEP_EPS, scalar2=1.0 - KEEP_EPS, op0=ALU.max, op1=ALU.min
             )
-            nc.vector.tensor_scalar(
-                out=k_and_rest[:, 1], in0=k_and_rest[:, 0], scalar1=-1.0, scalar2=1.0, op0=ALU.mult, op1=ALU.add
-            )
-            nc.scalar.activation(out=logs[:], in_=k_and_rest[:], func=ACT.Ln)
+            nc.vector.tensor_scalar(out=odds[:], in0=kept[:], scalar1=-1.0, scalar2=1.0, op0=ALU.mult, op1=ALU.add)
+            nc.vector.reciprocal(out=odds[:], in_=odds[:])
+            nc.vector.tensor_tensor(out=odds[:], in0=odds[:], in1=kept[:], op=ALU.mult)
+            nc.scalar.activation(out=keep_factor[:], in_=odds[:], func=ACT.Abs_reciprocal_sqrt)
 
         size = keep.tile([P, PAIRS, 3], F32)
         rate = keep.tile([P, PAIRS, 3], F32)
@@ -159,7 +163,7 @@ def tile_gaussianqueryassignment_kernel(
 
         presence_gap = keep.tile([P, PAIRS], F32)
         presence_max = keep.tile([P, PAIRS], F32)
-        background_shift = keep.tile([P, PAIRS, 1], F32)
+        background_gap = keep.tile([P, PAIRS, 1], F32)
         background = keep.tile([P, PAIRS, TILES], F32)
 
         def prepare_presence():
@@ -167,27 +171,33 @@ def tile_gaussianqueryassignment_kernel(
             for g in range(PAIRS):
                 nc.tensor.transpose(spread[:, g, :], presence[:, g : g + 1].to_broadcast([P, P]), ident_bf16[:])
             nc.vector.tensor_reduce(out=presence_max[:], in_=spread[:], axis=mybir.AxisListType.X, op=ALU.max)
-            nc.vector.tensor_tensor(
-                out=background[:], in0=logs[:, 0], in1=logs[:, 1], op=ALU.subtract
-            )
             nc.vector.tensor_tensor(out=presence_gap[:], in0=presence[:], in1=presence_max[:], op=ALU.subtract)
             nc.vector.tensor_scalar(
-                out=background_shift[:, :, 0], in0=presence_max[:], scalar1=-1.0, scalar2=bg_bias[:, 0:1], op0=ALU.mult, op1=ALU.add
-            )
-            nc.vector.scalar_tensor_tensor(
-                out=background[:],
-                in0=background[:],
-                scalar=-KEEP_W,
-                in1=background_shift[:].to_broadcast([P, PAIRS, TILES]),
+                out=background_gap[:, :, 0],
+                in0=presence_max[:],
+                scalar1=-1.0,
+                scalar2=bg_bias[:, 0:1],
                 op0=ALU.mult,
                 op1=ALU.add,
             )
             nc.vector.tensor_scalar(
-                out=background[:], in0=background[:], scalar1=GATE_TEMP, scalar2=GAP_MAX, op0=ALU.subtract, op1=ALU.min
+                out=background_gap[:], in0=background_gap[:], scalar1=GATE_TEMP, scalar2=GAP_MAX, op0=ALU.subtract, op1=ALU.min
             )
 
+        def hold_exponentials():
+            for gap in (presence_gap[:], background_gap[:, :, 0]):
+                nc.vector.scalar_tensor_tensor(
+                    out=gap, in0=inv_norm[UNITS - 1][:], scalar=0.0, in1=gap, op0=ALU.mult, op1=ALU.add
+                )
+
         def background_exponentials():
-            nc.scalar.activation(out=background[:], in_=background[:], func=ACT.Exp)
+            nc.scalar.activation(out=background_gap[:], in_=background_gap[:], func=ACT.Exp)
+            nc.vector.tensor_tensor(
+                out=background[:],
+                in0=keep_factor[:],
+                in1=background_gap[:].to_broadcast([P, PAIRS, TILES]),
+                op=ALU.mult,
+            )
 
         x_grouped, x_words, x_plane = {}, {}, {}
         y, square_sum, inv_norm = {}, {}, {}
@@ -199,12 +209,12 @@ def tile_gaussianqueryassignment_kernel(
         def is_pair(g):
             return 0 <= g < PAIRS
 
-        def turn(rows, half):
+        def turn(rows, half, pairs_of):
             turned = psum.tile([P, 2, 2, P], F32, tag="bank", name="turned")
             for i in range(2):
                 row_pairs = rows[:, 2 * half + i, :].bitcast(F32)
                 for u2 in range(2):
-                    nc.tensor.transpose(turned[:, i, u2, :], row_pairs[:, u2 : K // 2 : 2], ident_f32[:])
+                    nc.tensor.transpose(turned[:, i, u2, :], row_pairs[:, pairs_of[u2]], ident_f32[:])
             return turned
 
         def lay_side_by_side(turned, grouped, half, copy_out):
@@ -218,7 +228,7 @@ def tile_gaussianqueryassignment_kernel(
 
         def turn_inputs(u, half):
             if is_unit(u):
-                x_turned[u, half] = turn(xq if u == 0 else xg[:, u - 1], half)
+                x_turned[u, half] = turn(xq if u == 0 else xg[:, u - 1], half, (slice(0, 255, 2), slice(1, 256, 2)))
 
         def group_inputs(u, half, copy_out):
             if not is_unit(u):
@@ -277,8 +287,12 @@ def tile_gaussianqueryassignment_kernel(
             if not is_unit(u):
                 return
             inv_norm[u] = work.tile([P, TILES], F32, tag="inv_norm", name="inv_norm", bufs=UNITS)
-            nc.gpsimd.tensor_scalar_max(out=inv_norm[u][:], in0=square_sum[u][:], scalar1=NORM_EPS * NORM_EPS)
-            nc.gpsimd.tensor_tensor(out=inv_norm[u][:], in0=inv_norm[u][:], in1=minus_half[:], op=ALU.pow)
+            nc.scalar.activation(out=inv_norm[u][:], in_=square_sum[u][:], func=ACT.Abs_reciprocal_sqrt)
+
+        def clip_inverse_norm(engine, u):
+            if not is_unit(u):
+                return
+            engine.tensor_scalar_min(out=inv_norm[u][:], in0=inv_norm[u][:], scalar1=1.0 / NORM_EPS)
             f[u] = work.tile([P, TILES, D], BF16, tag="f", name="f", bufs=UNITS)
 
         def normalise(engine, u, i):
@@ -295,7 +309,7 @@ def tile_gaussianqueryassignment_kernel(
 
         def turn_features(u, half):
             if is_unit(u):
-                f_turned[u, half] = turn(f[u], half)
+                f_turned[u, half] = turn(f[u], half, (slice(0, P), slice(P, 2 * P)))
 
         def group_features(u, half, copy_out):
             if not is_unit(u):
@@ -322,7 +336,7 @@ def tile_gaussianqueryassignment_kernel(
             if not is_pair(g):
                 return
             if c == 0:
-                reach[g] = work.tile([P, 3, ROWS], F32, tag="reach", name="reach")
+                reach[g] = work.tile([P, 3, ROWS], F32, tag="reach", name="reach", bufs=PAIRS)
             spread = psum.tile([P, TILES, P], BF16, tag="bank", name="spread")
             for j in range(TILES):
                 nc.tensor.transpose(
@@ -365,10 +379,10 @@ def tile_gaussianqueryassignment_kernel(
                 stop=True,
             )
 
-        def exponentials(g):
+        def penalties(g):
             if not is_pair(g):
                 return
-            penalty[g] = work.tile([P, ROWS], F32, tag="penalty", name="penalty")
+            penalty[g] = work.tile([P, ROWS], F32, tag="penalty", name="penalty", bufs=PAIRS)
             nc.vector.scalar_tensor_tensor(
                 out=penalty[g][:],
                 in0=farthest[g][:],
@@ -377,7 +391,11 @@ def tile_gaussianqueryassignment_kernel(
                 op0=ALU.min,
                 op1=ALU.subtract,
             )
-            weights[g] = work.tile([P, ROWS], F32, tag="weights", name="weights")
+
+        def exponentials(g):
+            if not is_pair(g):
+                return
+            weights[g] = work.tile([P, ROWS], F32, tag="weights", name="weights", bufs=PAIRS)
             nc.scalar.activation(
                 out=weights[g][:], in_=penalty[g][:], func=ACT.Exp, scale=-FEAT_TEMP, bias=presence_gap[:, g : g + 1]
             )
@@ -396,7 +414,7 @@ def tile_gaussianqueryassignment_kernel(
                     row_sum[g][:, j : j + 1], lhsT=weights[g][:, P * j : P * (j + 1)], rhs=ones[:], start=True, stop=True
                 )
 
-        def finish(g):
+        def finish(g, on_scalar=False):
             if not is_pair(g):
                 return
             probs[g] = work.tile([P, TILES, CLASSES], F32, tag="probs", name="probs", bufs=PAIRS)
@@ -408,17 +426,31 @@ def tile_gaussianqueryassignment_kernel(
                 nc.vector.tensor_tensor(out=total[:, :, 0], in0=total[:, :, 0], in1=background[:, g, :], op=ALU.add)
             nc.vector.reciprocal(out=total[:], in_=total[:])
             nc.vector.tensor_tensor(out=probs[g][:, :, 0], in0=background[:, g, :], in1=total[:, :, 0], op=ALU.mult)
-            nc.vector.tensor_tensor(
-                out=probs[g][:, :, 1:CLASSES],
-                in0=rows_t[g][:],
-                in1=total[:].to_broadcast([P, TILES, QUERIES]),
-                op=ALU.mult,
-            )
+            if on_scalar:
+                for j in range(TILES):
+                    nc.scalar.activation(
+                        out=probs[g][:, j, 1:CLASSES], in_=rows_t[g][:, j, :], func=ACT.Copy, scale=total[:, j, :]
+                    )
+            else:
+                nc.vector.tensor_tensor(
+                    out=probs[g][:, :, 1:CLASSES],
+                    in0=rows_t[g][:],
+                    in1=total[:].to_broadcast([P, TILES, QUERIES]),
+                    op=ALU.mult,
+                )
             nc.sync.dma_start(out=out_rows[g], in_=probs[g][:].rearrange("p j c -> p (j c)"))
 
         def gate(g):
             for c in range(3):
                 gate_reach(g, c)
+
+        def gate_max(g):
+            gate_farthest(g, 1)
+            gate_farthest(g, 2)
+
+        def gate_max(g):
+            gate_farthest(g, 1)
+            gate_farthest(g, 2)
 
         def project(u):
             for i in range(TILES):
@@ -436,118 +468,122 @@ def tile_gaussianqueryassignment_kernel(
             for i in range(TILES):
                 square(u, i)
 
-        def turn_and_group_features(u, engine_1=nc.scalar.copy):
-            turn_both(turn_features, u)
+        def group_both_inputs(u, copy_out):
+            group_inputs(u, 0, copy_out)
+            group_inputs(u, 1, copy_out)
+
+        def group_both_features(u):
             group_features(u, 0, nc.scalar.copy)
-            group_features(u, 1, engine_1)
+            group_features(u, 1, nc.scalar.copy)
 
         def normalise_all(engine, u):
             for i in range(TILES):
                 normalise(engine, u, i)
 
-        with tc.manual_schedule():
-            keep_logs()
-            prepare_boxes()
-            prepare_presence()
-            gate(0)
-            background_exponentials()
-            turn_both(turn_inputs, 0)
-            group_inputs(0, 0, nc.vector.tensor_copy)
-            group_inputs(0, 1, nc.vector.tensor_copy)
-            gate(1)
-            quantise_inputs(0)
-            turn_both(turn_inputs, 1)
-            group_inputs(1, 0, nc.scalar.copy)
-            project(0)
-            gate_farthest(0, 1)
-            group_inputs(1, 1, nc.vector.tensor_copy)
-            gate_reach(2, 0)
-            gate_reach(2, 1)
-            adds(0)
-            squares(0)
-            inverse_norm(0)
-            normalise_all(nc.gpsimd, 0)
-            quantise_inputs(1)
-            gate_farthest(0, 2)
-            project(1)
-            turn_both(turn_inputs, 2)
-            group_inputs(2, 0, nc.scalar.copy)
-            adds(1)
-            squares(1)
-            inverse_norm(1)
-            normalise_all(nc.gpsimd, 1)
-            group_inputs(2, 1, nc.vector.tensor_copy)
-            quantise_inputs(2)
-            turn_both(turn_inputs, 3)
-            group_inputs(3, 0, nc.scalar.copy)
-            gate_farthest(1, 1)
-            project(2)
-            group_inputs(3, 1, nc.vector.tensor_copy)
-            turn_and_group_features(0)
-            turn_both(turn_inputs, 4)
-            add_bias(2, 0)
-            add_bias(2, 1)
-            quantise_inputs(3)
-            project(3)
-            add_bias(2, 2)
-            add_bias(2, 3)
-            squares(2)
-            inverse_norm(2)
-            normalise_all(nc.gpsimd, 2)
-            group_inputs(4, 0, nc.scalar.copy)
-            group_inputs(4, 1, nc.vector.tensor_copy)
-            add_bias(3, 0)
-            add_bias(3, 1)
-            turn_and_group_features(1)
-            quantise_inputs(4)
-            project(4)
-            add_bias(3, 2)
-            add_bias(3, 3)
-            squares(3)
-            inverse_norm(3)
-            normalise(nc.gpsimd, 3, 0)
-            normalise(nc.gpsimd, 3, 1)
-            quantise_features(0)
-            adds(4)
-            squares(4)
-            inverse_norm(4)
-            quantise_features(1)
-            turn_and_group_features(2)
-            gate_reach(2, 2)
-            similarity(0)
-            gate_farthest(1, 2)
-            normalise(nc.vector, 3, 2)
-            normalise(nc.vector, 3, 3)
-            gate_farthest(2, 1)
-            turn_and_group_features(3)
-            quantise_features(2)
-            normalise_all(nc.vector, 4)
-            exponentials(0)
-            gate_reach(3, 0)
-            turn_both(turn_features, 4)
-            similarity(1)
-            group_features(4, 0, nc.scalar.copy)
-            gate_reach(3, 1)
-            group_features(4, 1, nc.vector.tensor_copy)
-            quantise_features(3)
-            exponentials(1)
-            quantise_features(4)
-            gate_reach(3, 2)
-            sum_queries(0)
-            rows_to_partitions(0)
-            similarity(2)
-            gate_farthest(2, 2)
-            exponentials(2)
-            finish(0)
-            sum_queries(1)
-            rows_to_partitions(1)
-            similarity(3)
-            gate_farthest(3, 1)
-            gate_farthest(3, 2)
-            exponentials(3)
-            finish(1)
-            sum_queries(2)
-            rows_to_partitions(2)
-            rows_to_partitions(3)
-            finish(2)
-            finish(3)
+        def norm(engine, u):
+            inverse_norm(u)
+            clip_inverse_norm(engine, u)
+            normalise_all(engine, u)
+
+        load_root_table()
+        turn_both(turn_inputs, 0)
+        group_inputs(0, 0, nc.scalar.copy)
+        group_inputs(0, 1, nc.vector.tensor_copy)
+        quantise_inputs(0)
+        prepare_boxes()
+        gate(0)
+        project(0)
+        adds(0)
+        turn_both(turn_inputs, 1)
+        square(0, 0)
+        square(0, 1)
+        group_inputs(1, 0, nc.scalar.copy)
+        group_inputs(1, 1, nc.vector.tensor_copy)
+        square(0, 2)
+        square(0, 3)
+        norm(nc.gpsimd, 0)
+        quantise_inputs(1)
+        gate_max(0)
+        project(1)
+        turn_both(turn_inputs, 2)
+        adds(1)
+        square(1, 0)
+        square(1, 1)
+        group_inputs(2, 0, nc.scalar.copy)
+        group_inputs(2, 1, nc.vector.tensor_copy)
+        square(1, 2)
+        square(1, 3)
+        norm(nc.gpsimd, 1)
+        quantise_inputs(2)
+        turn_both(turn_inputs, 3)
+        prepare_keeps()
+        project(2)
+        prepare_presence()
+        group_inputs(3, 0, nc.scalar.copy)
+        turn_both(turn_features, 0)
+        group_both_features(0)
+        turn_both(turn_inputs, 4)
+        adds(2)
+        group_inputs(3, 1, nc.vector.tensor_copy)
+        quantise_inputs(3)
+        project(3)
+        squares(2)
+        norm(nc.gpsimd, 2)
+        group_inputs(4, 0, nc.scalar.copy)
+        group_inputs(4, 1, nc.vector.tensor_copy)
+        gate(1)
+        adds(3)
+        turn_both(turn_features, 1)
+        group_both_features(1)
+        quantise_inputs(4)
+        project(4)
+        squares(3)
+        norm(nc.gpsimd, 3)
+        quantise_features(0)
+        gate_farthest(1, 1)
+        adds(4)
+        squares(4)
+        inverse_norm(4)
+        quantise_features(1)
+        turn_both(turn_features, 2)
+        group_both_features(2)
+        similarity(0)
+        gate_farthest(1, 2)
+        clip_inverse_norm(nc.vector, 4)
+        hold_exponentials()
+        normalise_all(nc.vector, 4)
+        turn_both(turn_features, 4)
+        background_exponentials()
+        turn_both(turn_features, 3)
+        quantise_features(2)
+        penalties(0)
+        similarity(1)
+        group_features(4, 0, nc.scalar.copy)
+        group_features(4, 1, nc.vector.tensor_copy)
+        group_both_features(3)
+        exponentials(0)
+        quantise_features(4)
+        quantise_features(3)
+        gate(2)
+        penalties(1)
+        exponentials(1)
+        gate_max(2)
+        similarity(2)
+        gate(3)
+        penalties(2)
+        exponentials(2)
+        similarity(3)
+        sum_queries(0)
+        rows_to_partitions(0)
+        gate_max(3)
+        penalties(3)
+        exponentials(3)
+        finish(0)
+        sum_queries(1)
+        rows_to_partitions(1)
+        finish(1)
+        sum_queries(2)
+        rows_to_partitions(2)
+        rows_to_partitions(3)
+        finish(2)
+        finish(3)

@@ -22,6 +22,7 @@ K = 512
 AFFINITY = 384
 D = 512
 CLASSES = QUERIES + 1
+ALL_TILES = tuple(range(TILES))
 UNITS = 1 + PAIRS
 
 DILATION = 1.5
@@ -101,7 +102,11 @@ def tile_gaussianqueryassignment_kernel(
             nc.sync.dma_start(out=xg[:, g, :, AFFINITY:K], in_=motion_in[g])
 
         xq = keep.tile([P, PAIRS, K], BF16)
-        nc.sync.dma_start(out=xq[:], in_=query_feat.rearrange("b t m k -> m (b t) k"))
+        for first in range(0, PAIRS, 2):
+            nc.sync.dma_start(
+                out=xq[:, first : first + 2, :],
+                in_=query_feat.rearrange("b t m k -> m (b t) k")[:, first : first + 2, :],
+            )
         position = keep.tile([P, PAIRS, TILES, 3], BF16)
         nc.sync.dma_start(
             out=position[:].rearrange("p g j c -> p g (j c)"),
@@ -192,6 +197,8 @@ def tile_gaussianqueryassignment_kernel(
 
         def background_exponentials():
             nc.scalar.activation(out=background_gap[:], in_=background_gap[:], func=ACT.Exp)
+
+        def background_terms():
             nc.vector.tensor_tensor(
                 out=background[:],
                 in0=keep_factor[:],
@@ -283,17 +290,16 @@ def tile_gaussianqueryassignment_kernel(
                 out=squares[:], in_=y[u, i][:], func=ACT.Square, accum_out=square_sum[u][:, i : i + 1]
             )
 
-        def inverse_norm(u):
-            if not is_unit(u):
-                return
-            inv_norm[u] = work.tile([P, TILES], F32, tag="inv_norm", name="inv_norm", bufs=UNITS)
-            nc.scalar.activation(out=inv_norm[u][:], in_=square_sum[u][:], func=ACT.Abs_reciprocal_sqrt)
+        def inverse_norm(u, tiles=ALL_TILES):
+            cols = slice(tiles[0], tiles[-1] + 1)
+            if u not in inv_norm:
+                inv_norm[u] = work.tile([P, TILES], F32, tag="inv_norm", name="inv_norm", bufs=UNITS)
+                f[u] = work.tile([P, TILES, D], BF16, tag="f", name="f", bufs=UNITS)
+            nc.scalar.activation(out=inv_norm[u][:, cols], in_=square_sum[u][:, cols], func=ACT.Abs_reciprocal_sqrt)
 
-        def clip_inverse_norm(engine, u):
-            if not is_unit(u):
-                return
-            engine.tensor_scalar_min(out=inv_norm[u][:], in0=inv_norm[u][:], scalar1=1.0 / NORM_EPS)
-            f[u] = work.tile([P, TILES, D], BF16, tag="f", name="f", bufs=UNITS)
+        def clip_inverse_norm(engine, u, tiles=ALL_TILES):
+            cols = slice(tiles[0], tiles[-1] + 1)
+            engine.tensor_scalar_min(out=inv_norm[u][:, cols], in0=inv_norm[u][:, cols], scalar1=1.0 / NORM_EPS)
 
         def normalise(engine, u, i):
             if not is_unit(u):
@@ -359,7 +365,7 @@ def tile_gaussianqueryassignment_kernel(
                 out=farthest[g][:], in0=(reach[g][:, 0, :] if c == 1 else farthest[g][:]), in1=reach[g][:, c, :], op=ALU.max
             )
 
-        penalty, weights, probs, row_sum, rows_t = {}, {}, {}, {}, {}
+        penalty, weights, probs, rows_t = {}, {}, {}, {}
         out_rows = out.rearrange("b (t p j) c -> (b t) p (j c)", p=P, j=TILES)
 
         sim = {}
@@ -379,66 +385,67 @@ def tile_gaussianqueryassignment_kernel(
                 stop=True,
             )
 
-        def penalties(g):
-            if not is_pair(g):
-                return
-            penalty[g] = work.tile([P, ROWS], F32, tag="penalty", name="penalty", bufs=PAIRS)
+        def penalties(g, tiles=ALL_TILES):
+            cols = slice(P * tiles[0], P * (tiles[-1] + 1))
+            if g not in penalty:
+                penalty[g] = work.tile([P, ROWS], F32, tag="penalty", name="penalty", bufs=PAIRS)
             nc.vector.scalar_tensor_tensor(
-                out=penalty[g][:],
-                in0=farthest[g][:],
+                out=penalty[g][:, cols],
+                in0=farthest[g][:, cols],
                 scalar=(GATE_TEMP + GATE_CLIP) / FEAT_TEMP,
-                in1=sim[g][:],
+                in1=sim[g][:, cols],
                 op0=ALU.min,
                 op1=ALU.subtract,
             )
 
-        def exponentials(g):
-            if not is_pair(g):
-                return
-            weights[g] = work.tile([P, ROWS], F32, tag="weights", name="weights", bufs=PAIRS)
+        def exponentials(g, tiles=ALL_TILES):
+            cols = slice(P * tiles[0], P * (tiles[-1] + 1))
+            if g not in weights:
+                weights[g] = work.tile([P, ROWS], F32, tag="weights", name="weights", bufs=PAIRS)
             nc.scalar.activation(
-                out=weights[g][:], in_=penalty[g][:], func=ACT.Exp, scale=-FEAT_TEMP, bias=presence_gap[:, g : g + 1]
+                out=weights[g][:, cols],
+                in_=penalty[g][:, cols],
+                func=ACT.Exp,
+                scale=-FEAT_TEMP,
+                bias=presence_gap[:, g : g + 1],
             )
 
-        def rows_to_partitions(g):
-            if not is_pair(g):
-                return
-            rows_t[g] = psum.tile([P, TILES, QUERIES], F32, tag="bank", name="rows_t")
-            for j in range(TILES):
-                nc.tensor.transpose(rows_t[g][:, j, :], weights[g][:, P * j : P * (j + 1)], ident_f32[:])
+        def rows_to_partitions(g, tiles=ALL_TILES):
+            rows_t[g, tiles] = psum.tile([P, len(tiles), QUERIES], F32, tag="bank", name="rows_t")
+            for i, j in enumerate(tiles):
+                nc.tensor.transpose(rows_t[g, tiles][:, i, :], weights[g][:, P * j : P * (j + 1)], ident_f32[:])
 
-        def sum_queries(g):
-            row_sum[g] = psum.tile([P, TILES], F32, tag="bank", name="row_sum")
-            for j in range(TILES):
-                nc.tensor.matmul(
-                    row_sum[g][:, j : j + 1], lhsT=weights[g][:, P * j : P * (j + 1)], rhs=ones[:], start=True, stop=True
-                )
-
-        def finish(g, on_scalar=False):
-            if not is_pair(g):
-                return
-            probs[g] = work.tile([P, TILES, CLASSES], F32, tag="probs", name="probs", bufs=PAIRS)
-            total = work.tile([P, TILES, 1], F32, tag="total", name="total")
-            if g in row_sum:
-                nc.vector.tensor_tensor(out=total[:, :, 0], in0=row_sum[g][:], in1=background[:, g, :], op=ALU.add)
-            else:
-                nc.vector.tensor_reduce(out=total[:, :, 0], in_=rows_t[g][:], axis=mybir.AxisListType.X, op=ALU.add)
-                nc.vector.tensor_tensor(out=total[:, :, 0], in0=total[:, :, 0], in1=background[:, g, :], op=ALU.add)
+        def finish(g, tiles=ALL_TILES, on_scalar=False):
+            if g not in probs:
+                probs[g] = work.tile([P, TILES, CLASSES], F32, tag="probs", name="probs", bufs=PAIRS)
+            first, end = tiles[0], tiles[-1] + 1
+            total = work.tile([P, len(tiles), 1], F32, tag="total", name="total", bufs=PAIRS)
+            nc.vector.tensor_reduce(
+                out=total[:, :, 0], in_=rows_t[g, tiles][:], axis=mybir.AxisListType.X, op=ALU.add
+            )
+            nc.vector.tensor_tensor(
+                out=total[:, :, 0], in0=total[:, :, 0], in1=background[:, g, first:end], op=ALU.add
+            )
             nc.vector.reciprocal(out=total[:], in_=total[:])
-            nc.vector.tensor_tensor(out=probs[g][:, :, 0], in0=background[:, g, :], in1=total[:, :, 0], op=ALU.mult)
+            nc.vector.tensor_tensor(
+                out=probs[g][:, first:end, 0], in0=background[:, g, first:end], in1=total[:, :, 0], op=ALU.mult
+            )
             if on_scalar:
-                for j in range(TILES):
+                for i, j in enumerate(tiles):
                     nc.scalar.activation(
-                        out=probs[g][:, j, 1:CLASSES], in_=rows_t[g][:, j, :], func=ACT.Copy, scale=total[:, j, :]
+                        out=probs[g][:, j, 1:CLASSES], in_=rows_t[g, tiles][:, i, :], func=ACT.Copy, scale=total[:, i, :]
                     )
             else:
                 nc.vector.tensor_tensor(
-                    out=probs[g][:, :, 1:CLASSES],
-                    in0=rows_t[g][:],
-                    in1=total[:].to_broadcast([P, TILES, QUERIES]),
+                    out=probs[g][:, first:end, 1:CLASSES],
+                    in0=rows_t[g, tiles][:],
+                    in1=total[:].to_broadcast([P, len(tiles), QUERIES]),
                     op=ALU.mult,
                 )
-            nc.sync.dma_start(out=out_rows[g], in_=probs[g][:].rearrange("p j c -> p (j c)"))
+            nc.sync.dma_start(
+                out=out_rows[g][:, CLASSES * first : CLASSES * end],
+                in_=probs[g][:, first:end, :].rearrange("p j c -> p (j c)"),
+            )
 
         def gate(g):
             for c in range(3):
@@ -485,105 +492,104 @@ def tile_gaussianqueryassignment_kernel(
             clip_inverse_norm(engine, u)
             normalise_all(engine, u)
 
-        load_root_table()
-        turn_both(turn_inputs, 0)
-        group_inputs(0, 0, nc.scalar.copy)
-        group_inputs(0, 1, nc.vector.tensor_copy)
-        quantise_inputs(0)
-        prepare_boxes()
-        gate(0)
-        project(0)
-        adds(0)
-        turn_both(turn_inputs, 1)
-        square(0, 0)
-        square(0, 1)
-        group_inputs(1, 0, nc.scalar.copy)
-        group_inputs(1, 1, nc.vector.tensor_copy)
-        square(0, 2)
-        square(0, 3)
-        norm(nc.gpsimd, 0)
-        quantise_inputs(1)
-        gate_max(0)
-        project(1)
-        turn_both(turn_inputs, 2)
-        adds(1)
-        square(1, 0)
-        square(1, 1)
-        group_inputs(2, 0, nc.scalar.copy)
-        group_inputs(2, 1, nc.vector.tensor_copy)
-        square(1, 2)
-        square(1, 3)
-        norm(nc.gpsimd, 1)
-        quantise_inputs(2)
-        turn_both(turn_inputs, 3)
-        prepare_keeps()
-        project(2)
-        prepare_presence()
-        group_inputs(3, 0, nc.scalar.copy)
-        turn_both(turn_features, 0)
-        group_both_features(0)
-        turn_both(turn_inputs, 4)
-        adds(2)
-        group_inputs(3, 1, nc.vector.tensor_copy)
-        quantise_inputs(3)
-        project(3)
-        squares(2)
-        norm(nc.gpsimd, 2)
-        group_inputs(4, 0, nc.scalar.copy)
-        group_inputs(4, 1, nc.vector.tensor_copy)
-        gate(1)
-        adds(3)
-        turn_both(turn_features, 1)
-        group_both_features(1)
-        quantise_inputs(4)
-        project(4)
-        squares(3)
-        norm(nc.gpsimd, 3)
-        quantise_features(0)
-        gate_farthest(1, 1)
-        adds(4)
-        squares(4)
-        inverse_norm(4)
-        quantise_features(1)
-        turn_both(turn_features, 2)
-        group_both_features(2)
-        similarity(0)
-        gate_farthest(1, 2)
-        clip_inverse_norm(nc.vector, 4)
-        hold_exponentials()
-        normalise_all(nc.vector, 4)
-        turn_both(turn_features, 4)
-        background_exponentials()
-        turn_both(turn_features, 3)
-        quantise_features(2)
-        penalties(0)
-        similarity(1)
-        group_features(4, 0, nc.scalar.copy)
-        group_features(4, 1, nc.vector.tensor_copy)
-        group_both_features(3)
-        exponentials(0)
-        quantise_features(4)
-        quantise_features(3)
-        gate(2)
-        penalties(1)
-        exponentials(1)
-        gate_max(2)
-        similarity(2)
-        gate(3)
-        penalties(2)
-        exponentials(2)
-        similarity(3)
-        sum_queries(0)
-        rows_to_partitions(0)
-        gate_max(3)
-        penalties(3)
-        exponentials(3)
-        finish(0)
-        sum_queries(1)
-        rows_to_partitions(1)
-        finish(1)
-        sum_queries(2)
-        rows_to_partitions(2)
-        rows_to_partitions(3)
-        finish(2)
-        finish(3)
+        with tc.manual_schedule():
+            load_root_table()
+            turn_both(turn_inputs, 0)
+            prepare_boxes()
+            group_inputs(0, 0, nc.scalar.copy)
+            group_inputs(0, 1, nc.vector.tensor_copy)
+            quantise_inputs(0)
+            gate(0)
+            gate(1)
+            project(0)
+            gate_max(0)
+            adds(0)
+            turn_both(turn_inputs, 1)
+            square(0, 0)
+            square(0, 1)
+            group_inputs(1, 0, nc.scalar.copy)
+            group_inputs(1, 1, nc.vector.tensor_copy)
+            quantise_inputs(1)
+            square(0, 2)
+            square(0, 3)
+            norm(nc.gpsimd, 0)
+            turn_both(turn_inputs, 2)
+            gate_max(1)
+            project(1)
+            group_inputs(2, 0, nc.scalar.copy)
+            group_inputs(2, 1, nc.vector.tensor_copy)
+            gate(2)
+            gate_reach(3, 0)
+            adds(1)
+            quantise_inputs(2)
+            turn_both(turn_inputs, 3)
+            squares(1)
+            norm(nc.gpsimd, 1)
+            project(2)
+            gate_farthest(2, 1)
+            group_inputs(3, 0, nc.scalar.copy)
+            prepare_keeps()
+            adds(2)
+            turn_both(turn_features, 0)
+            group_both_features(0)
+            group_inputs(3, 1, nc.vector.tensor_copy)
+            quantise_inputs(3)
+            turn_both(turn_inputs, 4)
+            squares(2)
+            norm(nc.gpsimd, 2)
+            turn_both(turn_features, 1)
+            project(3)
+            group_inputs(4, 0, nc.scalar.copy)
+            group_inputs(4, 1, nc.vector.tensor_copy)
+            quantise_features(0)
+            adds(3)
+            group_both_features(1)
+            quantise_inputs(4)
+            squares(3)
+            norm(nc.gpsimd, 3)
+            gate_reach(3, 1)
+            prepare_presence()
+            gate_reach(3, 2)
+            project(4)
+            adds(4)
+            turn_both(turn_features, 2)
+            squares(4)
+            inverse_norm(4)
+            quantise_features(1)
+            gate_farthest(2, 2)
+            group_both_features(2)
+            similarity(0)
+            clip_inverse_norm(nc.vector, 4)
+            hold_exponentials()
+            background_exponentials()
+            normalise_all(nc.vector, 4)
+            turn_both(turn_features, 4)
+            turn_both(turn_features, 3)
+            penalties(0)
+            quantise_features(2)
+            similarity(1)
+            group_features(4, 0, nc.scalar.copy)
+            group_features(4, 1, nc.vector.tensor_copy)
+            penalties(1)
+            group_both_features(3)
+            exponentials(0)
+            quantise_features(4)
+            gate_farthest(3, 1)
+            quantise_features(3)
+            exponentials(1)
+            similarity(3)
+            background_terms()
+            similarity(2)
+            gate_farthest(3, 2)
+            penalties(3)
+            exponentials(3)
+            rows_to_partitions(0)
+            penalties(2)
+            exponentials(2)
+            rows_to_partitions(1)
+            finish(0, on_scalar=True)
+            rows_to_partitions(3)
+            finish(1, on_scalar=True)
+            rows_to_partitions(2)
+            finish(3)
+            finish(2)

@@ -65,8 +65,6 @@ def tile_gaussianqueryassignment_kernel(
 
         ident_f32 = keep.tile([P, P], F32)
         make_identity(nc, ident_f32[:])
-        ident_bf16 = keep.tile([P, P], BF16)
-        make_identity(nc, ident_bf16[:])
         warm = keep.tile([P, 1], F32)
 
         def load_root_table():
@@ -136,23 +134,16 @@ def tile_gaussianqueryassignment_kernel(
         odds = keep.tile([P, PAIRS, TILES], F32)
         keep_factor = keep.tile([P, PAIRS, TILES], F32)
 
-        def prepare_keeps():
-            nc.vector.tensor_scalar(
-                out=kept[:], in0=keep_in[:], scalar1=KEEP_EPS, scalar2=1.0 - KEEP_EPS, op0=ALU.max, op1=ALU.min
-            )
-            nc.vector.tensor_scalar(out=odds[:], in0=kept[:], scalar1=-1.0, scalar2=1.0, op0=ALU.mult, op1=ALU.add)
-            nc.vector.reciprocal(out=odds[:], in_=odds[:])
-            nc.vector.tensor_tensor(out=odds[:], in0=odds[:], in1=kept[:], op=ALU.mult)
-            nc.scalar.activation(out=keep_factor[:], in_=odds[:], func=ACT.Abs_reciprocal_sqrt)
-
         size = keep.tile([P, PAIRS, 3], F32)
         rate = keep.tile([P, PAIRS, 3], F32)
         shift = keep.tile([P, PAIRS, 3], F32)
 
-        def prepare_boxes():
+        def box_sizes():
             nc.vector.scalar_tensor_tensor(
                 out=size[:], in0=box[:, :, 3:6], scalar=-1.0, in1=box[:, :, 3:6], op0=ALU.mult, op1=ALU.max
             )
+
+        def box_scaled_sizes():
             nc.vector.tensor_scalar(
                 out=size[:],
                 in0=size[:],
@@ -161,22 +152,40 @@ def tile_gaussianqueryassignment_kernel(
                 op0=ALU.max,
                 op1=ALU.mult,
             )
+
+        def box_rates():
             nc.vector.reciprocal(out=rate[:], in_=size[:])
+
+        def box_shifts():
             nc.vector.scalar_tensor_tensor(
                 out=shift[:], in0=box[:, :, 0:3], scalar=-1.0, in1=rate[:], op0=ALU.mult, op1=ALU.mult
             )
 
+        presence_spread = []
         presence_gap = keep.tile([P, PAIRS], F32)
         presence_max = keep.tile([P, PAIRS], F32)
         background_gap = keep.tile([P, PAIRS, 1], F32)
         background = keep.tile([P, PAIRS, TILES], F32)
 
-        def prepare_presence():
-            spread = psum.tile([P, PAIRS, P], BF16, tag="bank", name="spread")
-            for g in range(PAIRS):
-                nc.tensor.transpose(spread[:, g, :], presence[:, g : g + 1].to_broadcast([P, P]), ident_bf16[:])
-            nc.vector.tensor_reduce(out=presence_max[:], in_=spread[:], axis=mybir.AxisListType.X, op=ALU.max)
+        def spread_presence():
+            spread = psum.tile([P, PAIRS // 2, P], F32, tag="bank", name="spread")
+            pairs = presence[:].bitcast(F32)
+            for h in range(PAIRS // 2):
+                nc.tensor.transpose(spread[:, h, :], pairs[:, h : h + 1].to_broadcast([P, P]), ident_f32[:])
+            presence_spread.append(spread)
+
+        def keep_and_presence_terms():
+            nc.vector.tensor_reduce(
+                out=presence_max[:].rearrange("m (h e) -> m h e", h=2),
+                in_=presence_spread[0][:].rearrange("m h p -> m (h p)").bitcast(BF16).rearrange("m (h p e) -> m h e p", h=2, e=2),
+                axis=mybir.AxisListType.X,
+                op=ALU.max,
+            )
+            nc.vector.tensor_scalar(
+                out=kept[:], in0=keep_in[:], scalar1=KEEP_EPS, scalar2=1.0 - KEEP_EPS, op0=ALU.max, op1=ALU.min
+            )
             nc.vector.tensor_tensor(out=presence_gap[:], in0=presence[:], in1=presence_max[:], op=ALU.subtract)
+            nc.vector.tensor_scalar(out=odds[:], in0=kept[:], scalar1=-1.0, scalar2=1.0, op0=ALU.mult, op1=ALU.add)
             nc.vector.tensor_scalar(
                 out=background_gap[:, :, 0],
                 in0=presence_max[:],
@@ -185,15 +194,12 @@ def tile_gaussianqueryassignment_kernel(
                 op0=ALU.mult,
                 op1=ALU.add,
             )
+            nc.vector.reciprocal(out=odds[:], in_=odds[:])
             nc.vector.tensor_scalar(
                 out=background_gap[:], in0=background_gap[:], scalar1=GATE_TEMP, scalar2=GAP_MAX, op0=ALU.subtract, op1=ALU.min
             )
-
-        def hold_exponentials():
-            for gap in (presence_gap[:], background_gap[:, :, 0]):
-                nc.vector.scalar_tensor_tensor(
-                    out=gap, in0=inv_norm[UNITS - 1][:], scalar=0.0, in1=gap, op0=ALU.mult, op1=ALU.add
-                )
+            nc.vector.tensor_tensor(out=odds[:], in0=odds[:], in1=kept[:], op=ALU.mult)
+            nc.scalar.activation(out=keep_factor[:], in_=odds[:], func=ACT.Abs_reciprocal_sqrt)
 
         def background_exponentials():
             nc.scalar.activation(out=background_gap[:], in_=background_gap[:], func=ACT.Exp)
@@ -338,19 +344,28 @@ def tile_gaussianqueryassignment_kernel(
 
         reach, farthest = {}, {}
 
+        by_coordinate = keep.tile([P, PAIRS, 3, TILES], BF16)
+        spread_positions = {}
+
+        def order_positions():
+            nc.vector.tensor_copy(out=by_coordinate[:], in_=position[:].rearrange("p g j c -> p g c j"))
+
+        def spread_coordinates(g, coordinates):
+            spread = psum.tile([P, 2, 2, P], F32, tag="bank", name="spread")
+            for i, c in enumerate(coordinates):
+                pairs = by_coordinate[:, g, c, :].bitcast(F32)
+                for h in range(2):
+                    nc.tensor.transpose(spread[:, i, h, :], pairs[:, h : h + 1].to_broadcast([P, P]), ident_f32[:])
+                spread_positions[g, c] = spread[:, i]
+
         def gate_reach(g, c):
-            if not is_pair(g):
-                return
-            if c == 0:
+            if g not in reach:
                 reach[g] = work.tile([P, 3, ROWS], F32, tag="reach", name="reach", bufs=PAIRS)
-            spread = psum.tile([P, TILES, P], BF16, tag="bank", name="spread")
-            for j in range(TILES):
-                nc.tensor.transpose(
-                    spread[:, j, :], position[:, g, j, c : c + 1].to_broadcast([P, P]), ident_bf16[:]
-                )
             nc.scalar.activation(
-                out=reach[g][:, c, :],
-                in_=spread[:].rearrange("m j p -> m (j p)"),
+                out=reach[g][:, c, :].rearrange("m (h e p) -> m h e p", h=2, e=2),
+                in_=spread_positions[g, c].rearrange("m h p -> m (h p)").bitcast(BF16).rearrange(
+                    "m (h p e) -> m h e p", h=2, e=2
+                ),
                 func=ACT.Abs,
                 scale=rate[:, g, c : c + 1],
                 bias=shift[:, g, c : c + 1],
@@ -365,7 +380,7 @@ def tile_gaussianqueryassignment_kernel(
                 out=farthest[g][:], in0=(reach[g][:, 0, :] if c == 1 else farthest[g][:]), in1=reach[g][:, c, :], op=ALU.max
             )
 
-        penalty, weights, probs, rows_t = {}, {}, {}, {}
+        penalty, weights, probs, rows_t, row_sum = {}, {}, {}, {}, {}
         out_rows = out.rearrange("b (t p j) c -> (b t) p (j c)", p=P, j=TILES)
 
         sim = {}
@@ -411,45 +426,72 @@ def tile_gaussianqueryassignment_kernel(
             )
 
         def rows_to_partitions(g, tiles=ALL_TILES):
-            rows_t[g, tiles] = psum.tile([P, len(tiles), QUERIES], F32, tag="bank", name="rows_t")
+            rows_t[g] = psum.tile([P, len(tiles), QUERIES], F32, tag="bank", name="rows_t")
             for i, j in enumerate(tiles):
-                nc.tensor.transpose(rows_t[g, tiles][:, i, :], weights[g][:, P * j : P * (j + 1)], ident_f32[:])
+                nc.tensor.transpose(rows_t[g][:, i, :], weights[g][:, P * j : P * (j + 1)], ident_f32[:])
 
-        def finish(g, tiles=ALL_TILES, on_scalar=False):
-            if g not in probs:
-                probs[g] = work.tile([P, TILES, CLASSES], F32, tag="probs", name="probs", bufs=PAIRS)
-            first, end = tiles[0], tiles[-1] + 1
-            total = work.tile([P, len(tiles), 1], F32, tag="total", name="total", bufs=PAIRS)
-            nc.vector.tensor_reduce(
-                out=total[:, :, 0], in_=rows_t[g, tiles][:], axis=mybir.AxisListType.X, op=ALU.add
-            )
+        def sum_queries(g):
+            row_sum[g] = psum.tile([P, TILES], F32, tag="bank", name="row_sum")
+            for j in range(TILES):
+                nc.tensor.matmul(
+                    row_sum[g][:, j : j + 1], lhsT=weights[g][:, P * j : P * (j + 1)], rhs=ones[:], start=True, stop=True
+                )
+
+        total = {}
+
+        def row_totals(g):
+            total[g] = work.tile([P, TILES, 1], F32, tag="total", name="total", bufs=PAIRS)
+            if g in row_sum:
+                return
+            nc.vector.tensor_reduce(out=total[g][:, :, 0], in_=rows_t[g][:], axis=mybir.AxisListType.X, op=ALU.add)
+
+        def add_background(g):
             nc.vector.tensor_tensor(
-                out=total[:, :, 0], in0=total[:, :, 0], in1=background[:, g, first:end], op=ALU.add
+                out=total[g][:, :, 0],
+                in0=row_sum[g][:] if g in row_sum else total[g][:, :, 0],
+                in1=background[:, g, :],
+                op=ALU.add,
             )
-            nc.vector.reciprocal(out=total[:], in_=total[:])
-            nc.vector.tensor_tensor(
-                out=probs[g][:, first:end, 0], in0=background[:, g, first:end], in1=total[:, :, 0], op=ALU.mult
-            )
+
+        def invert_totals(g):
+            nc.vector.reciprocal(out=total[g][:], in_=total[g][:])
+
+        def query_probabilities(g, on_scalar=False):
+            probs[g] = work.tile([P, TILES, CLASSES], F32, tag="probs", name="probs", bufs=PAIRS)
             if on_scalar:
-                for i, j in enumerate(tiles):
+                for j in range(TILES):
                     nc.scalar.activation(
-                        out=probs[g][:, j, 1:CLASSES], in_=rows_t[g, tiles][:, i, :], func=ACT.Copy, scale=total[:, i, :]
+                        out=probs[g][:, j, 1:CLASSES], in_=rows_t[g][:, j, :], func=ACT.Copy, scale=total[g][:, j, :]
                     )
             else:
                 nc.vector.tensor_tensor(
-                    out=probs[g][:, first:end, 1:CLASSES],
-                    in0=rows_t[g, tiles][:],
-                    in1=total[:].to_broadcast([P, len(tiles), QUERIES]),
+                    out=probs[g][:, :, 1:CLASSES],
+                    in0=rows_t[g][:],
+                    in1=total[g][:].to_broadcast([P, TILES, QUERIES]),
                     op=ALU.mult,
                 )
-            nc.sync.dma_start(
-                out=out_rows[g][:, CLASSES * first : CLASSES * end],
-                in_=probs[g][:, first:end, :].rearrange("p j c -> p (j c)"),
-            )
+
+        def background_probabilities(g):
+            nc.vector.tensor_tensor(out=probs[g][:, :, 0], in0=background[:, g, :], in1=total[g][:, :, 0], op=ALU.mult)
+
+        def store(g):
+            nc.sync.dma_start(out=out_rows[g], in_=probs[g][:].rearrange("p j c -> p (j c)"))
+
+        def finish_two(first, second, on_scalar=()):
+            for step in (row_totals, add_background, invert_totals):
+                for g in (first, second):
+                    step(g)
+            for g in (first, second):
+                query_probabilities(g, on_scalar=g in on_scalar)
+                background_probabilities(g)
+                store(g)
 
         def gate(g):
-            for c in range(3):
-                gate_reach(g, c)
+            spread_coordinates(g, (0, 1))
+            gate_reach(g, 0)
+            gate_reach(g, 1)
+            spread_coordinates(g, (2,))
+            gate_reach(g, 2)
 
         def gate_max(g):
             gate_farthest(g, 1)
@@ -495,31 +537,46 @@ def tile_gaussianqueryassignment_kernel(
         with tc.manual_schedule():
             load_root_table()
             turn_both(turn_inputs, 0)
-            prepare_boxes()
+            order_positions()
+            box_sizes()
+            box_scaled_sizes()
             group_inputs(0, 0, nc.scalar.copy)
             group_inputs(0, 1, nc.vector.tensor_copy)
+            box_rates()
             quantise_inputs(0)
+            box_shifts()
             gate(0)
-            gate(1)
             project(0)
-            gate_max(0)
-            adds(0)
             turn_both(turn_inputs, 1)
+            adds(0)
+            gate_farthest(0, 1)
             square(0, 0)
             square(0, 1)
             group_inputs(1, 0, nc.scalar.copy)
-            group_inputs(1, 1, nc.vector.tensor_copy)
-            quantise_inputs(1)
             square(0, 2)
             square(0, 3)
+            spread_coordinates(1, (0, 1))
+            gate_reach(1, 0)
+            gate_reach(1, 1)
+            group_inputs(1, 1, nc.vector.tensor_copy)
+            gate_farthest(0, 2)
+            quantise_inputs(1)
+            spread_coordinates(1, (2,))
+            gate_reach(1, 2)
             norm(nc.gpsimd, 0)
+            spread_coordinates(2, (0, 1))
+            gate_reach(2, 0)
             turn_both(turn_inputs, 2)
-            gate_max(1)
+            gate_farthest(1, 1)
             project(1)
             group_inputs(2, 0, nc.scalar.copy)
-            group_inputs(2, 1, nc.vector.tensor_copy)
-            gate(2)
+            gate_farthest(1, 2)
+            gate_reach(2, 1)
+            spread_coordinates(2, (2,))
+            gate_reach(2, 2)
+            spread_coordinates(3, (0,))
             gate_reach(3, 0)
+            group_inputs(2, 1, nc.vector.tensor_copy)
             adds(1)
             quantise_inputs(2)
             turn_both(turn_inputs, 3)
@@ -528,27 +585,37 @@ def tile_gaussianqueryassignment_kernel(
             project(2)
             gate_farthest(2, 1)
             group_inputs(3, 0, nc.scalar.copy)
-            prepare_keeps()
-            adds(2)
+            add_bias(2, 0)
+            add_bias(2, 1)
+            add_bias(2, 2)
             turn_both(turn_features, 0)
+            square(2, 0)
+            square(2, 1)
             group_both_features(0)
             group_inputs(3, 1, nc.vector.tensor_copy)
+            add_bias(2, 3)
             quantise_inputs(3)
             turn_both(turn_inputs, 4)
-            squares(2)
-            norm(nc.gpsimd, 2)
-            turn_both(turn_features, 1)
+            square(2, 2)
+            square(2, 3)
             project(3)
+            turn_both(turn_features, 1)
+            norm(nc.gpsimd, 2)
             group_inputs(4, 0, nc.scalar.copy)
             group_inputs(4, 1, nc.vector.tensor_copy)
             quantise_features(0)
-            adds(3)
+            add_bias(3, 0)
+            add_bias(3, 1)
             group_both_features(1)
             quantise_inputs(4)
+            add_bias(3, 2)
+            add_bias(3, 3)
             squares(3)
-            norm(nc.gpsimd, 3)
+            spread_coordinates(3, (1, 2))
             gate_reach(3, 1)
-            prepare_presence()
+            spread_presence()
+            norm(nc.gpsimd, 3)
+            keep_and_presence_terms()
             gate_reach(3, 2)
             project(4)
             adds(4)
@@ -560,36 +627,56 @@ def tile_gaussianqueryassignment_kernel(
             group_both_features(2)
             similarity(0)
             clip_inverse_norm(nc.vector, 4)
-            hold_exponentials()
+            turn_features(3, 0)
             background_exponentials()
+            gate_farthest(3, 1)
             normalise_all(nc.vector, 4)
             turn_both(turn_features, 4)
-            turn_both(turn_features, 3)
+            turn_features(3, 1)
             penalties(0)
             quantise_features(2)
             similarity(1)
             group_features(4, 0, nc.scalar.copy)
             group_features(4, 1, nc.vector.tensor_copy)
             penalties(1)
+            quantise_features(4)
             group_both_features(3)
             exponentials(0)
-            quantise_features(4)
-            gate_farthest(3, 1)
             quantise_features(3)
             exponentials(1)
             similarity(3)
+            gate_farthest(3, 2)
             background_terms()
             similarity(2)
-            gate_farthest(3, 2)
+            rows_to_partitions(0)
             penalties(3)
             exponentials(3)
-            rows_to_partitions(0)
             penalties(2)
-            exponentials(2)
             rows_to_partitions(1)
-            finish(0, on_scalar=True)
+            exponentials(2)
+            row_totals(0)
+            row_totals(1)
+            add_background(0)
+            add_background(1)
             rows_to_partitions(3)
-            finish(1, on_scalar=True)
+            invert_totals(0)
+            invert_totals(1)
+            query_probabilities(0, on_scalar=True)
             rows_to_partitions(2)
-            finish(3)
-            finish(2)
+            row_totals(3)
+            background_probabilities(0)
+            store(0)
+            row_totals(2)
+            add_background(3)
+            query_probabilities(1, on_scalar=True)
+            background_probabilities(1)
+            store(1)
+            invert_totals(3)
+            add_background(2)
+            query_probabilities(3)
+            invert_totals(2)
+            background_probabilities(3)
+            store(3)
+            query_probabilities(2, on_scalar=True)
+            background_probabilities(2)
+            store(2)

@@ -99,12 +99,10 @@ def tile_gaussianqueryassignment_kernel(
             nc.sync.dma_start(out=xg[:, g, :, 0:AFFINITY], in_=affinity_in[g])
             nc.sync.dma_start(out=xg[:, g, :, AFFINITY:K], in_=motion_in[g])
 
-        xq = keep.tile([P, PAIRS, K], BF16)
-        for first in range(0, PAIRS, 2):
-            nc.sync.dma_start(
-                out=xq[:, first : first + 2, :],
-                in_=query_feat.rearrange("b t m k -> m (b t) k")[:, first : first + 2, :],
-            )
+        xq = keep.tile([P, TILES, K], BF16)
+        query_rows = query_feat.rearrange("b t m k -> (b t m) k").rearrange("(p i) k -> p i k", i=TILES)
+        for first in range(0, TILES, 2):
+            nc.sync.dma_start(out=xq[:, first : first + 2, :], in_=query_rows[:, first : first + 2, :])
         position = keep.tile([P, PAIRS, TILES, 3], BF16)
         nc.sync.dma_start(
             out=position[:].rearrange("p g j c -> p g (j c)"),
@@ -328,7 +326,14 @@ def tile_gaussianqueryassignment_kernel(
                 return
             if half == 0:
                 f_grouped[u] = work.tile([P, ROWS, PACK], BF16, tag="f_grouped", name="f_grouped", align_bytes=64)
-            lay_side_by_side(f_turned[u, half], f_grouped[u], half, copy_out)
+            if u > 0:
+                lay_side_by_side(f_turned[u, half], f_grouped[u], half, copy_out)
+                return
+            grouped_pairs = f_grouped[u][:].bitcast(F32).rearrange("p (r i) u2 -> p r i u2", i=TILES)
+            copy_out(
+                out=grouped_pairs[:, :, 2 * half : 2 * half + 2, :],
+                in_=f_turned[u, half][:].rearrange("p i u2 r -> p r i u2"),
+            )
 
         def quantise_features(u):
             if not is_unit(u):
@@ -380,7 +385,7 @@ def tile_gaussianqueryassignment_kernel(
                 out=farthest[g][:], in0=(reach[g][:, 0, :] if c == 1 else farthest[g][:]), in1=reach[g][:, c, :], op=ALU.max
             )
 
-        penalty, weights, probs, rows_t, row_sum = {}, {}, {}, {}, {}
+        penalty, weights, rows_t = {}, {}, {}
         out_rows = out.rearrange("b (t p j) c -> (b t) p (j c)", p=P, j=TILES)
 
         sim = {}
@@ -430,68 +435,49 @@ def tile_gaussianqueryassignment_kernel(
             for i, j in enumerate(tiles):
                 nc.tensor.transpose(rows_t[g][:, i, :], weights[g][:, P * j : P * (j + 1)], ident_f32[:])
 
-        def sum_queries(g):
-            row_sum[g] = psum.tile([P, TILES], F32, tag="bank", name="row_sum")
-            for j in range(TILES):
-                nc.tensor.matmul(
-                    row_sum[g][:, j : j + 1], lhsT=weights[g][:, P * j : P * (j + 1)], rhs=ones[:], start=True, stop=True
-                )
-
-        total = {}
+        total = keep.tile([P, PAIRS, TILES, 1], F32)
+        probs = keep.tile([P, PAIRS, TILES, CLASSES], F32)
 
         def row_totals(g):
-            total[g] = work.tile([P, TILES, 1], F32, tag="total", name="total", bufs=PAIRS)
-            if g in row_sum:
-                return
-            nc.vector.tensor_reduce(out=total[g][:, :, 0], in_=rows_t[g][:], axis=mybir.AxisListType.X, op=ALU.add)
+            nc.vector.tensor_reduce(out=total[:, g, :, 0], in_=rows_t[g][:], axis=mybir.AxisListType.X, op=ALU.add)
 
-        def add_background(g):
+        def add_background(pairs):
             nc.vector.tensor_tensor(
-                out=total[g][:, :, 0],
-                in0=row_sum[g][:] if g in row_sum else total[g][:, :, 0],
-                in1=background[:, g, :],
-                op=ALU.add,
+                out=total[:, pairs, :, 0], in0=total[:, pairs, :, 0], in1=background[:, pairs, :], op=ALU.add
             )
 
-        def invert_totals(g):
-            nc.vector.reciprocal(out=total[g][:], in_=total[g][:])
+        def invert_totals(pairs):
+            nc.vector.reciprocal(out=total[:, pairs], in_=total[:, pairs])
+
+        def background_probabilities(pairs):
+            nc.vector.tensor_tensor(
+                out=probs[:, pairs, :, 0], in0=background[:, pairs, :], in1=total[:, pairs, :, 0], op=ALU.mult
+            )
 
         def query_probabilities(g, on_scalar=False):
-            probs[g] = work.tile([P, TILES, CLASSES], F32, tag="probs", name="probs", bufs=PAIRS)
             if on_scalar:
                 for j in range(TILES):
                     nc.scalar.activation(
-                        out=probs[g][:, j, 1:CLASSES], in_=rows_t[g][:, j, :], func=ACT.Copy, scale=total[g][:, j, :]
+                        out=probs[:, g, j, 1:CLASSES], in_=rows_t[g][:, j, :], func=ACT.Copy, scale=total[:, g, j, :]
                     )
             else:
                 nc.vector.tensor_tensor(
-                    out=probs[g][:, :, 1:CLASSES],
+                    out=probs[:, g, :, 1:CLASSES],
                     in0=rows_t[g][:],
-                    in1=total[g][:].to_broadcast([P, TILES, QUERIES]),
+                    in1=total[:, g].to_broadcast([P, TILES, QUERIES]),
                     op=ALU.mult,
                 )
 
-        def background_probabilities(g):
-            nc.vector.tensor_tensor(out=probs[g][:, :, 0], in0=background[:, g, :], in1=total[g][:, :, 0], op=ALU.mult)
-
         def store(g):
-            nc.sync.dma_start(out=out_rows[g], in_=probs[g][:].rearrange("p j c -> p (j c)"))
+            nc.sync.dma_start(out=out_rows[g], in_=probs[:, g].rearrange("p j c -> p (j c)"))
 
-        def finish_two(first, second, on_scalar=()):
-            for step in (row_totals, add_background, invert_totals):
-                for g in (first, second):
-                    step(g)
-            for g in (first, second):
-                query_probabilities(g, on_scalar=g in on_scalar)
-                background_probabilities(g)
-                store(g)
-
-        def gate(g):
+        def gate_spreads(g):
             spread_coordinates(g, (0, 1))
-            gate_reach(g, 0)
-            gate_reach(g, 1)
             spread_coordinates(g, (2,))
-            gate_reach(g, 2)
+
+        def gate_reaches(g):
+            for c in range(3):
+                gate_reach(g, c)
 
         def gate_max(g):
             gate_farthest(g, 1)
@@ -545,7 +531,8 @@ def tile_gaussianqueryassignment_kernel(
             box_rates()
             quantise_inputs(0)
             box_shifts()
-            gate(0)
+            gate_spreads(0)
+            gate_reaches(0)
             project(0)
             turn_both(turn_inputs, 1)
             adds(0)
@@ -554,7 +541,6 @@ def tile_gaussianqueryassignment_kernel(
             square(0, 1)
             group_inputs(1, 0, nc.scalar.copy)
             square(0, 2)
-            square(0, 3)
             spread_coordinates(1, (0, 1))
             gate_reach(1, 0)
             gate_reach(1, 1)
@@ -563,22 +549,28 @@ def tile_gaussianqueryassignment_kernel(
             quantise_inputs(1)
             spread_coordinates(1, (2,))
             gate_reach(1, 2)
+            square(0, 3)
             norm(nc.gpsimd, 0)
-            spread_coordinates(2, (0, 1))
+            gate_spreads(2)
             gate_reach(2, 0)
             turn_both(turn_inputs, 2)
             gate_farthest(1, 1)
-            project(1)
+            multiply(1, 0)
+            multiply(1, 1)
             group_inputs(2, 0, nc.scalar.copy)
             gate_farthest(1, 2)
             gate_reach(2, 1)
-            spread_coordinates(2, (2,))
             gate_reach(2, 2)
             spread_coordinates(3, (0,))
             gate_reach(3, 0)
+            multiply(1, 2)
+            multiply(1, 3)
             group_inputs(2, 1, nc.vector.tensor_copy)
-            adds(1)
+            add_bias(1, 0)
+            add_bias(1, 1)
+            add_bias(1, 2)
             quantise_inputs(2)
+            add_bias(1, 3)
             turn_both(turn_inputs, 3)
             squares(1)
             norm(nc.gpsimd, 1)
@@ -590,27 +582,31 @@ def tile_gaussianqueryassignment_kernel(
             add_bias(2, 2)
             turn_both(turn_features, 0)
             square(2, 0)
-            square(2, 1)
             group_both_features(0)
             group_inputs(3, 1, nc.vector.tensor_copy)
+            square(2, 1)
             add_bias(2, 3)
             quantise_inputs(3)
             turn_both(turn_inputs, 4)
             square(2, 2)
             square(2, 3)
+            turn_features(1, 0)
             project(3)
-            turn_both(turn_features, 1)
             norm(nc.gpsimd, 2)
+            turn_features(1, 1)
             group_inputs(4, 0, nc.scalar.copy)
             group_inputs(4, 1, nc.vector.tensor_copy)
             quantise_features(0)
             add_bias(3, 0)
             add_bias(3, 1)
+            square(3, 0)
+            square(3, 1)
             group_both_features(1)
             quantise_inputs(4)
             add_bias(3, 2)
             add_bias(3, 3)
-            squares(3)
+            square(3, 2)
+            square(3, 3)
             spread_coordinates(3, (1, 2))
             gate_reach(3, 1)
             spread_presence()
@@ -631,10 +627,10 @@ def tile_gaussianqueryassignment_kernel(
             background_exponentials()
             gate_farthest(3, 1)
             normalise_all(nc.vector, 4)
-            turn_both(turn_features, 4)
             turn_features(3, 1)
-            penalties(0)
+            turn_both(turn_features, 4)
             quantise_features(2)
+            penalties(0)
             similarity(1)
             group_features(4, 0, nc.scalar.copy)
             group_features(4, 1, nc.vector.tensor_copy)
@@ -651,32 +647,31 @@ def tile_gaussianqueryassignment_kernel(
             rows_to_partitions(0)
             penalties(3)
             exponentials(3)
-            penalties(2)
             rows_to_partitions(1)
+            penalties(2)
             exponentials(2)
             row_totals(0)
-            row_totals(1)
-            add_background(0)
-            add_background(1)
             rows_to_partitions(3)
-            invert_totals(0)
-            invert_totals(1)
-            query_probabilities(0, on_scalar=True)
+            row_totals(1)
+            add_background(slice(0, 1))
             rows_to_partitions(2)
             row_totals(3)
-            background_probabilities(0)
+            invert_totals(slice(0, 1))
+            add_background(slice(1, 2))
+            query_probabilities(0, on_scalar=True)
+            background_probabilities(slice(0, 1))
             store(0)
+            invert_totals(slice(1, 2))
             row_totals(2)
-            add_background(3)
             query_probabilities(1, on_scalar=True)
-            background_probabilities(1)
+            background_probabilities(slice(1, 2))
             store(1)
-            invert_totals(3)
-            add_background(2)
+            add_background(slice(3, 4))
+            add_background(slice(2, 3))
+            invert_totals(slice(3, 4))
+            invert_totals(slice(2, 3))
             query_probabilities(3)
-            invert_totals(2)
-            background_probabilities(3)
-            store(3)
             query_probabilities(2, on_scalar=True)
-            background_probabilities(2)
+            background_probabilities(slice(2, 4))
+            store(3)
             store(2)

@@ -80,11 +80,13 @@ def tile_gaussianqueryassignment_kernel(
         nc.vector.memset(wq_plane[:].bitcast(I32), 0)
         nc.vector.memset(wg_plane[:].bitcast(I32), 0)
 
-        def load_weight(words_in, scales_in, words, plane):
+        def load_words(words_in, words):
             nc.sync.dma_start(
                 out=words[:].bitcast(I32),
                 in_=words_in[0].rearrange("p n t -> p (n t)").bitcast(I32),
             )
+
+        def load_scales(scales_in, plane):
             for quadrant in range(4):
                 nc.sync.dma_start(
                     out=plane[32 * quadrant : 32 * quadrant + 4, :].bitcast(I32),
@@ -95,29 +97,39 @@ def tile_gaussianqueryassignment_kernel(
         affinity_in = instance_affinity.rearrange("b t (p j) a -> (b t) p j a", j=TILES)
         motion_in = motion_code.rearrange("b t (p j) c -> (b t) p j c", j=TILES)
 
-        def load_gaussians(g):
+        def load_affinity(g):
             nc.sync.dma_start(out=xg[:, g, :, 0:AFFINITY], in_=affinity_in[g])
+
+        def load_motion(g):
             nc.sync.dma_start(out=xg[:, g, :, AFFINITY:K], in_=motion_in[g])
 
-        xq = keep.tile([P, TILES, K], BF16)
-        query_rows = query_feat.rearrange("b t m k -> (b t m) k").rearrange("(p i) k -> p i k", i=TILES)
-        for first in range(0, TILES, 2):
-            nc.sync.dma_start(out=xq[:, first : first + 2, :], in_=query_rows[:, first : first + 2, :])
+        def load_gaussians(g):
+            load_affinity(g)
+            load_motion(g)
+
         position = keep.tile([P, PAIRS, TILES, 3], BF16)
-        nc.sync.dma_start(
+        nc.scalar.dma_start(
             out=position[:].rearrange("p g j c -> p g (j c)"),
             in_=center.rearrange("b t (p c) -> p (b t) c", c=3 * TILES),
         )
         box = keep.tile([P, PAIRS, 7], BF16)
-        nc.sync.dma_start(out=box[:], in_=query_box3d.rearrange("b t m c -> m (b t) c"))
-        load_weight(Wq_words, Wq_scales, wq_words, wq_plane)
+        nc.scalar.dma_start(out=box[:], in_=query_box3d.rearrange("b t m c -> m (b t) c"))
+        xq = keep.tile([P, TILES, K], BF16)
+        query_rows = query_feat.rearrange("b t m k -> (b t m) k").rearrange("(p i) k -> p i k", i=TILES)
+        for first in range(0, TILES, 2):
+            nc.sync.dma_start(out=xq[:, first : first + 2, :], in_=query_rows[:, first : first + 2, :])
+        load_words(Wq_words, wq_words)
+        load_gaussians(0)
+        load_scales(Wq_scales, wq_plane)
         bq_rows = keep.tile([P, D], BF16)
         nc.sync.dma_start(out=bq_rows[:], in_=bq.partition_broadcast(P))
-        load_gaussians(0)
-        load_weight(Wg_words, Wg_scales, wg_words, wg_plane)
+        load_words(Wg_words, wg_words)
+        load_gaussians(1)
+        load_scales(Wg_scales, wg_plane)
         bg_rows = keep.tile([P, D], BF16)
         nc.sync.dma_start(out=bg_rows[:], in_=bg.partition_broadcast(P))
-        load_gaussians(1)
+        load_gaussians(2)
+        load_gaussians(3)
         keep_in = keep.tile([P, PAIRS, TILES], BF16)
         nc.sync.dma_start(out=keep_in[:], in_=keep_score.rearrange("b t (p j) -> p (b t) j", j=TILES))
         presence = keep.tile([P, PAIRS], BF16)
@@ -125,8 +137,6 @@ def tile_gaussianqueryassignment_kernel(
             nc.sync.dma_start(out=presence[:], in_=presence_logit.rearrange("b t m -> m (b t)"))
         bg_bias = keep.tile([P, 1], BF16)
         nc.sync.dma_start(out=bg_bias[:], in_=background_bias.partition_broadcast(P))
-        load_gaussians(2)
-        load_gaussians(3)
 
         kept = keep.tile([P, PAIRS, TILES], F32)
         odds = keep.tile([P, PAIRS, TILES], F32)
@@ -184,23 +194,22 @@ def tile_gaussianqueryassignment_kernel(
             )
             nc.vector.tensor_tensor(out=presence_gap[:], in0=presence[:], in1=presence_max[:], op=ALU.subtract)
             nc.vector.tensor_scalar(out=odds[:], in0=kept[:], scalar1=-1.0, scalar2=1.0, op0=ALU.mult, op1=ALU.add)
+            nc.vector.reciprocal(out=odds[:], in_=odds[:])
             nc.vector.tensor_scalar(
                 out=background_gap[:, :, 0],
                 in0=presence_max[:],
-                scalar1=-1.0,
-                scalar2=bg_bias[:, 0:1],
-                op0=ALU.mult,
-                op1=ALU.add,
-            )
-            nc.vector.reciprocal(out=odds[:], in_=odds[:])
-            nc.vector.tensor_scalar(
-                out=background_gap[:], in0=background_gap[:], scalar1=GATE_TEMP, scalar2=GAP_MAX, op0=ALU.subtract, op1=ALU.min
+                scalar1=bg_bias[:, 0:1],
+                scalar2=-GAP_MAX,
+                op0=ALU.subtract,
+                op1=ALU.max,
             )
             nc.vector.tensor_tensor(out=odds[:], in0=odds[:], in1=kept[:], op=ALU.mult)
             nc.scalar.activation(out=keep_factor[:], in_=odds[:], func=ACT.Abs_reciprocal_sqrt)
 
         def background_exponentials():
-            nc.scalar.activation(out=background_gap[:], in_=background_gap[:], func=ACT.Exp)
+            nc.scalar.activation(
+                out=background_gap[:], in_=background_gap[:], func=ACT.Exp, scale=-1.0, bias=-GATE_TEMP
+            )
 
         def background_terms():
             nc.vector.tensor_tensor(
@@ -526,26 +535,27 @@ def tile_gaussianqueryassignment_kernel(
             order_positions()
             box_sizes()
             box_scaled_sizes()
+            box_rates()
+            box_shifts()
             group_inputs(0, 0, nc.scalar.copy)
             group_inputs(0, 1, nc.vector.tensor_copy)
-            box_rates()
-            quantise_inputs(0)
-            box_shifts()
             gate_spreads(0)
+            spread_coordinates(1, (0, 1))
+            quantise_inputs(0)
             gate_reaches(0)
+            gate_reach(1, 0)
+            gate_reach(1, 1)
             project(0)
             turn_both(turn_inputs, 1)
-            adds(0)
             gate_farthest(0, 1)
+            adds(0)
             square(0, 0)
             square(0, 1)
             group_inputs(1, 0, nc.scalar.copy)
             square(0, 2)
-            spread_coordinates(1, (0, 1))
-            gate_reach(1, 0)
-            gate_reach(1, 1)
             group_inputs(1, 1, nc.vector.tensor_copy)
             gate_farthest(0, 2)
+            gate_farthest(1, 1)
             quantise_inputs(1)
             spread_coordinates(1, (2,))
             gate_reach(1, 2)
@@ -554,7 +564,6 @@ def tile_gaussianqueryassignment_kernel(
             gate_spreads(2)
             gate_reach(2, 0)
             turn_both(turn_inputs, 2)
-            gate_farthest(1, 1)
             multiply(1, 0)
             multiply(1, 1)
             group_inputs(2, 0, nc.scalar.copy)
@@ -655,10 +664,10 @@ def tile_gaussianqueryassignment_kernel(
             row_totals(1)
             add_background(slice(0, 1))
             rows_to_partitions(2)
-            row_totals(3)
             invert_totals(slice(0, 1))
             add_background(slice(1, 2))
             query_probabilities(0, on_scalar=True)
+            row_totals(3)
             background_probabilities(slice(0, 1))
             store(0)
             invert_totals(slice(1, 2))

@@ -11,26 +11,25 @@ U8 = mybir.dt.uint8
 FP8X4 = mybir.dt.float8_e4m3fn_x4
 ALU = mybir.AluOpType
 ACT = mybir.ActivationFunctionType
+FREE_AXIS = mybir.AxisListType.X
 
 P = 128
 PACK = 4
 PAIRS = 4
 TILES = 4
 ROWS = TILES * P
+UNITS = 1 + PAIRS
 QUERIES = 128
 K = 512
 AFFINITY = 384
 D = 512
 CLASSES = QUERIES + 1
-ALL_TILES = tuple(range(TILES))
-UNITS = 1 + PAIRS
 
 DILATION = 1.5
 MIN_EXTENT = 0.5
 GATE_TEMP = 3.0
 GATE_CLIP = 8.0
 FEAT_TEMP = 6.0
-KEEP_W = 0.5
 KEEP_EPS = 1e-4
 NORM_EPS = 1e-12
 GAP_MAX = 80.0
@@ -65,11 +64,6 @@ def tile_gaussianqueryassignment_kernel(
 
         ident_f32 = keep.tile([P, P], F32)
         make_identity(nc, ident_f32[:])
-        warm = keep.tile([P, 1], F32)
-
-        def load_root_table():
-            nc.scalar.activation(out=warm[:], in_=ones[:], func=ACT.Abs_reciprocal_sqrt)
-
         ones = keep.tile([P, 1], F32)
         nc.gpsimd.memset(ones[:], 1.0)
 
@@ -93,65 +87,170 @@ def tile_gaussianqueryassignment_kernel(
                     in_=scales_in[0, 4 * quadrant : 4 * quadrant + 4, :].bitcast(I32),
                 )
 
+        xq = keep.tile([P, TILES, K], BF16)
+        query_rows = query_feat.rearrange("b t m k -> (b t m) k").rearrange("(p i) k -> p i k", i=TILES)
         xg = keep.tile([P, PAIRS, TILES, K], BF16)
         affinity_in = instance_affinity.rearrange("b t (p j) a -> (b t) p j a", j=TILES)
         motion_in = motion_code.rearrange("b t (p j) c -> (b t) p j c", j=TILES)
 
-        def load_affinity(g):
+        def load_gaussians(g):
             nc.sync.dma_start(out=xg[:, g, :, 0:AFFINITY], in_=affinity_in[g])
-
-        def load_motion(g):
             nc.sync.dma_start(out=xg[:, g, :, AFFINITY:K], in_=motion_in[g])
 
-        def load_gaussians(g):
-            load_affinity(g)
-            load_motion(g)
-
         position = keep.tile([P, PAIRS, TILES, 3], BF16)
-        nc.scalar.dma_start(
+        box = keep.tile([P, PAIRS, 7], BF16)
+        bq_rows = keep.tile([P, D], BF16)
+        bg_rows = keep.tile([P, D], BF16)
+        keep_in = keep.tile([P, PAIRS, TILES], BF16)
+        presence = keep.tile([P, PAIRS], BF16)
+        bg_bias = keep.tile([P, 1], BF16)
+
+        for first in range(0, TILES, 2):
+            nc.sync.dma_start(out=xq[:, first : first + 2, :], in_=query_rows[:, first : first + 2, :])
+        nc.sync.dma_start(
             out=position[:].rearrange("p g j c -> p g (j c)"),
             in_=center.rearrange("b t (p c) -> p (b t) c", c=3 * TILES),
         )
-        box = keep.tile([P, PAIRS, 7], BF16)
-        nc.scalar.dma_start(out=box[:], in_=query_box3d.rearrange("b t m c -> m (b t) c"))
-        xq = keep.tile([P, TILES, K], BF16)
-        query_rows = query_feat.rearrange("b t m k -> (b t m) k").rearrange("(p i) k -> p i k", i=TILES)
-        for first in range(0, TILES, 2):
-            nc.sync.dma_start(out=xq[:, first : first + 2, :], in_=query_rows[:, first : first + 2, :])
+        nc.sync.dma_start(out=box[:], in_=query_box3d.rearrange("b t m c -> m (b t) c"))
         load_words(Wq_words, wq_words)
-        load_gaussians(0)
         load_scales(Wq_scales, wq_plane)
-        bq_rows = keep.tile([P, D], BF16)
         nc.sync.dma_start(out=bq_rows[:], in_=bq.partition_broadcast(P))
+        load_gaussians(0)
         load_words(Wg_words, wg_words)
         load_gaussians(1)
         load_scales(Wg_scales, wg_plane)
-        bg_rows = keep.tile([P, D], BF16)
         nc.sync.dma_start(out=bg_rows[:], in_=bg.partition_broadcast(P))
         load_gaussians(2)
         load_gaussians(3)
-        keep_in = keep.tile([P, PAIRS, TILES], BF16)
         nc.sync.dma_start(out=keep_in[:], in_=keep_score.rearrange("b t (p j) -> p (b t) j", j=TILES))
-        presence = keep.tile([P, PAIRS], BF16)
         with nc.allow_non_contiguous_dma(reason="512 two-byte elements, one query to a partition"):
             nc.sync.dma_start(out=presence[:], in_=presence_logit.rearrange("b t m -> m (b t)"))
-        bg_bias = keep.tile([P, 1], BF16)
         nc.sync.dma_start(out=bg_bias[:], in_=background_bias.partition_broadcast(P))
 
-        kept = keep.tile([P, PAIRS, TILES], F32)
-        odds = keep.tile([P, PAIRS, TILES], F32)
-        keep_factor = keep.tile([P, PAIRS, TILES], F32)
+        x_turned, x_grouped, x_words, x_plane = {}, {}, {}, {}
+        y_psum, y, square_sum, inv_norm = {}, {}, {}, {}
+        f, f_turned, f_grouped, f_words, f_plane = {}, {}, {}, {}, {}
+
+        def turn(rows, half, pairs_of):
+            turned = psum.tile([P, 2, 2, P], F32, tag="bank", name="turned")
+            for i in range(2):
+                row_pairs = rows[:, 2 * half + i, :].bitcast(F32)
+                for u2 in range(2):
+                    nc.tensor.transpose(turned[:, i, u2, :], row_pairs[:, pairs_of[u2]], ident_f32[:])
+            return turned
+
+        def lay_side_by_side(turned, grouped, half, copy_out):
+            grouped_pairs = grouped[:].bitcast(F32)
+            copy_out(
+                out=grouped_pairs[:, 2 * P * half : 2 * P * (half + 1), :].rearrange("p (i r) u2 -> p i r u2", i=2),
+                in_=turned[:].rearrange("p i u2 r -> p i r u2"),
+            )
+
+        def turn_inputs(u, half):
+            x_turned[u, half] = turn(xq if u == 0 else xg[:, u - 1], half, (slice(0, 255, 2), slice(1, 256, 2)))
+
+        def group_inputs(u, half, copy_out):
+            if half == 0:
+                x_grouped[u] = work.tile([P, ROWS, PACK], BF16, tag="x_grouped", name="x_grouped", align_bytes=64)
+            lay_side_by_side(x_turned[u, half], x_grouped[u], half, copy_out)
+
+        def quantise_inputs(u):
+            x_words[u] = work.tile([P, ROWS], U32, tag="x_words", name="x_words", bufs=3, align_bytes=64)
+            x_plane[u] = work.tile([P, ROWS], U8, tag="x_plane", name="x_plane", bufs=3, align_bytes=64)
+            nc.vector.quantize_mx(
+                out=x_words[u][:].bitcast(FP8X4),
+                scales=x_plane[u][:],
+                in_=x_grouped[u][:].rearrange("p r t -> p (r t)"),
+            )
+
+        def multiply(u, i):
+            tile_cols = slice(P * i, P * (i + 1))
+            y_psum[u, i] = psum.tile([P, D], F32, tag="bank", name="y_psum")
+            nc.tensor.matmul_mx(
+                out=y_psum[u, i][:],
+                lhsT=x_words[u][:, tile_cols].bitcast(FP8X4),
+                lhsT_scale=x_plane[u][:, tile_cols],
+                rhs=(wq_words if u == 0 else wg_words)[:].bitcast(FP8X4),
+                rhs_scale=(wq_plane if u == 0 else wg_plane)[:],
+                start=True,
+                stop=True,
+            )
+
+        def add_bias(u, i):
+            if i == 0:
+                square_sum[u] = work.tile([P, TILES], F32, tag="square_sum", name="square_sum", bufs=UNITS)
+            y[u, i] = rows_pool.tile([P, D], F32, tag="y", name="y")
+            nc.vector.tensor_tensor(
+                out=y[u, i][:], in0=y_psum[u, i][:], in1=(bq_rows if u == 0 else bg_rows)[:], op=ALU.add
+            )
+
+        def square(u, i):
+            squares = work.tile([P, D], BF16, tag="squares", name="squares")
+            nc.scalar.activation(
+                out=squares[:], in_=y[u, i][:], func=ACT.Square, accum_out=square_sum[u][:, i : i + 1]
+            )
+
+        def load_root_table():
+            root_of_one = keep.tile([P, 1], F32)
+            nc.scalar.activation(out=root_of_one[:], in_=ones[:], func=ACT.Abs_reciprocal_sqrt)
+
+        def inverse_norm(u):
+            inv_norm[u] = work.tile([P, TILES], F32, tag="inv_norm", name="inv_norm", bufs=UNITS)
+            nc.scalar.activation(out=inv_norm[u][:], in_=square_sum[u][:], func=ACT.Abs_reciprocal_sqrt)
+
+        def clip_inverse_norm(engine, u):
+            engine.tensor_scalar_min(out=inv_norm[u][:], in0=inv_norm[u][:], scalar1=1.0 / NORM_EPS)
+
+        def normalise(engine, u):
+            f[u] = work.tile([P, TILES, D], BF16, tag="f", name="f", bufs=UNITS)
+            for i in range(TILES):
+                engine.tensor_scalar(
+                    out=f[u][:, i, :],
+                    in0=y[u, i][:],
+                    scalar1=inv_norm[u][:, i : i + 1],
+                    scalar2=0.0,
+                    op0=ALU.mult,
+                    op1=ALU.add,
+                )
+
+        def turn_features(u, half):
+            f_turned[u, half] = turn(f[u], half, (slice(0, P), slice(P, 2 * P)))
+
+        def group_features(u, half, copy_out):
+            if half == 0:
+                f_grouped[u] = work.tile([P, ROWS, PACK], BF16, tag="f_grouped", name="f_grouped", align_bytes=64)
+            if u > 0:
+                lay_side_by_side(f_turned[u, half], f_grouped[u], half, copy_out)
+                return
+            grouped_pairs = f_grouped[u][:].bitcast(F32).rearrange("p (r i) u2 -> p r i u2", i=TILES)
+            copy_out(
+                out=grouped_pairs[:, :, 2 * half : 2 * half + 2, :],
+                in_=f_turned[u, half][:].rearrange("p i u2 r -> p r i u2"),
+            )
+
+        def quantise_features(u):
+            pool, name = (keep, "qf") if u == 0 else (work, "gf")
+            f_words[u] = pool.tile([P, ROWS], U32, tag=name + "_words", name="f_words", align_bytes=64)
+            f_plane[u] = pool.tile([P, ROWS], U8, tag=name + "_plane", name="f_plane", align_bytes=64)
+            nc.vector.quantize_mx(
+                out=f_words[u][:].bitcast(FP8X4),
+                scales=f_plane[u][:],
+                in_=f_grouped[u][:].rearrange("p r t -> p (r t)"),
+            )
 
         size = keep.tile([P, PAIRS, 3], F32)
         rate = keep.tile([P, PAIRS, 3], F32)
         shift = keep.tile([P, PAIRS, 3], F32)
+        by_coordinate = keep.tile([P, PAIRS, 3, TILES], BF16)
+        spread_positions, reach, farthest = {}, {}, {}
 
-        def box_sizes():
+        def order_positions():
+            nc.vector.tensor_copy(out=by_coordinate[:], in_=position[:].rearrange("p g j c -> p g c j"))
+
+        def box_terms():
             nc.vector.scalar_tensor_tensor(
                 out=size[:], in0=box[:, :, 3:6], scalar=-1.0, in1=box[:, :, 3:6], op0=ALU.mult, op1=ALU.max
             )
-
-        def box_scaled_sizes():
             nc.vector.tensor_scalar(
                 out=size[:],
                 in0=size[:],
@@ -160,33 +259,68 @@ def tile_gaussianqueryassignment_kernel(
                 op0=ALU.max,
                 op1=ALU.mult,
             )
-
-        def box_rates():
             nc.vector.reciprocal(out=rate[:], in_=size[:])
-
-        def box_shifts():
             nc.vector.scalar_tensor_tensor(
                 out=shift[:], in0=box[:, :, 0:3], scalar=-1.0, in1=rate[:], op0=ALU.mult, op1=ALU.mult
             )
 
-        presence_spread = []
-        presence_gap = keep.tile([P, PAIRS], F32)
+        def gate_spread(g, coordinates):
+            spread = psum.tile([P, 2, 2, P], F32, tag="bank", name="spread")
+            for i, c in enumerate(coordinates):
+                pairs = by_coordinate[:, g, c, :].bitcast(F32)
+                for h in range(2):
+                    nc.tensor.transpose(spread[:, i, h, :], pairs[:, h : h + 1].to_broadcast([P, P]), ident_f32[:])
+                spread_positions[g, c] = spread[:, i]
+
+        def gate_reach(g, c):
+            if g not in reach:
+                reach[g] = work.tile([P, 3, ROWS], F32, tag="reach", name="reach", bufs=PAIRS)
+            nc.scalar.activation(
+                out=reach[g][:, c, :].rearrange("m (h e p) -> m h e p", h=2, e=2),
+                in_=spread_positions[g, c]
+                .rearrange("m h p -> m (h p)")
+                .bitcast(BF16)
+                .rearrange("m (h p e) -> m h e p", h=2, e=2),
+                func=ACT.Abs,
+                scale=rate[:, g, c : c + 1],
+                bias=shift[:, g, c : c + 1],
+            )
+
+        def gate_farthest(g, c):
+            if c == 1:
+                farthest[g] = keep.tile([P, ROWS], F32, tag="farthest%d" % g, name="farthest")
+            nc.vector.tensor_tensor(
+                out=farthest[g][:],
+                in0=reach[g][:, 0, :] if c == 1 else farthest[g][:],
+                in1=reach[g][:, c, :],
+                op=ALU.max,
+            )
+
+        kept = keep.tile([P, PAIRS, TILES], F32)
+        odds = keep.tile([P, PAIRS, TILES], F32)
+        keep_factor = keep.tile([P, PAIRS, TILES], F32)
         presence_max = keep.tile([P, PAIRS], F32)
+        presence_gap = keep.tile([P, PAIRS], F32)
         background_gap = keep.tile([P, PAIRS, 1], F32)
         background = keep.tile([P, PAIRS, TILES], F32)
+        presence_spread = {}
 
         def spread_presence():
-            spread = psum.tile([P, PAIRS // 2, P], F32, tag="bank", name="spread")
+            presence_spread[0] = psum.tile([P, PAIRS // 2, P], F32, tag="bank", name="spread")
             pairs = presence[:].bitcast(F32)
             for h in range(PAIRS // 2):
-                nc.tensor.transpose(spread[:, h, :], pairs[:, h : h + 1].to_broadcast([P, P]), ident_f32[:])
-            presence_spread.append(spread)
+                nc.tensor.transpose(
+                    presence_spread[0][:, h, :], pairs[:, h : h + 1].to_broadcast([P, P]), ident_f32[:]
+                )
 
         def keep_and_presence_terms():
             nc.vector.tensor_reduce(
                 out=presence_max[:].rearrange("m (h e) -> m h e", h=2),
-                in_=presence_spread[0][:].rearrange("m h p -> m (h p)").bitcast(BF16).rearrange("m (h p e) -> m h e p", h=2, e=2),
-                axis=mybir.AxisListType.X,
+                in_=presence_spread[0][:]
+                .rearrange("m h p -> m (h p)")
+                .bitcast(BF16)
+                .rearrange("m (h p e) -> m h e p", h=2, e=2),
+                axis=FREE_AXIS,
                 op=ALU.max,
             )
             nc.vector.tensor_scalar(
@@ -219,189 +353,12 @@ def tile_gaussianqueryassignment_kernel(
                 op=ALU.mult,
             )
 
-        x_grouped, x_words, x_plane = {}, {}, {}
-        y, square_sum, inv_norm = {}, {}, {}
-        f, f_grouped, f_words, f_plane = {}, {}, {}, {}
-
-        def is_unit(u):
-            return 0 <= u < UNITS
-
-        def is_pair(g):
-            return 0 <= g < PAIRS
-
-        def turn(rows, half, pairs_of):
-            turned = psum.tile([P, 2, 2, P], F32, tag="bank", name="turned")
-            for i in range(2):
-                row_pairs = rows[:, 2 * half + i, :].bitcast(F32)
-                for u2 in range(2):
-                    nc.tensor.transpose(turned[:, i, u2, :], row_pairs[:, pairs_of[u2]], ident_f32[:])
-            return turned
-
-        def lay_side_by_side(turned, grouped, half, copy_out):
-            grouped_pairs = grouped[:].bitcast(F32)
-            copy_out(
-                out=grouped_pairs[:, 2 * P * half : 2 * P * (half + 1), :].rearrange("p (i r) u2 -> p i r u2", i=2),
-                in_=turned[:].rearrange("p i u2 r -> p i r u2"),
-            )
-
-        x_turned, f_turned = {}, {}
-
-        def turn_inputs(u, half):
-            if is_unit(u):
-                x_turned[u, half] = turn(xq if u == 0 else xg[:, u - 1], half, (slice(0, 255, 2), slice(1, 256, 2)))
-
-        def group_inputs(u, half, copy_out):
-            if not is_unit(u):
-                return
-            if half == 0:
-                x_grouped[u] = work.tile([P, ROWS, PACK], BF16, tag="x_grouped", name="x_grouped", align_bytes=64)
-            lay_side_by_side(x_turned[u, half], x_grouped[u], half, copy_out)
-
-        def quantise_inputs(u):
-            if not is_unit(u):
-                return
-            x_words[u] = work.tile([P, ROWS], U32, tag="x_words", name="x_words", bufs=3, align_bytes=64)
-            x_plane[u] = work.tile([P, ROWS], U8, tag="x_plane", name="x_plane", bufs=3, align_bytes=64)
-            nc.vector.quantize_mx(
-                out=x_words[u][:].bitcast(FP8X4),
-                scales=x_plane[u][:],
-                in_=x_grouped[u][:].rearrange("p r t -> p (r t)"),
-            )
-
-        y_psum = {}
-
-        def multiply(u, i):
-            if not is_unit(u):
-                return
-            tile_cols = slice(P * i, P * (i + 1))
-            y_psum[u, i] = psum.tile([P, D], F32, tag="bank", name="y_psum")
-            nc.tensor.matmul_mx(
-                out=y_psum[u, i][:],
-                lhsT=x_words[u][:, tile_cols].bitcast(FP8X4),
-                lhsT_scale=x_plane[u][:, tile_cols],
-                rhs=(wq_words if u == 0 else wg_words)[:].bitcast(FP8X4),
-                rhs_scale=(wq_plane if u == 0 else wg_plane)[:],
-                start=True,
-                stop=True,
-            )
-
-        def add_bias(u, i):
-            if not is_unit(u):
-                return
-            if i == 0:
-                square_sum[u] = work.tile([P, TILES], F32, tag="square_sum", name="square_sum", bufs=UNITS)
-            y[u, i] = rows_pool.tile([P, D], F32, tag="y", name="y")
-            nc.vector.tensor_tensor(
-                out=y[u, i][:], in0=y_psum[u, i][:], in1=(bq_rows if u == 0 else bg_rows)[:], op=ALU.add
-            )
-
-        def square(u, i):
-            if not is_unit(u):
-                return
-            squares = work.tile([P, D], BF16, tag="squares", name="squares")
-            nc.scalar.activation(
-                out=squares[:], in_=y[u, i][:], func=ACT.Square, accum_out=square_sum[u][:, i : i + 1]
-            )
-
-        def inverse_norm(u, tiles=ALL_TILES):
-            cols = slice(tiles[0], tiles[-1] + 1)
-            if u not in inv_norm:
-                inv_norm[u] = work.tile([P, TILES], F32, tag="inv_norm", name="inv_norm", bufs=UNITS)
-                f[u] = work.tile([P, TILES, D], BF16, tag="f", name="f", bufs=UNITS)
-            nc.scalar.activation(out=inv_norm[u][:, cols], in_=square_sum[u][:, cols], func=ACT.Abs_reciprocal_sqrt)
-
-        def clip_inverse_norm(engine, u, tiles=ALL_TILES):
-            cols = slice(tiles[0], tiles[-1] + 1)
-            engine.tensor_scalar_min(out=inv_norm[u][:, cols], in0=inv_norm[u][:, cols], scalar1=1.0 / NORM_EPS)
-
-        def normalise(engine, u, i):
-            if not is_unit(u):
-                return
-            engine.tensor_scalar(
-                out=f[u][:, i, :],
-                in0=y[u, i][:],
-                scalar1=inv_norm[u][:, i : i + 1],
-                scalar2=0.0,
-                op0=ALU.mult,
-                op1=ALU.add,
-            )
-
-        def turn_features(u, half):
-            if is_unit(u):
-                f_turned[u, half] = turn(f[u], half, (slice(0, P), slice(P, 2 * P)))
-
-        def group_features(u, half, copy_out):
-            if not is_unit(u):
-                return
-            if half == 0:
-                f_grouped[u] = work.tile([P, ROWS, PACK], BF16, tag="f_grouped", name="f_grouped", align_bytes=64)
-            if u > 0:
-                lay_side_by_side(f_turned[u, half], f_grouped[u], half, copy_out)
-                return
-            grouped_pairs = f_grouped[u][:].bitcast(F32).rearrange("p (r i) u2 -> p r i u2", i=TILES)
-            copy_out(
-                out=grouped_pairs[:, :, 2 * half : 2 * half + 2, :],
-                in_=f_turned[u, half][:].rearrange("p i u2 r -> p r i u2"),
-            )
-
-        def quantise_features(u):
-            if not is_unit(u):
-                return
-            pool = keep if u == 0 else work
-            f_words[u] = pool.tile([P, ROWS], U32, tag="qf_words" if u == 0 else "gf_words", name="f_words", align_bytes=64)
-            f_plane[u] = pool.tile([P, ROWS], U8, tag="qf_plane" if u == 0 else "gf_plane", name="f_plane", align_bytes=64)
-            nc.vector.quantize_mx(
-                out=f_words[u][:].bitcast(FP8X4),
-                scales=f_plane[u][:],
-                in_=f_grouped[u][:].rearrange("p r t -> p (r t)"),
-            )
-
-        reach, farthest = {}, {}
-
-        by_coordinate = keep.tile([P, PAIRS, 3, TILES], BF16)
-        spread_positions = {}
-
-        def order_positions():
-            nc.vector.tensor_copy(out=by_coordinate[:], in_=position[:].rearrange("p g j c -> p g c j"))
-
-        def spread_coordinates(g, coordinates):
-            spread = psum.tile([P, 2, 2, P], F32, tag="bank", name="spread")
-            for i, c in enumerate(coordinates):
-                pairs = by_coordinate[:, g, c, :].bitcast(F32)
-                for h in range(2):
-                    nc.tensor.transpose(spread[:, i, h, :], pairs[:, h : h + 1].to_broadcast([P, P]), ident_f32[:])
-                spread_positions[g, c] = spread[:, i]
-
-        def gate_reach(g, c):
-            if g not in reach:
-                reach[g] = work.tile([P, 3, ROWS], F32, tag="reach", name="reach", bufs=PAIRS)
-            nc.scalar.activation(
-                out=reach[g][:, c, :].rearrange("m (h e p) -> m h e p", h=2, e=2),
-                in_=spread_positions[g, c].rearrange("m h p -> m (h p)").bitcast(BF16).rearrange(
-                    "m (h p e) -> m h e p", h=2, e=2
-                ),
-                func=ACT.Abs,
-                scale=rate[:, g, c : c + 1],
-                bias=shift[:, g, c : c + 1],
-            )
-
-        def gate_farthest(g, c):
-            if not is_pair(g):
-                return
-            if c == 1:
-                farthest[g] = keep.tile([P, ROWS], F32, tag="farthest%d" % g, name="farthest")
-            nc.vector.tensor_tensor(
-                out=farthest[g][:], in0=(reach[g][:, 0, :] if c == 1 else farthest[g][:]), in1=reach[g][:, c, :], op=ALU.max
-            )
-
-        penalty, weights, rows_t = {}, {}, {}
+        sim, penalty, weights, rows_t = {}, {}, {}, {}
+        total = keep.tile([P, PAIRS, TILES, 1], F32)
+        probs = keep.tile([P, PAIRS, TILES, CLASSES], F32)
         out_rows = out.rearrange("b (t p j) c -> (b t) p (j c)", p=P, j=TILES)
 
-        sim = {}
-
         def similarity(g):
-            if not is_pair(g):
-                return
             query_cols = slice(QUERIES * g, QUERIES * (g + 1))
             sim[g] = psum.tile([P, ROWS], F32, tag="bank", name="sim")
             nc.tensor.matmul_mx(
@@ -414,238 +371,197 @@ def tile_gaussianqueryassignment_kernel(
                 stop=True,
             )
 
-        def penalties(g, tiles=ALL_TILES):
-            cols = slice(P * tiles[0], P * (tiles[-1] + 1))
-            if g not in penalty:
-                penalty[g] = work.tile([P, ROWS], F32, tag="penalty", name="penalty", bufs=PAIRS)
+        def penalties(g):
+            penalty[g] = work.tile([P, ROWS], F32, tag="penalty", name="penalty", bufs=PAIRS)
             nc.vector.scalar_tensor_tensor(
-                out=penalty[g][:, cols],
-                in0=farthest[g][:, cols],
+                out=penalty[g][:],
+                in0=farthest[g][:],
                 scalar=(GATE_TEMP + GATE_CLIP) / FEAT_TEMP,
-                in1=sim[g][:, cols],
+                in1=sim[g][:],
                 op0=ALU.min,
                 op1=ALU.subtract,
             )
 
-        def exponentials(g, tiles=ALL_TILES):
-            cols = slice(P * tiles[0], P * (tiles[-1] + 1))
-            if g not in weights:
-                weights[g] = work.tile([P, ROWS], F32, tag="weights", name="weights", bufs=PAIRS)
+        def exponentials(g):
+            weights[g] = work.tile([P, ROWS], F32, tag="weights", name="weights", bufs=PAIRS)
             nc.scalar.activation(
-                out=weights[g][:, cols],
-                in_=penalty[g][:, cols],
+                out=weights[g][:],
+                in_=penalty[g][:],
                 func=ACT.Exp,
                 scale=-FEAT_TEMP,
                 bias=presence_gap[:, g : g + 1],
             )
 
-        def rows_to_partitions(g, tiles=ALL_TILES):
-            rows_t[g] = psum.tile([P, len(tiles), QUERIES], F32, tag="bank", name="rows_t")
-            for i, j in enumerate(tiles):
-                nc.tensor.transpose(rows_t[g][:, i, :], weights[g][:, P * j : P * (j + 1)], ident_f32[:])
-
-        total = keep.tile([P, PAIRS, TILES, 1], F32)
-        probs = keep.tile([P, PAIRS, TILES, CLASSES], F32)
+        def rows_to_partitions(g):
+            rows_t[g] = psum.tile([P, TILES, QUERIES], F32, tag="bank", name="rows_t")
+            for j in range(TILES):
+                nc.tensor.transpose(rows_t[g][:, j, :], weights[g][:, P * j : P * (j + 1)], ident_f32[:])
 
         def row_totals(g):
-            nc.vector.tensor_reduce(out=total[:, g, :, 0], in_=rows_t[g][:], axis=mybir.AxisListType.X, op=ALU.add)
+            nc.vector.tensor_reduce(out=total[:, g, :, 0], in_=rows_t[g][:], axis=FREE_AXIS, op=ALU.add)
 
-        def add_background(pairs):
+        def add_background(g):
             nc.vector.tensor_tensor(
-                out=total[:, pairs, :, 0], in0=total[:, pairs, :, 0], in1=background[:, pairs, :], op=ALU.add
+                out=total[:, g : g + 1, :, 0],
+                in0=total[:, g : g + 1, :, 0],
+                in1=background[:, g : g + 1, :],
+                op=ALU.add,
             )
 
-        def invert_totals(pairs):
-            nc.vector.reciprocal(out=total[:, pairs], in_=total[:, pairs])
+        def invert_totals(g):
+            nc.vector.reciprocal(out=total[:, g : g + 1], in_=total[:, g : g + 1])
+
+        def query_probabilities(g):
+            nc.vector.tensor_tensor(
+                out=probs[:, g, :, 1:CLASSES],
+                in0=rows_t[g][:],
+                in1=total[:, g].to_broadcast([P, TILES, QUERIES]),
+                op=ALU.mult,
+            )
+
+        def query_probabilities_on_scalar(g):
+            for j in range(TILES):
+                nc.scalar.activation(
+                    out=probs[:, g, j, 1:CLASSES], in_=rows_t[g][:, j, :], func=ACT.Copy, scale=total[:, g, j, :]
+                )
 
         def background_probabilities(pairs):
             nc.vector.tensor_tensor(
                 out=probs[:, pairs, :, 0], in0=background[:, pairs, :], in1=total[:, pairs, :, 0], op=ALU.mult
             )
 
-        def query_probabilities(g, on_scalar=False):
-            if on_scalar:
-                for j in range(TILES):
-                    nc.scalar.activation(
-                        out=probs[:, g, j, 1:CLASSES], in_=rows_t[g][:, j, :], func=ACT.Copy, scale=total[:, g, j, :]
-                    )
-            else:
-                nc.vector.tensor_tensor(
-                    out=probs[:, g, :, 1:CLASSES],
-                    in0=rows_t[g][:],
-                    in1=total[:, g].to_broadcast([P, TILES, QUERIES]),
-                    op=ALU.mult,
-                )
-
         def store(g):
             nc.sync.dma_start(out=out_rows[g], in_=probs[:, g].rearrange("p j c -> p (j c)"))
-
-        def gate_spreads(g):
-            spread_coordinates(g, (0, 1))
-            spread_coordinates(g, (2,))
-
-        def gate_reaches(g):
-            for c in range(3):
-                gate_reach(g, c)
-
-        def gate_max(g):
-            gate_farthest(g, 1)
-            gate_farthest(g, 2)
-
-        def gate_max(g):
-            gate_farthest(g, 1)
-            gate_farthest(g, 2)
-
-        def project(u):
-            for i in range(TILES):
-                multiply(u, i)
 
         def turn_both(turn_half, u):
             turn_half(u, 0)
             turn_half(u, 1)
 
-        def adds(u):
-            for i in range(TILES):
-                add_bias(u, i)
+        def group_on_both(group, u):
+            group(u, 0, nc.scalar.copy)
+            group(u, 1, nc.vector.tensor_copy)
 
-        def squares(u):
-            for i in range(TILES):
-                square(u, i)
+        def group_on_scalar(group, u):
+            group(u, 0, nc.scalar.copy)
+            group(u, 1, nc.scalar.copy)
 
-        def group_both_inputs(u, copy_out):
-            group_inputs(u, 0, copy_out)
-            group_inputs(u, 1, copy_out)
+        def each(step, u, tiles=range(TILES)):
+            for i in tiles:
+                step(u, i)
 
-        def group_both_features(u):
-            group_features(u, 0, nc.scalar.copy)
-            group_features(u, 1, nc.scalar.copy)
+        def each_coordinate(step, g, coordinates=range(3)):
+            for c in coordinates:
+                step(g, c)
 
-        def normalise_all(engine, u):
-            for i in range(TILES):
-                normalise(engine, u, i)
-
-        def norm(engine, u):
+        def norm_on_gpsimd(u):
             inverse_norm(u)
-            clip_inverse_norm(engine, u)
-            normalise_all(engine, u)
+            clip_inverse_norm(nc.gpsimd, u)
+            normalise(nc.gpsimd, u)
+
+        LAST = UNITS - 1
 
         with tc.manual_schedule():
             load_root_table()
             turn_both(turn_inputs, 0)
             order_positions()
-            box_sizes()
-            box_scaled_sizes()
-            box_rates()
-            box_shifts()
-            group_inputs(0, 0, nc.scalar.copy)
-            group_inputs(0, 1, nc.vector.tensor_copy)
-            gate_spreads(0)
-            spread_coordinates(1, (0, 1))
+            box_terms()
+            group_on_both(group_inputs, 0)
+            gate_spread(0, (0, 1))
+            gate_spread(0, (2,))
+            gate_spread(1, (0, 1))
             quantise_inputs(0)
-            gate_reaches(0)
-            gate_reach(1, 0)
-            gate_reach(1, 1)
-            project(0)
+            each_coordinate(gate_reach, 0)
+            each_coordinate(gate_reach, 1, (0, 1))
+            each(multiply, 0)
             turn_both(turn_inputs, 1)
             gate_farthest(0, 1)
-            adds(0)
-            square(0, 0)
-            square(0, 1)
+            each(add_bias, 0)
+            each(square, 0, (0, 1))
             group_inputs(1, 0, nc.scalar.copy)
             square(0, 2)
             group_inputs(1, 1, nc.vector.tensor_copy)
             gate_farthest(0, 2)
             gate_farthest(1, 1)
             quantise_inputs(1)
-            spread_coordinates(1, (2,))
+            gate_spread(1, (2,))
             gate_reach(1, 2)
             square(0, 3)
-            norm(nc.gpsimd, 0)
-            gate_spreads(2)
-            gate_reach(2, 0)
+            norm_on_gpsimd(0)
+
+            gate_spread(2, (0, 1))
+            gate_spread(2, (2,))
+            each_coordinate(gate_reach, 2)
+            gate_spread(3, (0,))
             turn_both(turn_inputs, 2)
-            multiply(1, 0)
-            multiply(1, 1)
+            each(multiply, 1, (0, 1))
             group_inputs(2, 0, nc.scalar.copy)
             gate_farthest(1, 2)
-            gate_reach(2, 1)
-            gate_reach(2, 2)
-            spread_coordinates(3, (0,))
             gate_reach(3, 0)
-            multiply(1, 2)
-            multiply(1, 3)
+            each(multiply, 1, (2, 3))
             group_inputs(2, 1, nc.vector.tensor_copy)
-            add_bias(1, 0)
-            add_bias(1, 1)
-            add_bias(1, 2)
+            each(add_bias, 1, (0, 1, 2))
             quantise_inputs(2)
             add_bias(1, 3)
             turn_both(turn_inputs, 3)
-            squares(1)
-            norm(nc.gpsimd, 1)
-            project(2)
+            each(square, 1)
+            norm_on_gpsimd(1)
+
+            each(multiply, 2)
             gate_farthest(2, 1)
             group_inputs(3, 0, nc.scalar.copy)
-            add_bias(2, 0)
-            add_bias(2, 1)
-            add_bias(2, 2)
+            each(add_bias, 2, (0, 1, 2))
             turn_both(turn_features, 0)
             square(2, 0)
-            group_both_features(0)
+            group_on_scalar(group_features, 0)
             group_inputs(3, 1, nc.vector.tensor_copy)
             square(2, 1)
             add_bias(2, 3)
             quantise_inputs(3)
             turn_both(turn_inputs, 4)
-            square(2, 2)
-            square(2, 3)
+            each(square, 2, (2, 3))
             turn_features(1, 0)
-            project(3)
-            norm(nc.gpsimd, 2)
+            each(multiply, 3)
+            norm_on_gpsimd(2)
+
             turn_features(1, 1)
-            group_inputs(4, 0, nc.scalar.copy)
-            group_inputs(4, 1, nc.vector.tensor_copy)
+            group_on_both(group_inputs, 4)
             quantise_features(0)
-            add_bias(3, 0)
-            add_bias(3, 1)
-            square(3, 0)
-            square(3, 1)
-            group_both_features(1)
+            each(add_bias, 3, (0, 1))
+            each(square, 3, (0, 1))
+            group_on_scalar(group_features, 1)
             quantise_inputs(4)
-            add_bias(3, 2)
-            add_bias(3, 3)
-            square(3, 2)
-            square(3, 3)
-            spread_coordinates(3, (1, 2))
+            each(add_bias, 3, (2, 3))
+            each(square, 3, (2, 3))
+            gate_spread(3, (1, 2))
             gate_reach(3, 1)
             spread_presence()
-            norm(nc.gpsimd, 3)
+            norm_on_gpsimd(3)
             keep_and_presence_terms()
             gate_reach(3, 2)
-            project(4)
-            adds(4)
+            each(multiply, 4)
+
+            each(add_bias, LAST)
             turn_both(turn_features, 2)
-            squares(4)
-            inverse_norm(4)
+            each(square, LAST)
+            inverse_norm(LAST)
             quantise_features(1)
             gate_farthest(2, 2)
-            group_both_features(2)
+            group_on_scalar(group_features, 2)
             similarity(0)
-            clip_inverse_norm(nc.vector, 4)
+            clip_inverse_norm(nc.vector, LAST)
             turn_features(3, 0)
             background_exponentials()
             gate_farthest(3, 1)
-            normalise_all(nc.vector, 4)
+            normalise(nc.vector, LAST)
             turn_features(3, 1)
-            turn_both(turn_features, 4)
+            turn_both(turn_features, LAST)
             quantise_features(2)
             penalties(0)
             similarity(1)
-            group_features(4, 0, nc.scalar.copy)
-            group_features(4, 1, nc.vector.tensor_copy)
+            group_on_both(group_features, LAST)
             penalties(1)
-            quantise_features(4)
-            group_both_features(3)
+            quantise_features(LAST)
+            group_on_scalar(group_features, 3)
             exponentials(0)
             quantise_features(3)
             exponentials(1)
@@ -653,6 +569,7 @@ def tile_gaussianqueryassignment_kernel(
             gate_farthest(3, 2)
             background_terms()
             similarity(2)
+
             rows_to_partitions(0)
             penalties(3)
             exponentials(3)
@@ -662,25 +579,25 @@ def tile_gaussianqueryassignment_kernel(
             row_totals(0)
             rows_to_partitions(3)
             row_totals(1)
-            add_background(slice(0, 1))
+            add_background(0)
             rows_to_partitions(2)
-            invert_totals(slice(0, 1))
-            add_background(slice(1, 2))
-            query_probabilities(0, on_scalar=True)
+            add_background(1)
+            invert_totals(0)
+            query_probabilities_on_scalar(0)
             row_totals(3)
             background_probabilities(slice(0, 1))
             store(0)
-            invert_totals(slice(1, 2))
+            invert_totals(1)
             row_totals(2)
-            query_probabilities(1, on_scalar=True)
+            query_probabilities_on_scalar(1)
             background_probabilities(slice(1, 2))
             store(1)
-            add_background(slice(3, 4))
-            add_background(slice(2, 3))
-            invert_totals(slice(3, 4))
-            invert_totals(slice(2, 3))
+            add_background(3)
+            add_background(2)
+            invert_totals(3)
+            invert_totals(2)
             query_probabilities(3)
-            query_probabilities(2, on_scalar=True)
+            query_probabilities_on_scalar(2)
             background_probabilities(slice(2, 4))
             store(3)
             store(2)

from contextlib import ExitStack

import concourse.mybir as mybir
from concourse.masks import make_identity

F32 = mybir.dt.float32
BF16 = mybir.dt.bfloat16
I32 = mybir.dt.int32
U32 = mybir.dt.uint32
U8 = mybir.dt.uint8
FP8X4 = mybir.dt.float8_e4m3fn_x4
ALU = mybir.AluOpType
ACT = mybir.ActivationFunctionType
FREE_AXIS = mybir.AxisListType.X

P = 128
PACK = 4
PAIRS = 4
TILES = 4
ROWS = TILES * P
UNITS = 1 + PAIRS
QUERIES = 128
K = 512
AFFINITY = 384
D = 512
CLASSES = QUERIES + 1

DILATION = 1.5
MIN_EXTENT = 0.5
GATE_TEMP = 3.0
GATE_CLIP = 8.0
FEAT_TEMP = 6.0
KEEP_EPS = 1e-4
NORM_EPS = 1e-12
GAP_MAX = 80.0

FLOPS = 2 * (PAIRS * QUERIES + PAIRS * ROWS) * K * D + 2 * PAIRS * ROWS * QUERIES * D


def tile_gaussianqueryassignment_kernel(
    tc,
    center,
    instance_affinity,
    motion_code,
    keep_score,
    query_box3d,
    query_feat,
    presence_logit,
    Wq_words,
    Wq_scales,
    bq,
    Wg_words,
    Wg_scales,
    bg,
    background_bias,
    out,
):
    nc = tc.nc
    with ExitStack() as ctx:
        keep = ctx.enter_context(tc.tile_pool(name="keep", bufs=1))
        work = ctx.enter_context(tc.tile_pool(name="work", bufs=2))
        rows_pool = ctx.enter_context(tc.tile_pool(name="rows", bufs=UNITS * TILES))
        psum = ctx.enter_context(tc.psum_pool(name="psum", bufs=8))

        ident_f32 = keep.tile([P, P], F32)
        make_identity(nc, ident_f32[:])
        ones = keep.tile([P, 1], F32)
        nc.gpsimd.memset(ones[:], 1.0)

        wq_words = keep.tile([P, D], U32, align_bytes=64)
        wq_plane = keep.tile([P, D], U8, align_bytes=64)
        wg_words = keep.tile([P, D], U32, align_bytes=64)
        wg_plane = keep.tile([P, D], U8, align_bytes=64)
        nc.vector.memset(wq_plane[:].bitcast(I32), 0)
        nc.vector.memset(wg_plane[:].bitcast(I32), 0)

        def load_words(words_in, words):
            nc.sync.dma_start(
                out=words[:].bitcast(I32),
                in_=words_in[0].rearrange("p n t -> p (n t)").bitcast(I32),
            )

        def load_scales(scales_in, plane):
            for quadrant in range(4):
                nc.sync.dma_start(
                    out=plane[32 * quadrant : 32 * quadrant + 4, :].bitcast(I32),
                    in_=scales_in[0, 4 * quadrant : 4 * quadrant + 4, :].bitcast(I32),
                )

        xq = keep.tile([P, TILES, K], BF16)
        query_rows = query_feat.rearrange("b t m k -> (b t m) k").rearrange("(p i) k -> p i k", i=TILES)
        xg = keep.tile([P, PAIRS, TILES, K], BF16)
        affinity_in = instance_affinity.rearrange("b t (p j) a -> (b t) p j a", j=TILES)
        motion_in = motion_code.rearrange("b t (p j) c -> (b t) p j c", j=TILES)

        def load_gaussians(g):
            nc.sync.dma_start(out=xg[:, g, :, 0:AFFINITY], in_=affinity_in[g])
            nc.sync.dma_start(out=xg[:, g, :, AFFINITY:K], in_=motion_in[g])

        position = keep.tile([P, PAIRS, TILES, 3], BF16)
        box = keep.tile([P, PAIRS, 7], BF16)
        bq_rows = keep.tile([P, D], BF16)
        bg_rows = keep.tile([P, D], BF16)
        keep_in = keep.tile([P, PAIRS, TILES], BF16)
        presence = keep.tile([P, PAIRS], BF16)
        bg_bias = keep.tile([P, 1], BF16)

        for first in range(0, TILES, 2):
            nc.sync.dma_start(out=xq[:, first : first + 2, :], in_=query_rows[:, first : first + 2, :])
        nc.sync.dma_start(
            out=position[:].rearrange("p g j c -> p g (j c)"),
            in_=center.rearrange("b t (p c) -> p (b t) c", c=3 * TILES),
        )
        nc.sync.dma_start(out=box[:], in_=query_box3d.rearrange("b t m c -> m (b t) c"))
        load_words(Wq_words, wq_words)
        load_scales(Wq_scales, wq_plane)
        nc.sync.dma_start(out=bq_rows[:], in_=bq.partition_broadcast(P))
        load_gaussians(0)
        load_words(Wg_words, wg_words)
        load_gaussians(1)
        load_scales(Wg_scales, wg_plane)
        nc.sync.dma_start(out=bg_rows[:], in_=bg.partition_broadcast(P))
        load_gaussians(2)
        load_gaussians(3)
        nc.sync.dma_start(out=keep_in[:], in_=keep_score.rearrange("b t (p j) -> p (b t) j", j=TILES))
        with nc.allow_non_contiguous_dma(reason="512 two-byte elements, one query to a partition"):
            nc.sync.dma_start(out=presence[:], in_=presence_logit.rearrange("b t m -> m (b t)"))
        nc.sync.dma_start(out=bg_bias[:], in_=background_bias.partition_broadcast(P))

        x_turned, x_grouped, x_words, x_plane = {}, {}, {}, {}
        y_psum, y, square_sum, inv_norm = {}, {}, {}, {}
        f, f_turned, f_grouped, f_words, f_plane = {}, {}, {}, {}, {}

        def turn(rows, half, pairs_of):
            turned = psum.tile([P, 2, 2, P], F32, tag="bank", name="turned")
            for i in range(2):
                row_pairs = rows[:, 2 * half + i, :].bitcast(F32)
                for u2 in range(2):
                    nc.tensor.transpose(turned[:, i, u2, :], row_pairs[:, pairs_of[u2]], ident_f32[:])
            return turned

        def lay_side_by_side(turned, grouped, half, copy_out):
            grouped_pairs = grouped[:].bitcast(F32)
            copy_out(
                out=grouped_pairs[:, 2 * P * half : 2 * P * (half + 1), :].rearrange("p (i r) u2 -> p i r u2", i=2),
                in_=turned[:].rearrange("p i u2 r -> p i r u2"),
            )

        def turn_inputs(u, half):
            x_turned[u, half] = turn(xq if u == 0 else xg[:, u - 1], half, (slice(0, 255, 2), slice(1, 256, 2)))

        def group_inputs(u, half, copy_out):
            if half == 0:
                x_grouped[u] = work.tile([P, ROWS, PACK], BF16, tag="x_grouped", name="x_grouped", align_bytes=64)
            lay_side_by_side(x_turned[u, half], x_grouped[u], half, copy_out)

        def quantise_inputs(u):
            x_words[u] = work.tile([P, ROWS], U32, tag="x_words", name="x_words", bufs=3, align_bytes=64)
            x_plane[u] = work.tile([P, ROWS], U8, tag="x_plane", name="x_plane", bufs=3, align_bytes=64)
            nc.vector.quantize_mx(
                out=x_words[u][:].bitcast(FP8X4),
                scales=x_plane[u][:],
                in_=x_grouped[u][:].rearrange("p r t -> p (r t)"),
            )

        def multiply(u, i):
            tile_cols = slice(P * i, P * (i + 1))
            y_psum[u, i] = psum.tile([P, D], F32, tag="bank", name="y_psum")
            nc.tensor.matmul_mx(
                out=y_psum[u, i][:],
                lhsT=x_words[u][:, tile_cols].bitcast(FP8X4),
                lhsT_scale=x_plane[u][:, tile_cols],
                rhs=(wq_words if u == 0 else wg_words)[:].bitcast(FP8X4),
                rhs_scale=(wq_plane if u == 0 else wg_plane)[:],
                start=True,
                stop=True,
            )

        def add_bias(u, i):
            if i == 0:
                square_sum[u] = work.tile([P, TILES], F32, tag="square_sum", name="square_sum", bufs=UNITS)
            y[u, i] = rows_pool.tile([P, D], F32, tag="y", name="y")
            nc.vector.tensor_tensor(
                out=y[u, i][:], in0=y_psum[u, i][:], in1=(bq_rows if u == 0 else bg_rows)[:], op=ALU.add
            )

        def square(u, i):
            squares = work.tile([P, D], BF16, tag="squares", name="squares")
            nc.scalar.activation(
                out=squares[:], in_=y[u, i][:], func=ACT.Square, accum_out=square_sum[u][:, i : i + 1]
            )

        def load_root_table():
            root_of_one = keep.tile([P, 1], F32)
            nc.scalar.activation(out=root_of_one[:], in_=ones[:], func=ACT.Abs_reciprocal_sqrt)

        def inverse_norm(u):
            inv_norm[u] = work.tile([P, TILES], F32, tag="inv_norm", name="inv_norm", bufs=UNITS)
            nc.scalar.activation(out=inv_norm[u][:], in_=square_sum[u][:], func=ACT.Abs_reciprocal_sqrt)

        def clip_inverse_norm(engine, u):
            engine.tensor_scalar_min(out=inv_norm[u][:], in0=inv_norm[u][:], scalar1=1.0 / NORM_EPS)

        def normalise(engine, u):
            f[u] = work.tile([P, TILES, D], BF16, tag="f", name="f", bufs=UNITS)
            for i in range(TILES):
                engine.tensor_scalar(
                    out=f[u][:, i, :],
                    in0=y[u, i][:],
                    scalar1=inv_norm[u][:, i : i + 1],
                    scalar2=0.0,
                    op0=ALU.mult,
                    op1=ALU.add,
                )

        def turn_features(u, half):
            f_turned[u, half] = turn(f[u], half, (slice(0, P), slice(P, 2 * P)))

        def group_features(u, half, copy_out):
            if half == 0:
                f_grouped[u] = work.tile([P, ROWS, PACK], BF16, tag="f_grouped", name="f_grouped", align_bytes=64)
            if u > 0:
                lay_side_by_side(f_turned[u, half], f_grouped[u], half, copy_out)
                return
            grouped_pairs = f_grouped[u][:].bitcast(F32).rearrange("p (r i) u2 -> p r i u2", i=TILES)
            copy_out(
                out=grouped_pairs[:, :, 2 * half : 2 * half + 2, :],
                in_=f_turned[u, half][:].rearrange("p i u2 r -> p r i u2"),
            )

        def quantise_features(u):
            pool, name = (keep, "qf") if u == 0 else (work, "gf")
            f_words[u] = pool.tile([P, ROWS], U32, tag=name + "_words", name="f_words", align_bytes=64)
            f_plane[u] = pool.tile([P, ROWS], U8, tag=name + "_plane", name="f_plane", align_bytes=64)
            nc.vector.quantize_mx(
                out=f_words[u][:].bitcast(FP8X4),
                scales=f_plane[u][:],
                in_=f_grouped[u][:].rearrange("p r t -> p (r t)"),
            )

        size = keep.tile([P, PAIRS, 3], F32)
        rate = keep.tile([P, PAIRS, 3], F32)
        shift = keep.tile([P, PAIRS, 3], F32)
        by_coordinate = keep.tile([P, PAIRS, 3, TILES], BF16)
        spread_positions, reach, farthest = {}, {}, {}

        def order_positions():
            nc.vector.tensor_copy(out=by_coordinate[:], in_=position[:].rearrange("p g j c -> p g c j"))

        def box_terms():
            nc.vector.scalar_tensor_tensor(
                out=size[:], in0=box[:, :, 3:6], scalar=-1.0, in1=box[:, :, 3:6], op0=ALU.mult, op1=ALU.max
            )
            nc.vector.tensor_scalar(
                out=size[:],
                in0=size[:],
                scalar1=MIN_EXTENT,
                scalar2=0.5 * DILATION * FEAT_TEMP / GATE_TEMP,
                op0=ALU.max,
                op1=ALU.mult,
            )
            nc.vector.reciprocal(out=rate[:], in_=size[:])
            nc.vector.scalar_tensor_tensor(
                out=shift[:], in0=box[:, :, 0:3], scalar=-1.0, in1=rate[:], op0=ALU.mult, op1=ALU.mult
            )

        def gate_spread(g, coordinates):
            spread = psum.tile([P, 2, 2, P], F32, tag="bank", name="spread")
            for i, c in enumerate(coordinates):
                pairs = by_coordinate[:, g, c, :].bitcast(F32)
                for h in range(2):
                    nc.tensor.transpose(spread[:, i, h, :], pairs[:, h : h + 1].to_broadcast([P, P]), ident_f32[:])
                spread_positions[g, c] = spread[:, i]

        def gate_reach(g, c):
            if g not in reach:
                reach[g] = work.tile([P, 3, ROWS], F32, tag="reach", name="reach", bufs=PAIRS)
            nc.scalar.activation(
                out=reach[g][:, c, :].rearrange("m (h e p) -> m h e p", h=2, e=2),
                in_=spread_positions[g, c]
                .rearrange("m h p -> m (h p)")
                .bitcast(BF16)
                .rearrange("m (h p e) -> m h e p", h=2, e=2),
                func=ACT.Abs,
                scale=rate[:, g, c : c + 1],
                bias=shift[:, g, c : c + 1],
            )

        def gate_farthest(g, c):
            if c == 1:
                farthest[g] = keep.tile([P, ROWS], F32, tag="farthest%d" % g, name="farthest")
            nc.vector.tensor_tensor(
                out=farthest[g][:],
                in0=reach[g][:, 0, :] if c == 1 else farthest[g][:],
                in1=reach[g][:, c, :],
                op=ALU.max,
            )

        kept = keep.tile([P, PAIRS, TILES], F32)
        odds = keep.tile([P, PAIRS, TILES], F32)
        keep_factor = keep.tile([P, PAIRS, TILES], F32)
        presence_max = keep.tile([P, PAIRS], F32)
        presence_gap = keep.tile([P, PAIRS], F32)
        background_gap = keep.tile([P, PAIRS, 1], F32)
        background = keep.tile([P, PAIRS, TILES], F32)
        presence_spread = {}

        def spread_presence():
            presence_spread[0] = psum.tile([P, PAIRS // 2, P], F32, tag="bank", name="spread")
            pairs = presence[:].bitcast(F32)
            for h in range(PAIRS // 2):
                nc.tensor.transpose(
                    presence_spread[0][:, h, :], pairs[:, h : h + 1].to_broadcast([P, P]), ident_f32[:]
                )

        def keep_and_presence_terms():
            nc.vector.tensor_reduce(
                out=presence_max[:].rearrange("m (h e) -> m h e", h=2),
                in_=presence_spread[0][:]
                .rearrange("m h p -> m (h p)")
                .bitcast(BF16)
                .rearrange("m (h p e) -> m h e p", h=2, e=2),
                axis=FREE_AXIS,
                op=ALU.max,
            )
            nc.vector.tensor_scalar(
                out=kept[:], in0=keep_in[:], scalar1=KEEP_EPS, scalar2=1.0 - KEEP_EPS, op0=ALU.max, op1=ALU.min
            )
            nc.vector.tensor_tensor(out=presence_gap[:], in0=presence[:], in1=presence_max[:], op=ALU.subtract)
            nc.vector.tensor_scalar(out=odds[:], in0=kept[:], scalar1=-1.0, scalar2=1.0, op0=ALU.mult, op1=ALU.add)
            nc.vector.reciprocal(out=odds[:], in_=odds[:])
            nc.vector.tensor_scalar(
                out=background_gap[:, :, 0],
                in0=presence_max[:],
                scalar1=bg_bias[:, 0:1],
                scalar2=-GAP_MAX,
                op0=ALU.subtract,
                op1=ALU.max,
            )
            nc.vector.tensor_tensor(out=odds[:], in0=odds[:], in1=kept[:], op=ALU.mult)
            nc.scalar.activation(out=keep_factor[:], in_=odds[:], func=ACT.Abs_reciprocal_sqrt)

        def background_exponentials():
            nc.scalar.activation(
                out=background_gap[:], in_=background_gap[:], func=ACT.Exp, scale=-1.0, bias=-GATE_TEMP
            )

        def background_terms():
            nc.vector.tensor_tensor(
                out=background[:],
                in0=keep_factor[:],
                in1=background_gap[:].to_broadcast([P, PAIRS, TILES]),
                op=ALU.mult,
            )

        sim, penalty, weights, rows_t = {}, {}, {}, {}
        total = keep.tile([P, PAIRS, TILES, 1], F32)
        probs = keep.tile([P, PAIRS, TILES, CLASSES], F32)
        out_rows = out.rearrange("b (t p j) c -> (b t) p (j c)", p=P, j=TILES)

        def similarity(g):
            query_cols = slice(QUERIES * g, QUERIES * (g + 1))
            sim[g] = psum.tile([P, ROWS], F32, tag="bank", name="sim")
            nc.tensor.matmul_mx(
                out=sim[g][:],
                lhsT=f_words[0][:, query_cols].bitcast(FP8X4),
                lhsT_scale=f_plane[0][:, query_cols],
                rhs=f_words[1 + g][:].bitcast(FP8X4),
                rhs_scale=f_plane[1 + g][:],
                start=True,
                stop=True,
            )

        def penalties(g):
            penalty[g] = work.tile([P, ROWS], F32, tag="penalty", name="penalty", bufs=PAIRS)
            nc.vector.scalar_tensor_tensor(
                out=penalty[g][:],
                in0=farthest[g][:],
                scalar=(GATE_TEMP + GATE_CLIP) / FEAT_TEMP,
                in1=sim[g][:],
                op0=ALU.min,
                op1=ALU.subtract,
            )

        def exponentials(g):
            weights[g] = work.tile([P, ROWS], F32, tag="weights", name="weights", bufs=PAIRS)
            nc.scalar.activation(
                out=weights[g][:],
                in_=penalty[g][:],
                func=ACT.Exp,
                scale=-FEAT_TEMP,
                bias=presence_gap[:, g : g + 1],
            )

        def rows_to_partitions(g):
            rows_t[g] = psum.tile([P, TILES, QUERIES], F32, tag="bank", name="rows_t")
            for j in range(TILES):
                nc.tensor.transpose(rows_t[g][:, j, :], weights[g][:, P * j : P * (j + 1)], ident_f32[:])

        def row_totals(g):
            nc.vector.tensor_reduce(out=total[:, g, :, 0], in_=rows_t[g][:], axis=FREE_AXIS, op=ALU.add)

        def add_background(g):
            nc.vector.tensor_tensor(
                out=total[:, g : g + 1, :, 0],
                in0=total[:, g : g + 1, :, 0],
                in1=background[:, g : g + 1, :],
                op=ALU.add,
            )

        def invert_totals(g):
            nc.vector.reciprocal(out=total[:, g : g + 1], in_=total[:, g : g + 1])

        def query_probabilities(g):
            nc.vector.tensor_tensor(
                out=probs[:, g, :, 1:CLASSES],
                in0=rows_t[g][:],
                in1=total[:, g].to_broadcast([P, TILES, QUERIES]),
                op=ALU.mult,
            )

        def query_probabilities_on_scalar(g):
            for j in range(TILES):
                nc.scalar.activation(
                    out=probs[:, g, j, 1:CLASSES], in_=rows_t[g][:, j, :], func=ACT.Copy, scale=total[:, g, j, :]
                )

        def background_probabilities(pairs):
            nc.vector.tensor_tensor(
                out=probs[:, pairs, :, 0], in0=background[:, pairs, :], in1=total[:, pairs, :, 0], op=ALU.mult
            )

        def store(g):
            nc.sync.dma_start(out=out_rows[g], in_=probs[:, g].rearrange("p j c -> p (j c)"))

        def turn_both(turn_half, u):
            turn_half(u, 0)
            turn_half(u, 1)

        def group_on_both(group, u):
            group(u, 0, nc.scalar.copy)
            group(u, 1, nc.vector.tensor_copy)

        def group_on_scalar(group, u):
            group(u, 0, nc.scalar.copy)
            group(u, 1, nc.scalar.copy)

        def each(step, u, tiles=range(TILES)):
            for i in tiles:
                step(u, i)

        def each_coordinate(step, g, coordinates=range(3)):
            for c in coordinates:
                step(g, c)

        def norm_on_gpsimd(u):
            inverse_norm(u)
            clip_inverse_norm(nc.gpsimd, u)
            normalise(nc.gpsimd, u)

        LAST = UNITS - 1

        with tc.manual_schedule():
            load_root_table()
            turn_both(turn_inputs, 0)
            order_positions()
            box_terms()
            group_on_both(group_inputs, 0)
            gate_spread(0, (0, 1))
            gate_spread(0, (2,))
            gate_spread(1, (0, 1))
            quantise_inputs(0)
            each_coordinate(gate_reach, 0)
            each_coordinate(gate_reach, 1, (0, 1))
            each(multiply, 0)
            turn_both(turn_inputs, 1)
            gate_farthest(0, 1)
            each(add_bias, 0)
            each(square, 0, (0, 1))
            group_inputs(1, 0, nc.scalar.copy)
            square(0, 2)
            group_inputs(1, 1, nc.vector.tensor_copy)
            gate_farthest(0, 2)
            gate_farthest(1, 1)
            quantise_inputs(1)
            gate_spread(1, (2,))
            gate_reach(1, 2)
            square(0, 3)
            norm_on_gpsimd(0)

            gate_spread(2, (0, 1))
            gate_spread(2, (2,))
            each_coordinate(gate_reach, 2)
            gate_spread(3, (0,))
            turn_both(turn_inputs, 2)
            each(multiply, 1, (0, 1))
            group_inputs(2, 0, nc.scalar.copy)
            gate_farthest(1, 2)
            gate_reach(3, 0)
            each(multiply, 1, (2, 3))
            group_inputs(2, 1, nc.vector.tensor_copy)
            each(add_bias, 1, (0, 1, 2))
            quantise_inputs(2)
            add_bias(1, 3)
            turn_both(turn_inputs, 3)
            each(square, 1)
            norm_on_gpsimd(1)

            each(multiply, 2)
            gate_farthest(2, 1)
            group_inputs(3, 0, nc.scalar.copy)
            each(add_bias, 2, (0, 1, 2))
            turn_both(turn_features, 0)
            square(2, 0)
            group_on_scalar(group_features, 0)
            group_inputs(3, 1, nc.vector.tensor_copy)
            square(2, 1)
            add_bias(2, 3)
            quantise_inputs(3)
            turn_both(turn_inputs, 4)
            each(square, 2, (2, 3))
            turn_features(1, 0)
            each(multiply, 3)
            norm_on_gpsimd(2)

            turn_features(1, 1)
            group_on_both(group_inputs, 4)
            quantise_features(0)
            each(add_bias, 3, (0, 1))
            each(square, 3, (0, 1))
            group_on_scalar(group_features, 1)
            quantise_inputs(4)
            each(add_bias, 3, (2, 3))
            each(square, 3, (2, 3))
            gate_spread(3, (1, 2))
            gate_reach(3, 1)
            spread_presence()
            norm_on_gpsimd(3)
            keep_and_presence_terms()
            gate_reach(3, 2)
            each(multiply, 4)

            each(add_bias, LAST)
            turn_both(turn_features, 2)
            each(square, LAST)
            inverse_norm(LAST)
            quantise_features(1)
            gate_farthest(2, 2)
            group_on_scalar(group_features, 2)
            similarity(0)
            clip_inverse_norm(nc.vector, LAST)
            turn_features(3, 0)
            background_exponentials()
            gate_farthest(3, 1)
            normalise(nc.vector, LAST)
            turn_features(3, 1)
            turn_both(turn_features, LAST)
            quantise_features(2)
            penalties(0)
            similarity(1)
            group_on_both(group_features, LAST)
            penalties(1)
            quantise_features(LAST)
            group_on_scalar(group_features, 3)
            exponentials(0)
            quantise_features(3)
            exponentials(1)
            similarity(3)
            gate_farthest(3, 2)
            background_terms()
            similarity(2)

            rows_to_partitions(0)
            penalties(3)
            exponentials(3)
            rows_to_partitions(1)
            penalties(2)
            exponentials(2)
            row_totals(0)
            rows_to_partitions(3)
            row_totals(1)
            add_background(0)
            rows_to_partitions(2)
            add_background(1)
            invert_totals(0)
            query_probabilities_on_scalar(0)
            row_totals(3)
            background_probabilities(slice(0, 1))
            store(0)
            invert_totals(1)
            row_totals(2)
            query_probabilities_on_scalar(1)
            background_probabilities(slice(1, 2))
            store(1)
            add_background(3)
            add_background(2)
            invert_totals(3)
            invert_totals(2)
            query_probabilities(3)
            query_probabilities_on_scalar(2)
            background_probabilities(slice(2, 4))
            store(3)
            store(2)
